import numpy as np
import ml_dtypes


def mxq(x, axis, fmt="e4m3"):
    dtype, down = {"e4m3": (ml_dtypes.float8_e4m3fn, 7), "e5m2": (ml_dtypes.float8_e5m2, 14)}[fmt]
    v = np.moveaxis(np.asarray(x, np.float32).astype(ml_dtypes.bfloat16).astype(np.float64), axis, -1)
    blocks = v.reshape(v.shape[:-1] + (-1, 32))
    amax = np.abs(blocks).max(-1, keepdims=True)
    byte = np.maximum(np.where(amax > 0, np.frexp(amax)[1] - 1 + 127, 0) - down, 1)
    scale = np.exp2(byte - 127.0)
    codes = (blocks / scale).astype(np.float32).astype(dtype).astype(np.float64)
    return np.moveaxis((codes * scale).reshape(v.shape), -1, axis)


WIDE = False


def mx_kscale(k):
    if not WIDE:
        return np.ones(k)
    levels = np.array([10, -10, 5, -5, 0])
    if k % 512:
        return np.exp2(np.random.permutation(np.resize(levels, k // 32))).repeat(32)
    a = np.empty((k // 512, 16))
    for p in range(k // 512):
        a[p, :8] = np.random.permutation(np.resize(levels, 8))
        for g in range(8):
            far = levels[np.abs(levels - a[p, g]) >= 10]
            a[p, g + 8] = far[np.random.randint(len(far))]
    return np.exp2(a.ravel()).repeat(32)


BF16 = ml_dtypes.bfloat16


def bf(x):
    return np.asarray(x, np.float32).astype(BF16)


def f64(x):
    return np.asarray(x).astype(np.float64)


B, IN, L = 256, 2048, 1536


def sigmoid(v):
    return 1.0 / (1.0 + np.exp(-v))


def draw0():
    s = mx_kscale(IN)
    return {"input": bf(np.random.standard_normal((B, IN)) * s),
            "h0": bf(np.random.standard_normal((B, L))),
            "gh0": bf(np.random.standard_normal((B, 3 * L)) * 0.75),
            "W_ih0": bf(np.random.standard_normal((3 * L, IN)) * 0.7 / np.sqrt(IN) / s),
            "b_ih0": bf(np.random.standard_normal(3 * L) * 0.3)}


def core(input, h0, gh0, W_ih0, b_ih0):
    h, gh = f64(h0), f64(gh0)
    gi = (mxq(f64(input), 1, "e4m3") @ mxq(f64(W_ih0), 1, "e4m3").T) + f64(b_ih0)
    i_r, i_z, i_n = gi[:, :L], gi[:, L:2 * L], gi[:, 2 * L:]
    h_r, h_z, h_n = gh[:, :L], gh[:, L:2 * L], gh[:, 2 * L:]
    r = sigmoid(i_r + h_r)
    z = sigmoid(i_z + h_z)
    n = np.tanh(i_n + r * h_n)
    return (1.0 - z) * n + z * h


def e4m3fn_bytes(y):
    return np.clip(np.asarray(y, np.float64), -448.0, 448.0).astype(np.float32).astype(ml_dtypes.float8_e4m3fn).view(np.uint8)


def e4m3fn_values(b):
    return np.asarray(b, np.uint8).view(ml_dtypes.float8_e4m3fn).astype(np.float64)


def setup_inputs():
    d = draw0()
    x0 = np.asarray(d['W_ih0']).astype(np.float64)
    s = (np.max(np.abs(x0), axis=(0,), keepdims=True) / 448.0).astype(np.float32)
    out = {}
    for k, v in d.items():
        if k == 'W_ih0':
            out['W_ih0_bytes'] = e4m3fn_bytes(x0 / s.astype(np.float64))
            out['W_ih0_scale'] = s
        else:
            out[k] = v
    return out


def reference(input, h0, gh0, W_ih0_bytes, W_ih0_scale, b_ih0):
    return core(input, h0, gh0, e4m3fn_values(W_ih0_bytes) * W_ih0_scale.astype(np.float64), b_ih0)

@@ -1,0 +1,394 @@
+from contextlib import ExitStack
+
+import concourse.mybir as mybir
+from concourse.masks import make_identity
+
+F32 = mybir.dt.float32
+BF16 = mybir.dt.bfloat16
+U8 = mybir.dt.uint8
+U32 = mybir.dt.uint32
+FP8 = mybir.dt.float8_e4m3fn
+FP8X4 = mybir.dt.float8_e4m3fn_x4
+ACT = mybir.ActivationFunctionType
+ALU = mybir.AluOpType
+
+B, IN, L = 256, 2048, 1536
+FLOPS = 2 * B * IN * 3 * L
+
+P = 128
+NPASS = IN // 512
+NPAIR = L // 256
+TPB = 5
+D_EVEN = 2
+D_ODD = 2
+D_HEAD = 6
+KV = IN - 512
+
+
+def tile_grucellstack_pa_kernel(tc, x_in, h0, gh0, w_bytes, w_scale, b_ih0, out):
+    nc = tc.nc
+    with ExitStack() as ctx:
+        const = ctx.enter_context(tc.tile_pool(name="const", bufs=1))
+        wpool = ctx.enter_context(tc.tile_pool(name="wpool", bufs=1))
+        work = ctx.enter_context(tc.tile_pool(name="work", bufs=3))
+        ep = ctx.enter_context(tc.tile_pool(name="ep", bufs=2))
+        psum = ctx.enter_context(tc.psum_pool(name="psum", bufs=1))
+        ctx.enter_context(tc.manual_schedule())
+
+        w_view = w_bytes.rearrange("(g j p) k -> p g j k", g=3, p=P)
+        wq = {}
+        wqs = {}
+        for J in range(NPAIR):
+            wqs[J] = wpool.tile([P, 4, 512], U8, name="wqs_%d" % J)
+            for g in range(3):
+                wq[(J, g)] = wpool.tile([P, 2, KV if g < 2 else IN], U8, name="wq_%d_%d" % (J, g))
+        sc = const.tile([P, IN], F32, name="sc")
+        s_t = const.tile([P, 4, 4], F32, name="s_t")
+        x_sb = const.tile([P, 2, IN], BF16, name="x_sb")
+        h_sb = const.tile([P, 2, L], BF16, name="h_sb")
+        gh_sb = {}
+        for g in range(3):
+            gh_sb[g] = const.tile([P, 2, L], BF16, name="gh_sb_%d" % g)
+        b_rows = const.tile([P, P], BF16, name="b_rows")
+        warm = const.tile([P, 1], F32, name="warm")
+        warm2 = const.tile([P, 1], F32, name="warm2")
+
+        nc.vector.memset(warm[:], 0.0)
+        nc.vector.memset(b_rows[:], 0.0)
+        ones = const.tile([P, 2048], BF16, name="ones", align_bytes=64)
+        fcodes = const.tile([P, 512], U32, name="fcodes", align_bytes=64)
+        fplane = const.tile([P, 512], U8, name="fplane", align_bytes=64)
+        nc.vector.memset(ones[:].bitcast(mybir.dt.int32), 1065369472)
+        nc.vector.quantize_mx(out=fcodes[:].bitcast(FP8X4), scales=fplane[:], in_=ones[:])
+        nc.scalar.activation(out=warm2[:], in_=warm[:], func=ACT.Sigmoid)
+
+        def load_sc(c):
+            nc.sync.dma_start(
+                out=sc[:, c * 512:(c + 1) * 512],
+                in_=w_scale[0:1, c * 512:(c + 1) * 512].rearrange("o k -> (o k)").partition_broadcast(P),
+            )
+
+        def load_s(J):
+            for g in range(2):
+                nc.sync.dma_start(out=wqs[J][:, 2 * g:2 * g + 2, :], in_=w_view[:, g, 2 * J:2 * J + 2, KV:IN])
+
+        def load_v(J, g):
+            nc.sync.dma_start(out=wq[(J, g)][:], in_=w_view[:, g, 2 * J:2 * J + 2, 0:(KV if g < 2 else IN)])
+
+        nc.sync.dma_start(out=wq[(0, 0)][:, 0, :], in_=w_view[:, 0, 0, 0:KV])
+        load_sc(0)
+        load_s(0)
+        load_sc(1)
+        load_sc(2)
+        nc.sync.dma_start(out=s_t[:], in_=w_scale.rearrange("o (g p t) -> p (o g) t", p=P, t=4))
+        nc.sync.dma_start(out=wq[(0, 0)][:, 1, :], in_=w_view[:, 0, 1, 0:KV])
+        x_view = x_in.rearrange("(h p) k -> p h k", p=P)
+        for h in range(2):
+            nc.sync.dma_start(out=x_sb[:, h, :], in_=x_view[:, h, :])
+        load_v(0, 1)
+        load_sc(3)
+        nc.sync.dma_start(out=b_rows[0:36, :], in_=b_ih0.rearrange("(c p) -> c p", p=P))
+        gh_view = gh0.rearrange("(h p) (g c) -> p h g c", p=P, g=3)
+        nc.sync.dma_start(out=gh_sb[0][:], in_=gh_view[:, :, 0, :])
+        nc.sync.dma_start(out=gh_sb[2][:], in_=gh_view[:, :, 2, :])
+        load_v(0, 2)
+        load_s(1)
+        nc.sync.dma_start(out=h_sb[:], in_=h0.rearrange("(h p) c -> p h c", p=P))
+        nc.sync.dma_start(out=gh_sb[1][:], in_=gh_view[:, :, 1, :])
+        for J in range(1, NPAIR):
+            if J + 1 < NPAIR:
+                load_s(J + 1)
+            for g in range(3):
+                load_v(J, g)
+
+        ident_f = const.tile([P, P], F32, name="ident_f")
+        make_identity(nc, ident_f[:])
+        ident_b = const.tile([P, P], BF16, name="ident_b")
+        make_identity(nc, ident_b[:])
+
+        xgrp = const.tile([P, NPASS * B * 4], BF16, name="xgrp", align_bytes=64)
+        xcodes = const.tile([P, NPASS * B], U32, name="xcodes", align_bytes=64)
+        xplane = const.tile([P, NPASS * B], U8, name="xplane", align_bytes=64)
+        bias_sb = const.tile([P, 36], F32, name="bias_sb")
+        negb = const.tile([P, 12], F32, name="negb")
+
+        NT = 6 * NPAIR
+        NU = NT // 2
+        st = {}
+
+        def is_sr(i):
+            return (i % 6) < 4
+
+        def get_grp(m):
+            if ("grp", m) not in st:
+                st[("grp", m)] = work.tile([P, 2, IN], BF16, name="grp", bufs=4, align_bytes=64)
+            return st[("grp", m)]
+
+        def get_acc(m):
+            if ("acc", m) not in st:
+                st[("acc", m)] = psum.tile([P, 512], F32, name="acc_%d" % (m % 3), tag="acc_%d" % (m % 3), bufs=1)
+            return st[("acc", m)]
+
+        def sr_cast(J):
+            wc = work.tile([P, 4 * 512], BF16, name="wc", bufs=2)
+            st[("wc", J)] = wc
+            nc.scalar.copy(out=wc[:], in_=wqs[J][:].rearrange("p q k -> p (q k)").bitcast(FP8))
+
+        def sr_turn(J):
+            wcw = st[("wc", J)][:].bitcast(F32)
+            for u in range(2):
+                tq = psum.tile([P, 512], F32, name="tq", tag="tp", bufs=TPB)
+                st[("tq", J, u)] = tq
+                for q in range(4):
+                    nc.tensor.transpose(tq[:, q * P:(q + 1) * P], wcw[:, q * 256 + u:(q + 1) * 256:2], ident_f[:])
+
+        def sr_scale(J, u):
+            if u == 0:
+                st[("pl", J)] = work.tile([P, 4 * 512], BF16, name="pl", bufs=2)
+            pl = st[("pl", J)]
+            halves = st[("tq", J, u)][:].bitcast(BF16)
+            for e in range(2):
+                t = 2 * u + e
+                nc.scalar.activation(
+                    out=pl[:, t * 512:(t + 1) * 512], in_=halves[:, e:1024:2],
+                    func=ACT.Copy, scale=s_t[:, 3, t:t + 1],
+                )
+
+        def sr_weave(J, g):
+            grp = get_grp(3 * J + g)
+            nc.scalar.copy(
+                out=grp[:, :, KV:IN].rearrange("p j (c t) -> p j c t", t=4),
+                in_=st[("pl", J)][:].rearrange("p (t q c) -> p q c t", t=4, q=4)[:, 2 * g:2 * g + 2, :, :],
+            )
+
+        def tt(i):
+            J, g, jj = i // 6, (i % 6) // 2, i % 2
+            wb = work.tile([P, IN], BF16, name="wb", bufs=3)
+            st[("wb", i)] = wb
+            src = wq[(J, g)][:, jj, :].bitcast(FP8)
+            width = KV if is_sr(i) else IN
+            w = 512 if i == 0 else width
+            for c in range(width // w):
+                nc.vector.tensor_tensor(
+                    out=wb[:, c * w:(c + 1) * w], in0=src[:, c * w:(c + 1) * w],
+                    in1=sc[:, c * w:(c + 1) * w], op=ALU.mult,
+                )
+
+        def tr(i):
+            words = st[("wb", i)][:].bitcast(F32)
+            gw = get_grp(i // 2)[:, i % 2, :].bitcast(F32)
+            npass = 3 if is_sr(i) else 4
+            tpa = psum.tile([P, 512], F32, name="tpa", tag="tp", bufs=TPB)
+            tpb = psum.tile([P, 512], F32, name="tpb", tag="tp", bufs=TPB)
+            for g in range(npass):
+                bank = tpa if g < 2 else tpb
+                for u in range(2):
+                    col = ((g % 2) * 2 + u) * P
+                    nc.tensor.transpose(bank[:, col:col + P], words[:, 256 * g + u:256 * (g + 1):2], ident_f[:])
+            nc.scalar.copy(
+                out=gw[:, 0:512].rearrange("p (g c u) -> p g c u", g=2, u=2),
+                in_=tpa[:].rearrange("p (g u c) -> p g c u", g=2, u=2),
+            )
+            if npass == 3:
+                nc.scalar.copy(
+                    out=gw[:, 512:768].rearrange("p (c u) -> p c u", u=2),
+                    in_=tpb[:, 0:256].rearrange("p (u c) -> p c u", u=2),
+                )
+            else:
+                nc.scalar.copy(
+                    out=gw[:, 512:1024].rearrange("p (g c u) -> p g c u", g=2, u=2),
+                    in_=tpb[:].rearrange("p (g u c) -> p g c u", g=2, u=2),
+                )
+
+        def qz(m):
+            codes = work.tile([P, 1024], U32, name="codes", bufs=2, align_bytes=64)
+            plane = work.tile([P, 1024], U8, name="plane", bufs=2, align_bytes=64)
+            st[("codes", m)] = codes
+            st[("plane", m)] = plane
+            nc.vector.quantize_mx(
+                out=codes[:].bitcast(FP8X4), scales=plane[:], in_=st[("grp", m)][:].rearrange("p j k -> p (j k)"),
+            )
+
+        def mm(m, jj):
+            acc = get_acc(m)
+            codes = st[("codes", m)]
+            plane = st[("plane", m)]
+            for k in range(NPASS):
+                col = jj * 512 + k * P
+                nc.tensor.matmul_mx(
+                    out=acc[:, jj * B:(jj + 1) * B],
+                    lhsT=codes[:, col:col + P].bitcast(FP8X4),
+                    lhsT_scale=plane[:, col:col + P],
+                    rhs=xcodes[:, k * B:(k + 1) * B].bitcast(FP8X4),
+                    rhs_scale=xplane[:, k * B:(k + 1) * B],
+                    start=(k == 0), stop=(k == NPASS - 1),
+                )
+
+        def dummies(m, n):
+            acc = get_acc(m)
+            for k in range(n):
+                nc.tensor.matmul_mx(
+                    out=acc[:],
+                    lhsT=fcodes[:, 0:P].bitcast(FP8X4), lhsT_scale=fplane[:, 0:P],
+                    rhs=fcodes[:].bitcast(FP8X4), rhs_scale=fplane[:],
+                    start=True, stop=True,
+                )
+
+        def x_turn():
+            xgw = xgrp[:].bitcast(F32)
+            for g in range(NPASS):
+                tpx = psum.tile([P, 512], F32, name="tpx", tag="tp", bufs=TPB)
+                for u in range(2):
+                    for h in range(2):
+                        col = (u * 2 + h) * P
+                        nc.tensor.transpose(
+                            tpx[:, col:col + P],
+                            x_sb[:, h, :].bitcast(F32)[:, 256 * g + u:256 * (g + 1):2], ident_f[:],
+                        )
+                nc.scalar.copy(
+                    out=xgw[:, g * 512:(g + 1) * 512].rearrange("p (r u) -> p r u", u=2),
+                    in_=tpx[:].rearrange("p (u r) -> p r u", u=2),
+                )
+
+        def x_quant():
+            nc.vector.quantize_mx(out=xcodes[:].bitcast(FP8X4), scales=xplane[:], in_=xgrp[:])
+
+        def biaspath():
+            tpv = psum.tile([P, 1024], BF16, name="tpv", tag="tp", bufs=TPB)
+            nc.tensor.transpose(tpv[:, 0:P], b_rows[:], ident_b[:])
+            nc.scalar.copy(out=bias_sb[:], in_=tpv[:, 0:36])
+            nc.scalar.mul(out=negb[:], in_=bias_sb[:, 12:24], mul=-1.0)
+
+        def ghprep(J, nm):
+            srcs = (gh_sb[0], gh_sb[2]) if nm == "gA" else (gh_sb[1], h_sb)
+            tg = psum.tile([P, 1024], BF16, name="tg", tag="tp", bufs=TPB)
+            for s, src in enumerate(srcs):
+                for jj in range(2):
+                    for h in range(2):
+                        col = s * 512 + jj * 256 + h * P
+                        blk = (2 * J + jj) * P
+                        nc.tensor.matmul(out=tg[:, col:col + P], lhsT=src[:, h, blk:blk + P], rhs=ident_b[:], start=True, stop=True)
+            gt = ep.tile([P, 1024], BF16, name=nm)
+            nc.scalar.copy(out=gt[:], in_=tg[:])
+            st[(nm, J)] = gt
+
+        def act2(dst, src, func, btile, c0, scale):
+            for jj in range(2):
+                nc.scalar.activation(
+                    out=dst[:, jj * B:(jj + 1) * B], in_=src[:, jj * B:(jj + 1) * B],
+                    func=func, bias=btile[:, c0 + jj:c0 + jj + 1], scale=scale,
+                )
+
+        def v1(J):
+            a_r = ep.tile([P, 512], F32, name="a_r")
+            nc.vector.tensor_tensor(out=a_r[:], in0=st[("acc", 3 * J)][:], in1=st[("gA", J)][:, 0:512], op=ALU.add)
+            r = a_r
+            act2(r, a_r, ACT.Sigmoid, bias_sb, 2 * J, 1.0)
+            st[("r", J)] = r
+
+        def v3(J):
+            t = st[("r", J)]
+            nc.vector.tensor_tensor(out=t[:], in0=st[("r", J)][:], in1=st[("gA", J)][:, 512:1024], op=ALU.mult)
+            st[("t", J)] = t
+
+        def v2(J):
+            a_z = ep.tile([P, 512], F32, name="a_z")
+            nc.vector.tensor_tensor(out=a_z[:], in0=st[("acc", 3 * J + 1)][:], in1=st[("gB", J)][:, 0:512], op=ALU.add)
+            z = ep.tile([P, 512], F32, name="z")
+            act2(z, a_z, ACT.Sigmoid, bias_sb, 12 + 2 * J, 1.0)
+            u = a_z
+            act2(u, a_z, ACT.Sigmoid, negb, 2 * J, -1.0)
+            st[("z", J)] = z
+            st[("u", J)] = u
+
+        def vzh(J):
+            zh = st[("z", J)]
+            nc.vector.tensor_tensor(out=zh[:], in0=st[("z", J)][:], in1=st[("gB", J)][:, 512:1024], op=ALU.mult)
+            st[("zh", J)] = zh
+
+        def v4(J):
+            a_n = ep.tile([P, 512], F32, name="a_n")
+            nc.vector.tensor_tensor(out=a_n[:], in0=st[("acc", 3 * J + 2)][:], in1=st[("t", J)][:], op=ALU.add)
+            n = a_n
+            act2(n, a_n, ACT.Tanh, bias_sb, 24 + 2 * J, 1.0)
+            st[("n", J)] = n
+
+        def vun(J):
+            un = st[("u", J)]
+            nc.vector.tensor_tensor(out=un[:], in0=st[("u", J)][:], in1=st[("n", J)][:], op=ALU.mult)
+            st[("un", J)] = un
+
+        out_view = out.rearrange("(h p) c -> p h c", p=P)
+
+        def finish(J):
+            tpo = psum.tile([P, 512], F32, name="tpo", tag="tp", bufs=TPB)
+            for h in range(2):
+                for jj in range(2):
+                    dst = tpo[:, h * 256 + jj * P:h * 256 + (jj + 1) * P]
+                    blk = slice(jj * 256 + h * P, jj * 256 + (h + 1) * P)
+                    nc.tensor.matmul(out=dst, lhsT=st[("zh", J)][:, blk], rhs=ident_f[:], is_transpose=True, start=True, stop=False)
+                    nc.tensor.matmul(out=dst, lhsT=st[("un", J)][:, blk], rhs=ident_f[:], is_transpose=True, start=False, stop=True)
+            o_sb = ep.tile([P, 512], F32, name="o_sb")
+            nc.scalar.copy(out=o_sb[:], in_=tpo[:])
+            nc.sync.dma_start(
+                out=out_view[:, :, J * 256:(J + 1) * 256],
+                in_=o_sb[:].rearrange("p (h c) -> p h c", h=2),
+            )
+
+        dummies(0, D_HEAD)
+        sr_cast(0)
+        for i in range(-2, NT + 14):
+            for J in range(NPAIR):
+                off = i - 6 * J
+                if off == (15 if J == 0 else 13):
+                    finish(J)
+            if 0 <= i < NT:
+                tt(i)
+                if i == 1:
+                    x_turn()
+                tr(i)
+            for J in range(NPAIR):
+                off = i - 6 * J
+                if off == (0 if J == 0 else -3):
+                    sr_turn(J)
+                if off == (0 if J == 0 else -3):
+                    sr_scale(J, 0)
+                if off == (0 if J == 0 else -3):
+                    sr_scale(J, 1)
+                if off == (0 if J == 0 else -2):
+                    sr_weave(J, 0)
+                if off == (2 if J == 0 else 0):
+                    sr_weave(J, 1)
+            if i == 2:
+                biaspath()
+            if i == 2:
+                x_quant()
+            if i >= 3 and i % 2 == 1 and (i - 3) // 2 < NU:
+                qz((i - 3) // 2)
+                mm((i - 3) // 2, 0)
+            if i >= 4 and i % 2 == 0 and (i - 4) // 2 < NU:
+                mm((i - 4) // 2, 1)
+            for J in range(NPAIR):
+                off = i - 6 * J
+                if off == (3 if J == 0 else -2):
+                    ghprep(J, "gA")
+                if off == (5 if J == 0 else 2):
+                    ghprep(J, "gB")
+            if 0 <= i < NT:
+                dummies(max(0, min(NU - 1, (i - 3) // 2 + 1)), D_EVEN if i % 2 == 0 else D_ODD)
+            for J in range(NPAIR):
+                off = i - 6 * J
+                if off == (5 if J == 0 else 5):
+                    v1(J)
+                if off == (8 if J == 0 else 8):
+                    v3(J)
+                if off == (8 if J == 0 else 7):
+                    v2(J)
+                if off == (11 if J == 0 else 11):
+                    vzh(J)
+                if off == (9 if J == 0 else 9):
+                    v4(J)
+                if off == (11 if J == 0 else 11):
+                    vun(J)
+                if J > 0 and off == -5:
+                    sr_cast(J)

@@ -110,7 +110,6 @@ def tile_grucellstack_pa_kernel(tc, x_in, h0, gh0, w_bytes, w_scale, b_ih0, out)
         xcodes = const.tile([P, NPASS * B], U32, name="xcodes", align_bytes=64)
         xplane = const.tile([P, NPASS * B], U8, name="xplane", align_bytes=64)
         bias_sb = const.tile([P, 36], F32, name="bias_sb")
-        negb = const.tile([P, 12], F32, name="negb")
 
         NT = 6 * NPAIR
         NU = NT // 2
@@ -257,7 +256,6 @@ def tile_grucellstack_pa_kernel(tc, x_in, h0, gh0, w_bytes, w_scale, b_ih0, out)
             tpv = psum.tile([P, 1024], BF16, name="tpv", tag="tp", bufs=TPB)
             nc.tensor.transpose(tpv[:, 0:P], b_rows[:], ident_b[:])
             nc.scalar.copy(out=bias_sb[:], in_=tpv[:, 0:36])
-            nc.scalar.mul(out=negb[:], in_=bias_sb[:, 12:24], mul=-1.0)
 
         def ghprep(J, nm):
             srcs = (gh_sb[0], gh_sb[2]) if nm == "gA" else (gh_sb[1], h_sb)
@@ -294,17 +292,9 @@ def tile_grucellstack_pa_kernel(tc, x_in, h0, gh0, w_bytes, w_scale, b_ih0, out)
         def v2(J):
             a_z = ep.tile([P, 512], F32, name="a_z")
             nc.vector.tensor_tensor(out=a_z[:], in0=st[("acc", 3 * J + 1)][:], in1=st[("gB", J)][:, 0:512], op=ALU.add)
-            z = ep.tile([P, 512], F32, name="z")
+            z = a_z
             act2(z, a_z, ACT.Sigmoid, bias_sb, 12 + 2 * J, 1.0)
-            u = a_z
-            act2(u, a_z, ACT.Sigmoid, negb, 2 * J, -1.0)
             st[("z", J)] = z
-            st[("u", J)] = u
-
-        def vzh(J):
-            zh = st[("z", J)]
-            nc.vector.tensor_tensor(out=zh[:], in0=st[("z", J)][:], in1=st[("gB", J)][:, 512:1024], op=ALU.mult)
-            st[("zh", J)] = zh
 
         def v4(J):
             a_n = ep.tile([P, 512], F32, name="a_n")
@@ -313,10 +303,15 @@ def tile_grucellstack_pa_kernel(tc, x_in, h0, gh0, w_bytes, w_scale, b_ih0, out)
             act2(n, a_n, ACT.Tanh, bias_sb, 24 + 2 * J, 1.0)
             st[("n", J)] = n
 
-        def vun(J):
-            un = st[("u", J)]
-            nc.vector.tensor_tensor(out=un[:], in0=st[("u", J)][:], in1=st[("n", J)][:], op=ALU.mult)
-            st[("un", J)] = un
+        def vd(J):
+            d = ep.tile([P, 512], F32, name="d")
+            nc.vector.tensor_tensor(out=d[:], in0=st[("gB", J)][:, 512:1024], in1=st[("n", J)][:], op=ALU.subtract)
+            st[("d", J)] = d
+
+        def ve(J):
+            e = st[("d", J)]
+            nc.vector.tensor_tensor(out=e[:], in0=st[("d", J)][:], in1=st[("z", J)][:], op=ALU.mult)
+            st[("e", J)] = e
 
         out_view = out.rearrange("(h p) c -> p h c", p=P)
 
@@ -326,8 +321,8 @@ def tile_grucellstack_pa_kernel(tc, x_in, h0, gh0, w_bytes, w_scale, b_ih0, out)
                 for jj in range(2):
                     dst = tpo[:, h * 256 + jj * P:h * 256 + (jj + 1) * P]
                     blk = slice(jj * 256 + h * P, jj * 256 + (h + 1) * P)
-                    nc.tensor.matmul(out=dst, lhsT=st[("zh", J)][:, blk], rhs=ident_f[:], is_transpose=True, start=True, stop=False)
-                    nc.tensor.matmul(out=dst, lhsT=st[("un", J)][:, blk], rhs=ident_f[:], is_transpose=True, start=False, stop=True)
+                    nc.tensor.matmul(out=dst, lhsT=st[("n", J)][:, blk], rhs=ident_f[:], is_transpose=True, start=True, stop=False)
+                    nc.tensor.matmul(out=dst, lhsT=st[("e", J)][:, blk], rhs=ident_f[:], is_transpose=True, start=False, stop=True)
             o_sb = ep.tile([P, 512], F32, name="o_sb")
             nc.scalar.copy(out=o_sb[:], in_=tpo[:])
             nc.sync.dma_start(
@@ -384,11 +379,11 @@ def tile_grucellstack_pa_kernel(tc, x_in, h0, gh0, w_bytes, w_scale, b_ih0, out)
                     v3(J)
                 if off == (8 if J == 0 else 7):
                     v2(J)
-                if off == (11 if J == 0 else 11):
-                    vzh(J)
                 if off == (9 if J == 0 else 9):
                     v4(J)
-                if off == (11 if J == 0 else 11):
-                    vun(J)
+                if off == 10:
+                    vd(J)
+                if off == 11:
+                    ve(J)
                 if J > 0 and off == -5:
                     sr_cast(J)

@@ -18,11 +18,38 @@ FLOPS = 2 * B * IN * 3 * L
 P = 128
 NPASS = IN // 512
 NPAIR = L // 256
-TPB = 5
-D_EVEN = 2
-D_ODD = 2
-D_HEAD = 6
+NT = 6 * NPAIR
+NU = NT // 2
 KV = IN - 512
+GATE = (2, 0, 1)
+TPB = 4
+NACC = 2
+TBB = 2
+D_HEAD = 6
+D_SLOT = 2
+S_X = 2
+S_XQ = 5
+S_CAST = (-1, -1)
+S_TURN = 0
+S_SCALE = (0, 0)
+S_WEAVE = (2, 3)
+S_HEAD = 1
+QL = 5
+GRPB = 5
+QCUT = (4, 7)
+D_EX = 2
+D_OPEN = 2
+D_BACK = 3
+D_SIG = 4
+D_BACKN = 6
+D_V3 = 5
+D_V4 = 7
+D_TH = 8
+D_VD = 9
+D_VE = 9
+D_VO = 11
+ORDER = ((0, 1, 2), (0, 1, 2), (0, 1, 2), (0, 1, 2), (0, 1, 2), (1, 0, 2))
+S_RFIRST = -1
 
 
 def tile_grucellstack_pa_kernel(tc, x_in, h0, gh0, w_bytes, w_scale, b_ih0, out):
@@ -41,7 +68,7 @@ def tile_grucellstack_pa_kernel(tc, x_in, h0, gh0, w_bytes, w_scale, b_ih0, out)
         for J in range(NPAIR):
             wqs[J] = wpool.tile([P, 4, 512], U8, name="wqs_%d" % J)
             for g in range(3):
-                wq[(J, g)] = wpool.tile([P, 2, KV if g < 2 else IN], U8, name="wq_%d_%d" % (J, g))
+                wq[(J, g)] = wpool.tile([P, 2, KV if g > 0 else IN], U8, name="wq_%d_%d" % (J, g))
         sc = const.tile([P, IN], F32, name="sc")
         s_t = const.tile([P, 4, 4], F32, name="s_t")
         x_sb = const.tile([P, 2, IN], BF16, name="x_sb")
@@ -69,37 +96,48 @@ def tile_grucellstack_pa_kernel(tc, x_in, h0, gh0, w_bytes, w_scale, b_ih0, out)
             )
 
         def load_s(J):
-            for g in range(2):
-                nc.sync.dma_start(out=wqs[J][:, 2 * g:2 * g + 2, :], in_=w_view[:, g, 2 * J:2 * J + 2, KV:IN])
+            for s in range(2):
+                nc.sync.dma_start(out=wqs[J][:, 2 * s:2 * s + 2, :], in_=w_view[:, GATE[s + 1], 2 * J:2 * J + 2, KV:IN])
 
         def load_v(J, g):
-            nc.sync.dma_start(out=wq[(J, g)][:], in_=w_view[:, g, 2 * J:2 * J + 2, 0:(KV if g < 2 else IN)])
+            nc.sync.dma_start(out=wq[(J, g)][:], in_=w_view[:, GATE[g], 2 * J:2 * J + 2, 0:(KV if g > 0 else IN)])
 
-        nc.sync.dma_start(out=wq[(0, 0)][:, 0, :], in_=w_view[:, 0, 0, 0:KV])
+        x_view = x_in.rearrange("(h p) k -> p h k", p=P)
+        gh_view = gh0.rearrange("(h p) (g c) -> p h g c", p=P, g=3)
+
+        def load_x(h):
+            nc.sync.dma_start(out=x_sb[:, h, :], in_=x_view[:, h, :])
+
+        def load_gh(g):
+            nc.sync.dma_start(out=gh_sb[g][:], in_=gh_view[:, :, g, :])
+
+        nc.sync.dma_start(out=wq[(0, 0)][:, 0, 0:512], in_=w_view[:, GATE[0], 0, 0:512])
         load_sc(0)
-        load_s(0)
+        nc.sync.dma_start(out=wq[(0, 0)][:, 0, 512:IN], in_=w_view[:, GATE[0], 0, 512:IN])
         load_sc(1)
         load_sc(2)
-        nc.sync.dma_start(out=s_t[:], in_=w_scale.rearrange("o (g p t) -> p (o g) t", p=P, t=4))
-        nc.sync.dma_start(out=wq[(0, 0)][:, 1, :], in_=w_view[:, 0, 1, 0:KV])
-        x_view = x_in.rearrange("(h p) k -> p h k", p=P)
-        for h in range(2):
-            nc.sync.dma_start(out=x_sb[:, h, :], in_=x_view[:, h, :])
-        load_v(0, 1)
         load_sc(3)
+        nc.sync.dma_start(out=wq[(0, 0)][:, 1, :], in_=w_view[:, GATE[0], 1, :])
+        load_s(0)
+        load_v(0, 1)
+        load_x(0)
+        load_x(1)
+        nc.sync.dma_start(out=s_t[:], in_=w_scale.rearrange("o (g p t) -> p (o g) t", p=P, t=4))
         nc.sync.dma_start(out=b_rows[0:36, :], in_=b_ih0.rearrange("(c p) -> c p", p=P))
-        gh_view = gh0.rearrange("(h p) (g c) -> p h g c", p=P, g=3)
-        nc.sync.dma_start(out=gh_sb[0][:], in_=gh_view[:, :, 0, :])
-        nc.sync.dma_start(out=gh_sb[2][:], in_=gh_view[:, :, 2, :])
         load_v(0, 2)
+        load_gh(0)
+        load_v(1, 0)
+        load_gh(2)
+        load_gh(1)
         load_s(1)
+        load_v(1, 1)
         nc.sync.dma_start(out=h_sb[:], in_=h0.rearrange("(h p) c -> p h c", p=P))
-        nc.sync.dma_start(out=gh_sb[1][:], in_=gh_view[:, :, 1, :])
-        for J in range(1, NPAIR):
-            if J + 1 < NPAIR:
-                load_s(J + 1)
-            for g in range(3):
-                load_v(J, g)
+        load_v(1, 2)
+        for J in range(2, NPAIR):
+            load_v(J, ORDER[J][0])
+            load_s(J)
+            load_v(J, ORDER[J][1])
+            load_v(J, ORDER[J][2])
 
         ident_f = const.tile([P, P], F32, name="ident_f")
         make_identity(nc, ident_f[:])
@@ -111,32 +149,43 @@ def tile_grucellstack_pa_kernel(tc, x_in, h0, gh0, w_bytes, w_scale, b_ih0, out)
         xplane = const.tile([P, NPASS * B], U8, name="xplane", align_bytes=64)
         bias_sb = const.tile([P, 36], F32, name="bias_sb")
 
-        NT = 6 * NPAIR
-        NU = NT // 2
         st = {}
 
+        def role(m):
+            return ORDER[m // 3][m % 3]
+
+        def unit(J, ro):
+            return 3 * J + ORDER[J].index(ro)
+
         def is_sr(i):
-            return (i % 6) < 4
+            return role(i // 2) > 0
 
         def get_grp(m):
             if ("grp", m) not in st:
-                st[("grp", m)] = work.tile([P, 2, IN], BF16, name="grp", bufs=4, align_bytes=64)
+                st[("grp", m)] = work.tile([P, 2, IN], BF16, name="grp", bufs=GRPB, align_bytes=64)
             return st[("grp", m)]
 
         def get_acc(m):
             if ("acc", m) not in st:
-                st[("acc", m)] = psum.tile([P, 512], F32, name="acc_%d" % (m % 3), tag="acc_%d" % (m % 3), bufs=1)
+                st[("acc", m)] = psum.tile([P, 512], F32, name="acc_%d" % (m % NACC), tag="acc_%d" % (m % NACC), bufs=1)
             return st[("acc", m)]
 
-        def sr_cast(J):
-            wc = work.tile([P, 4 * 512], BF16, name="wc", bufs=2)
-            st[("wc", J)] = wc
-            nc.scalar.copy(out=wc[:], in_=wqs[J][:].rearrange("p q k -> p (q k)").bitcast(FP8))
+        def ring():
+            return psum.tile([P, 512], F32, name="tp", tag="tp", bufs=TPB)
+
+        def sr_cast(J, s):
+            if s == 0:
+                st[("wc", J)] = work.tile([P, 4 * 512], BF16, name="wc", bufs=2)
+            wc = st[("wc", J)]
+            nc.scalar.copy(
+                out=wc[:, s * 1024:(s + 1) * 1024],
+                in_=wqs[J][:, 2 * s:2 * s + 2, :].rearrange("p q k -> p (q k)").bitcast(FP8),
+            )
 
         def sr_turn(J):
             wcw = st[("wc", J)][:].bitcast(F32)
             for u in range(2):
-                tq = psum.tile([P, 512], F32, name="tq", tag="tp", bufs=TPB)
+                tq = ring()
                 st[("tq", J, u)] = tq
                 for q in range(4):
                     nc.tensor.transpose(tq[:, q * P:(q + 1) * P], wcw[:, q * 256 + u:(q + 1) * 256:2], ident_f[:])
@@ -153,15 +202,15 @@ def tile_grucellstack_pa_kernel(tc, x_in, h0, gh0, w_bytes, w_scale, b_ih0, out)
                     func=ACT.Copy, scale=s_t[:, 3, t:t + 1],
                 )
 
-        def sr_weave(J, g):
-            grp = get_grp(3 * J + g)
+        def sr_weave(J, s):
+            grp = get_grp(unit(J, s + 1))
             nc.scalar.copy(
                 out=grp[:, :, KV:IN].rearrange("p j (c t) -> p j c t", t=4),
-                in_=st[("pl", J)][:].rearrange("p (t q c) -> p q c t", t=4, q=4)[:, 2 * g:2 * g + 2, :, :],
+                in_=st[("pl", J)][:].rearrange("p (t q c) -> p q c t", t=4, q=4)[:, 2 * s:2 * s + 2, :, :],
             )
 
         def tt(i):
-            J, g, jj = i // 6, (i % 6) // 2, i % 2
+            J, g, jj = i // 6, role(i // 2), i % 2
             wb = work.tile([P, IN], BF16, name="wb", bufs=3)
             st[("wb", i)] = wb
             src = wq[(J, g)][:, jj, :].bitcast(FP8)
@@ -175,20 +224,24 @@ def tile_grucellstack_pa_kernel(tc, x_in, h0, gh0, w_bytes, w_scale, b_ih0, out)
 
         def tr(i):
             words = st[("wb", i)][:].bitcast(F32)
-            gw = get_grp(i // 2)[:, i % 2, :].bitcast(F32)
             npass = 3 if is_sr(i) else 4
-            tpa = psum.tile([P, 512], F32, name="tpa", tag="tp", bufs=TPB)
-            tpb = psum.tile([P, 512], F32, name="tpb", tag="tp", bufs=TPB)
+            tpa = ring()
+            tpb = ring()
+            st[("tp", i)] = (tpa, tpb)
             for g in range(npass):
                 bank = tpa if g < 2 else tpb
                 for u in range(2):
                     col = ((g % 2) * 2 + u) * P
                     nc.tensor.transpose(bank[:, col:col + P], words[:, 256 * g + u:256 * (g + 1):2], ident_f[:])
+
+        def te(i):
+            gw = get_grp(i // 2)[:, i % 2, :].bitcast(F32)
+            tpa, tpb = st[("tp", i)]
             nc.scalar.copy(
                 out=gw[:, 0:512].rearrange("p (g c u) -> p g c u", g=2, u=2),
                 in_=tpa[:].rearrange("p (g u c) -> p g c u", g=2, u=2),
             )
-            if npass == 3:
+            if is_sr(i):
                 nc.scalar.copy(
                     out=gw[:, 512:768].rearrange("p (c u) -> p c u", u=2),
                     in_=tpb[:, 0:256].rearrange("p (u c) -> p c u", u=2),
@@ -223,167 +276,174 @@ def tile_grucellstack_pa_kernel(tc, x_in, h0, gh0, w_bytes, w_scale, b_ih0, out)
                     start=(k == 0), stop=(k == NPASS - 1),
                 )
 
-        def dummies(m, n):
+        def dummies(m, n, lo):
             acc = get_acc(m)
-            for k in range(n):
+            for k in range(n * 512 // (512 - lo)):
                 nc.tensor.matmul_mx(
-                    out=acc[:],
+                    out=acc[:, lo:512],
                     lhsT=fcodes[:, 0:P].bitcast(FP8X4), lhsT_scale=fplane[:, 0:P],
-                    rhs=fcodes[:].bitcast(FP8X4), rhs_scale=fplane[:],
+                    rhs=fcodes[:, lo:512].bitcast(FP8X4), rhs_scale=fplane[:, lo:512],
                     start=True, stop=True,
                 )
 
-        def x_turn():
-            xgw = xgrp[:].bitcast(F32)
-            for g in range(NPASS):
-                tpx = psum.tile([P, 512], F32, name="tpx", tag="tp", bufs=TPB)
-                for u in range(2):
-                    for h in range(2):
-                        col = (u * 2 + h) * P
-                        nc.tensor.transpose(
-                            tpx[:, col:col + P],
-                            x_sb[:, h, :].bitcast(F32)[:, 256 * g + u:256 * (g + 1):2], ident_f[:],
-                        )
-                nc.scalar.copy(
-                    out=xgw[:, g * 512:(g + 1) * 512].rearrange("p (r u) -> p r u", u=2),
-                    in_=tpx[:].rearrange("p (u r) -> p r u", u=2),
-                )
+        def x_turn(g):
+            tpx = ring()
+            st[("tpx", g)] = tpx
+            for u in range(2):
+                for h in range(2):
+                    col = (u * 2 + h) * P
+                    nc.tensor.transpose(
+                        tpx[:, col:col + P],
+                        x_sb[:, h, :].bitcast(F32)[:, 256 * g + u:256 * (g + 1):2], ident_f[:],
+                    )
+
+        def x_exit(g):
+            nc.scalar.copy(
+                out=xgrp[:].bitcast(F32)[:, g * 512:(g + 1) * 512].rearrange("p (r u) -> p r u", u=2),
+                in_=st[("tpx", g)][:].rearrange("p (u r) -> p r u", u=2),
+            )
 
         def x_quant():
             nc.vector.quantize_mx(out=xcodes[:].bitcast(FP8X4), scales=xplane[:], in_=xgrp[:])
 
-        def biaspath():
+        def bias_turn():
             tpv = psum.tile([P, 1024], BF16, name="tpv", tag="tp", bufs=TPB)
+            st["tpv"] = tpv
             nc.tensor.transpose(tpv[:, 0:P], b_rows[:], ident_b[:])
-            nc.scalar.copy(out=bias_sb[:], in_=tpv[:, 0:36])
 
-        def ghprep(J, nm):
-            srcs = (gh_sb[0], gh_sb[2]) if nm == "gA" else (gh_sb[1], h_sb)
-            tg = psum.tile([P, 1024], BF16, name="tg", tag="tp", bufs=TPB)
-            for s, src in enumerate(srcs):
-                for jj in range(2):
-                    for h in range(2):
-                        col = s * 512 + jj * 256 + h * P
-                        blk = (2 * J + jj) * P
-                        nc.tensor.matmul(out=tg[:, col:col + P], lhsT=src[:, h, blk:blk + P], rhs=ident_b[:], start=True, stop=True)
-            gt = ep.tile([P, 1024], BF16, name=nm)
-            nc.scalar.copy(out=gt[:], in_=tg[:])
-            st[(nm, J)] = gt
+        def bias_exit():
+            nc.scalar.copy(out=bias_sb[:], in_=st["tpv"][:, 0:36])
 
-        def act2(dst, src, func, btile, c0, scale):
+        def ex(m):
+            J, g = m // 3, role(m)
+            eb = ep.tile([P, 512], F32, name="eb", bufs=4)
+            st[("eb", m)] = eb
             for jj in range(2):
+                c = GATE[g] * 12 + 2 * J + jj
                 nc.scalar.activation(
-                    out=dst[:, jj * B:(jj + 1) * B], in_=src[:, jj * B:(jj + 1) * B],
-                    func=func, bias=btile[:, c0 + jj:c0 + jj + 1], scale=scale,
+                    out=eb[:, jj * B:(jj + 1) * B], in_=st[("acc", m)][:, jj * B:(jj + 1) * B],
+                    func=ACT.Identity, bias=bias_sb[:, c:c + 1], scale=1.0,
                 )
 
-        def v1(J):
-            a_r = ep.tile([P, 512], F32, name="a_r")
-            nc.vector.tensor_tensor(out=a_r[:], in0=st[("acc", 3 * J)][:], in1=st[("gA", J)][:, 0:512], op=ALU.add)
-            r = a_r
-            act2(r, a_r, ACT.Sigmoid, bias_sb, 2 * J, 1.0)
-            st[("r", J)] = r
+        def tbank(m):
+            if TBB:
+                return psum.tile([P, 512], F32, name="tb", tag="tb", bufs=TBB)
+            return ring()
+
+        def gh_open(m):
+            J, g = m // 3, role(m)
+            tb = tbank(m)
+            st[("tb", m)] = tb
+            nc.tensor.matmul(
+                out=tb[:].rearrange("p (h c) -> p h c", h=2), lhsT=ident_b[:],
+                rhs=gh_sb[GATE[g]][:, :, J * 256:(J + 1) * 256], start=True, stop=False,
+            )
+
+        def back(m):
+            g = role(m)
+            if g == 0:
+                st[("tb", m)] = tbank(m)
+            tb = st[("tb", m)]
+            eb = st[("eb", m)]
+            for h in range(2):
+                for jj in range(2):
+                    nc.tensor.matmul(
+                        out=tb[:, h * 256 + jj * P:h * 256 + (jj + 1) * P],
+                        lhsT=eb[:, jj * 256 + h * P:jj * 256 + (h + 1) * P], rhs=ident_f[:], is_transpose=True,
+                        start=(g == 0), stop=(g == 0 or (h == 1 and jj == 1)),
+                    )
+
+        def cols(t, J):
+            return t[:, :, J * 256:(J + 1) * 256]
+
+        def v3d(t):
+            return t[:].rearrange("p (h c) -> p h c", h=2)
+
+        def sig(m):
+            J, g = m // 3, role(m)
+            nm = "r" if g == 1 else "z"
+            o = ep.tile([P, 512], F32, name=nm, bufs=3 if g == 1 else 2)
+            st[(nm, J)] = o
+            nc.scalar.activation(out=o[:], in_=st[("tb", m)][:], func=ACT.Sigmoid)
 
         def v3(J):
-            t = st[("r", J)]
-            nc.vector.tensor_tensor(out=t[:], in0=st[("r", J)][:], in1=st[("gA", J)][:, 512:1024], op=ALU.mult)
-            st[("t", J)] = t
-
-        def v2(J):
-            a_z = ep.tile([P, 512], F32, name="a_z")
-            nc.vector.tensor_tensor(out=a_z[:], in0=st[("acc", 3 * J + 1)][:], in1=st[("gB", J)][:, 0:512], op=ALU.add)
-            z = a_z
-            act2(z, a_z, ACT.Sigmoid, bias_sb, 12 + 2 * J, 1.0)
-            st[("z", J)] = z
+            r = st[("r", J)]
+            nc.vector.tensor_tensor(out=v3d(r), in0=v3d(r), in1=cols(gh_sb[2], J), op=ALU.mult)
 
         def v4(J):
-            a_n = ep.tile([P, 512], F32, name="a_n")
-            nc.vector.tensor_tensor(out=a_n[:], in0=st[("acc", 3 * J + 2)][:], in1=st[("t", J)][:], op=ALU.add)
-            n = a_n
-            act2(n, a_n, ACT.Tanh, bias_sb, 24 + 2 * J, 1.0)
-            st[("n", J)] = n
+            r = st[("r", J)]
+            nc.vector.tensor_tensor(out=r[:], in0=st[("tb", unit(J, 0))][:], in1=r[:], op=ALU.add)
+
+        def th(J):
+            r = st[("r", J)]
+            nc.scalar.activation(out=r[:], in_=r[:], func=ACT.Tanh)
 
         def vd(J):
             d = ep.tile([P, 512], F32, name="d")
-            nc.vector.tensor_tensor(out=d[:], in0=st[("gB", J)][:, 512:1024], in1=st[("n", J)][:], op=ALU.subtract)
             st[("d", J)] = d
+            nc.vector.tensor_tensor(out=v3d(d), in0=cols(h_sb, J), in1=v3d(st[("r", J)]), op=ALU.subtract)
 
         def ve(J):
-            e = st[("d", J)]
-            nc.vector.tensor_tensor(out=e[:], in0=st[("d", J)][:], in1=st[("z", J)][:], op=ALU.mult)
-            st[("e", J)] = e
+            d = st[("d", J)]
+            nc.vector.tensor_tensor(out=d[:], in0=d[:], in1=st[("z", J)][:], op=ALU.mult)
 
         out_view = out.rearrange("(h p) c -> p h c", p=P)
 
-        def finish(J):
-            tpo = psum.tile([P, 512], F32, name="tpo", tag="tp", bufs=TPB)
-            for h in range(2):
-                for jj in range(2):
-                    dst = tpo[:, h * 256 + jj * P:h * 256 + (jj + 1) * P]
-                    blk = slice(jj * 256 + h * P, jj * 256 + (h + 1) * P)
-                    nc.tensor.matmul(out=dst, lhsT=st[("n", J)][:, blk], rhs=ident_f[:], is_transpose=True, start=True, stop=False)
-                    nc.tensor.matmul(out=dst, lhsT=st[("e", J)][:, blk], rhs=ident_f[:], is_transpose=True, start=False, stop=True)
-            o_sb = ep.tile([P, 512], F32, name="o_sb")
-            nc.scalar.copy(out=o_sb[:], in_=tpo[:])
-            nc.sync.dma_start(
-                out=out_view[:, :, J * 256:(J + 1) * 256],
-                in_=o_sb[:].rearrange("p (h c) -> p h c", h=2),
-            )
+        def vo(J):
+            d = st[("d", J)]
+            nc.vector.tensor_tensor(out=d[:], in0=d[:], in1=st[("r", J)][:], op=ALU.add)
+            nc.sync.dma_start(out=out_view[:, :, J * 256:(J + 1) * 256], in_=v3d(d))
 
-        dummies(0, D_HEAD)
-        sr_cast(0)
-        for i in range(-2, NT + 14):
-            for J in range(NPAIR):
-                off = i - 6 * J
-                if off == (15 if J == 0 else 13):
-                    finish(J)
-            if 0 <= i < NT:
-                tt(i)
-                if i == 1:
-                    x_turn()
-                tr(i)
-            for J in range(NPAIR):
-                off = i - 6 * J
-                if off == (0 if J == 0 else -3):
-                    sr_turn(J)
-                if off == (0 if J == 0 else -3):
-                    sr_scale(J, 0)
-                if off == (0 if J == 0 else -3):
-                    sr_scale(J, 1)
-                if off == (0 if J == 0 else -2):
-                    sr_weave(J, 0)
-                if off == (2 if J == 0 else 0):
-                    sr_weave(J, 1)
-            if i == 2:
-                biaspath()
-            if i == 2:
-                x_quant()
-            if i >= 3 and i % 2 == 1 and (i - 3) // 2 < NU:
-                qz((i - 3) // 2)
-                mm((i - 3) // 2, 0)
-            if i >= 4 and i % 2 == 0 and (i - 4) // 2 < NU:
-                mm((i - 4) // 2, 1)
-            for J in range(NPAIR):
-                off = i - 6 * J
-                if off == (3 if J == 0 else -2):
-                    ghprep(J, "gA")
-                if off == (5 if J == 0 else 2):
-                    ghprep(J, "gB")
-            if 0 <= i < NT:
-                dummies(max(0, min(NU - 1, (i - 3) // 2 + 1)), D_EVEN if i % 2 == 0 else D_ODD)
-            for J in range(NPAIR):
-                off = i - 6 * J
-                if off == (5 if J == 0 else 5):
-                    v1(J)
-                if off == (8 if J == 0 else 8):
-                    v3(J)
-                if off == (8 if J == 0 else 7):
-                    v2(J)
-                if off == (9 if J == 0 else 9):
-                    v4(J)
-                if off == 10:
-                    vd(J)
-                if off == 11:
-                    ve(J)
-                if J > 0 and off == -5:
-                    sr_cast(J)
+        steps = []
+
+        def at(slot, place, fn, *args):
+            steps.append((slot, place, len(steps), fn, args))
+
+        def qs(m):
+            return 2 * m + QL - sum([1 for c in QCUT if m >= c])
+
+        at(-1, 0, dummies, 0, D_HEAD, 0)
+        for i in range(NT):
+            at(i, 10, tt, i)
+            at(i, 31, tr, i)
+            at(i, 40, te, i)
+            now = [m for m in range(NU) if qs(m) == i]
+            if now:
+                at(i, 64, dummies, now[0], D_SLOT, B)
+            else:
+                at(i, 64, dummies, min([m for m in range(NU) if qs(m) > i] + [NU - 1]), D_SLOT, 0)
+        for g in range(NPASS):
+            at(S_X, 41 + 2 * g, x_turn, g)
+            at(S_X, 42 + 2 * g, x_exit, g)
+        at(S_XQ, 49, x_quant)
+        at(S_X + 1, 41, bias_turn)
+        at(S_X + 1, 42, bias_exit)
+        for m in range(NU):
+            at(qs(m), 50, qz, m)
+            at(qs(m), 60, mm, m, 0)
+            at(qs(m) + 1, 60, mm, m, 1)
+            at(qs(m) + D_EX, 26 + m % 3, ex, m)
+        for J in range(NPAIR):
+            q = 6 * J + (S_HEAD if J == 0 else (S_RFIRST if ORDER[J][0] == 1 else 0))
+            for s in range(2):
+                at(q + S_CAST[s], 80 + s, sr_cast, J, s)
+            at(q + S_TURN, 32, sr_turn, J)
+            at(q + S_SCALE[0], 82, sr_scale, J, 0)
+            at(q + S_SCALE[1], 83, sr_scale, J, 1)
+            at(q + S_WEAVE[0], 84, sr_weave, J, 0)
+            at(q + S_WEAVE[1], 85, sr_weave, J, 1)
+            qr = qs(unit(J, 1))
+            qzz = qs(unit(J, 2))
+            for m in (unit(J, 1), unit(J, 2)):
+                at(qs(m) + D_OPEN, 62, gh_open, m)
+                at(qs(m) + D_BACK, 30, back, m)
+                at(qs(m) + D_SIG, 21 + m % 3, sig, m)
+            at(qr + D_BACKN, 30, back, unit(J, 0))
+            at(qr + D_V3, 70, v3, J)
+            at(qr + D_V4, 73, v4, J)
+            at(qr + D_TH, 20, th, J)
+            at(qr + D_VD, 71, vd, J)
+            at(qzz + D_VE, 74, ve, J)
+            at(qzz + D_VO, 72, vo, J)
+        for step in sorted(steps, key=lambda e: e[0:3]):
+            step[3](*step[4])

@@ -26,7 +26,7 @@ TPB = 4
 NACC = 2
 TBB = 2
 D_HEAD = 6
-D_SLOT = 2
+D_SLOT = 1
 S_X = 2
 S_XQ = 5
 S_CAST = (-1, -1)

@@ -26,7 +26,7 @@ TPB = 4
 NACC = 2
 TBB = 2
 D_HEAD = 6
-D_SLOT = 1
+D_SLOT = 0
 S_X = 2
 S_XQ = 5
 S_CAST = (-1, -1)

@@ -50,6 +50,12 @@ D_VE = 9
 D_VO = 11
 ORDER = ((0, 1, 2), (0, 1, 2), (0, 1, 2), (0, 1, 2), (0, 1, 2), (1, 0, 2))
 S_RFIRST = -1
+F_TOPEN = 0
+F_OPEN = 0
+K_LATE = 0
+N_V4 = 1
+DL = (2, 3, 30, 4, 5, 6, 7, 8, 9, 9, 11, 7)
+DL_LAST = (1, 2, 32, 3, 4, 5, 6, 7, 8, 7, 9, 6)
 
 
 def tile_grucellstack_pa_kernel(tc, x_in, h0, gh0, w_bytes, w_scale, b_ih0, out):
@@ -215,7 +221,7 @@ def tile_grucellstack_pa_kernel(tc, x_in, h0, gh0, w_bytes, w_scale, b_ih0, out)
             st[("wb", i)] = wb
             src = wq[(J, g)][:, jj, :].bitcast(FP8)
             width = KV if is_sr(i) else IN
-            w = 512 if i == 0 else width
+            w = 512 if i in (0, NT - 1) else width
             for c in range(width // w):
                 nc.vector.tensor_tensor(
                     out=wb[:, c * w:(c + 1) * w], in0=src[:, c * w:(c + 1) * w],
@@ -316,7 +322,7 @@ def tile_grucellstack_pa_kernel(tc, x_in, h0, gh0, w_bytes, w_scale, b_ih0, out)
 
         def ex(m):
             J, g = m // 3, role(m)
-            eb = ep.tile([P, 512], F32, name="eb", bufs=4)
+            eb = ep.tile([P, 512], F32, name="en" if g == 0 else "eb", bufs=2)
             st[("eb", m)] = eb
             for jj in range(2):
                 c = GATE[g] * 12 + 2 * J + jj
@@ -339,9 +345,17 @@ def tile_grucellstack_pa_kernel(tc, x_in, h0, gh0, w_bytes, w_scale, b_ih0, out)
                 rhs=gh_sb[GATE[g]][:, :, J * 256:(J + 1) * 256], start=True, stop=False,
             )
 
+        def t_open(J):
+            tb = tbank(J)
+            st[("tb", unit(J, 0))] = tb
+            nc.tensor.matmul(out=tb[:], lhsT=ident_f[:], rhs=st[("r", J)][:], start=True, stop=False)
+
+        def on_pe(J):
+            return J < NPAIR - N_V4
+
         def back(m):
-            g = role(m)
-            if g == 0:
+            lone = role(m) == 0 and not on_pe(m // 3)
+            if lone:
                 st[("tb", m)] = tbank(m)
             tb = st[("tb", m)]
             eb = st[("eb", m)]
@@ -350,7 +364,7 @@ def tile_grucellstack_pa_kernel(tc, x_in, h0, gh0, w_bytes, w_scale, b_ih0, out)
                     nc.tensor.matmul(
                         out=tb[:, h * 256 + jj * P:h * 256 + (jj + 1) * P],
                         lhsT=eb[:, jj * 256 + h * P:jj * 256 + (h + 1) * P], rhs=ident_f[:], is_transpose=True,
-                        start=(g == 0), stop=(g == 0 or (h == 1 and jj == 1)),
+                        start=lone, stop=(lone or (h == 1 and jj == 1)),
                     )
 
         def cols(t, J):
@@ -362,7 +376,7 @@ def tile_grucellstack_pa_kernel(tc, x_in, h0, gh0, w_bytes, w_scale, b_ih0, out)
         def sig(m):
             J, g = m // 3, role(m)
             nm = "r" if g == 1 else "z"
-            o = ep.tile([P, 512], F32, name=nm, bufs=3 if g == 1 else 2)
+            o = ep.tile([P, 512], F32, name=nm, bufs=3)
             st[(nm, J)] = o
             nc.scalar.activation(out=o[:], in_=st[("tb", m)][:], func=ACT.Sigmoid)
 
@@ -376,7 +390,7 @@ def tile_grucellstack_pa_kernel(tc, x_in, h0, gh0, w_bytes, w_scale, b_ih0, out)
 
         def th(J):
             r = st[("r", J)]
-            nc.scalar.activation(out=r[:], in_=r[:], func=ACT.Tanh)
+            nc.scalar.activation(out=r[:], in_=(st[("tb", unit(J, 0))] if on_pe(J) else r)[:], func=ACT.Tanh)
 
         def vd(J):
             d = ep.tile([P, 512], F32, name="d")
@@ -402,16 +416,26 @@ def tile_grucellstack_pa_kernel(tc, x_in, h0, gh0, w_bytes, w_scale, b_ih0, out)
         def qs(m):
             return 2 * m + QL - sum([1 for c in QCUT if m >= c])
 
+        def late(slot):
+            return slot + K_LATE if slot >= NT - K_LATE else slot
+
         at(-1, 0, dummies, 0, D_HEAD, 0)
+        plain = {}
+        for J in range(NPAIR):
+            dl = DL_LAST if J == NPAIR - 1 else DL
+            if J < NPAIR - N_V4:
+                plain[late(qs(unit(J, 1)) + dl[5])] = F_TOPEN
+            for ro in (1, 2):
+                plain[qs(unit(J, ro)) + dl[0]] = F_OPEN
         for i in range(NT):
             at(i, 10, tt, i)
             at(i, 31, tr, i)
             at(i, 40, te, i)
             now = [m for m in range(NU) if qs(m) == i]
             if now:
-                at(i, 64, dummies, now[0], D_SLOT, B)
+                at(i, 64, dummies, now[0], D_SLOT - plain.get(i, 0), B)
             else:
-                at(i, 64, dummies, min([m for m in range(NU) if qs(m) > i] + [NU - 1]), D_SLOT, 0)
+                at(i, 64, dummies, min([m for m in range(NU) if qs(m) > i] + [NU - 1]), D_SLOT - plain.get(i, 0), 0)
         for g in range(NPASS):
             at(S_X, 41 + 2 * g, x_turn, g)
             at(S_X, 42 + 2 * g, x_exit, g)
@@ -427,23 +451,27 @@ def tile_grucellstack_pa_kernel(tc, x_in, h0, gh0, w_bytes, w_scale, b_ih0, out)
             q = 6 * J + (S_HEAD if J == 0 else (S_RFIRST if ORDER[J][0] == 1 else 0))
             for s in range(2):
                 at(q + S_CAST[s], 80 + s, sr_cast, J, s)
-            at(q + S_TURN, 32, sr_turn, J)
+            at(q + S_TURN, 63, sr_turn, J)
             at(q + S_SCALE[0], 82, sr_scale, J, 0)
             at(q + S_SCALE[1], 83, sr_scale, J, 1)
             at(q + S_WEAVE[0], 84, sr_weave, J, 0)
             at(q + S_WEAVE[1], 85, sr_weave, J, 1)
             qr = qs(unit(J, 1))
             qzz = qs(unit(J, 2))
+            dl = DL_LAST if J == NPAIR - 1 else DL
             for m in (unit(J, 1), unit(J, 2)):
-                at(qs(m) + D_OPEN, 62, gh_open, m)
-                at(qs(m) + D_BACK, 30, back, m)
-                at(qs(m) + D_SIG, 21 + m % 3, sig, m)
-            at(qr + D_BACKN, 30, back, unit(J, 0))
-            at(qr + D_V3, 70, v3, J)
-            at(qr + D_V4, 73, v4, J)
-            at(qr + D_TH, 20, th, J)
-            at(qr + D_VD, 71, vd, J)
-            at(qzz + D_VE, 74, ve, J)
-            at(qzz + D_VO, 72, vo, J)
+                at(qs(m) + dl[0], 62, gh_open, m)
+                at(qs(m) + dl[1], dl[2], back, m)
+                at(qs(m) + dl[3], 21 + m % 3, sig, m)
+            at(late(qr + dl[6]), 30, back, unit(J, 0))
+            at(late(qr + dl[4]), 70, v3, J)
+            if on_pe(J):
+                at(late(qr + dl[5]), 62, t_open, J)
+            else:
+                at(late(qr + dl[11]), 73, v4, J)
+            at(late(qr + dl[7]), 20, th, J)
+            at(late(qr + dl[8]), 71, vd, J)
+            at(late(qzz + dl[9]), 74, ve, J)
+            at(late(qzz + dl[10]), 72, vo, J)
         for step in sorted(steps, key=lambda e: e[0:3]):
             step[3](*step[4])

@@ -22,9 +22,9 @@ NT = 6 * NPAIR
 NU = NT // 2
 KV = IN - 512
 GATE = (2, 0, 1)
-TPB = 4
+TPB = 3
 NACC = 2
-TBB = 2
+TBB = 3
 D_HEAD = 6
 D_SLOT = 0
 S_X = 2
@@ -55,7 +55,8 @@ F_OPEN = 0
 K_LATE = 0
 N_V4 = 1
 DL = (2, 3, 30, 4, 5, 6, 7, 8, 9, 9, 11, 7)
-DL_LAST = (1, 2, 32, 3, 4, 5, 6, 7, 8, 7, 9, 6)
+DL_LAST = (1, 2, 32, 3, 4, 5, 5, 7, 8, 7, 9, 6)
+N_VD = 2
 
 
 def tile_grucellstack_pa_kernel(tc, x_in, h0, gh0, w_bytes, w_scale, b_ih0, out):
@@ -149,6 +150,8 @@ def tile_grucellstack_pa_kernel(tc, x_in, h0, gh0, w_bytes, w_scale, b_ih0, out)
         make_identity(nc, ident_f[:])
         ident_b = const.tile([P, P], BF16, name="ident_b")
         make_identity(nc, ident_b[:])
+        ident_n = const.tile([P, P], F32, name="ident_n")
+        nc.scalar.mul(out=ident_n[:], in_=ident_f[:], mul=-1.0)
 
         xgrp = const.tile([P, NPASS * B * 4], BF16, name="xgrp", align_bytes=64)
         xcodes = const.tile([P, NPASS * B], U32, name="xcodes", align_bytes=64)
@@ -397,9 +400,23 @@ def tile_grucellstack_pa_kernel(tc, x_in, h0, gh0, w_bytes, w_scale, b_ih0, out)
             st[("d", J)] = d
             nc.vector.tensor_tensor(out=v3d(d), in0=cols(h_sb, J), in1=v3d(st[("r", J)]), op=ALU.subtract)
 
+        def pd(J):
+            tb = tbank(3 * J)
+            st[("pd", J)] = tb
+            nc.tensor.matmul(out=tb[:], lhsT=ident_n[:], rhs=st[("r", J)][:], start=True, stop=False)
+            nc.tensor.matmul(out=v3d(tb), lhsT=ident_b[:], rhs=cols(h_sb, J), start=False, stop=True)
+
+        def d_on_pe(J):
+            return J < NPAIR - N_VD
+
         def ve(J):
-            d = st[("d", J)]
-            nc.vector.tensor_tensor(out=d[:], in0=d[:], in1=st[("z", J)][:], op=ALU.mult)
+            if d_on_pe(J):
+                d = ep.tile([P, 512], F32, name="d")
+                st[("d", J)] = d
+                nc.vector.tensor_tensor(out=d[:], in0=st[("pd", J)][:], in1=st[("z", J)][:], op=ALU.mult)
+            else:
+                d = st[("d", J)]
+                nc.vector.tensor_tensor(out=d[:], in0=d[:], in1=st[("z", J)][:], op=ALU.mult)
 
         out_view = out.rearrange("(h p) c -> p h c", p=P)
 
@@ -470,7 +487,10 @@ def tile_grucellstack_pa_kernel(tc, x_in, h0, gh0, w_bytes, w_scale, b_ih0, out)
             else:
                 at(late(qr + dl[11]), 73, v4, J)
             at(late(qr + dl[7]), 20, th, J)
-            at(late(qr + dl[8]), 71, vd, J)
+            if d_on_pe(J):
+                at(late(qr + dl[8]), 62, pd, J)
+            else:
+                at(late(qr + dl[8]), 71, vd, J)
             at(late(qzz + dl[9]), 74, ve, J)
             at(late(qzz + dl[10]), 72, vo, J)
         for step in sorted(steps, key=lambda e: e[0:3]):

@@ -57,6 +57,8 @@ N_V4 = 1
 DL = (2, 3, 30, 4, 5, 6, 7, 8, 9, 9, 11, 7)
 DL_LAST = (1, 2, 32, 3, 4, 5, 5, 7, 8, 7, 9, 6)
 N_VD = 2
+SRR_EARLY = (2,)
+J_EARLY = 2
 
 
 def tile_grucellstack_pa_kernel(tc, x_in, h0, gh0, w_bytes, w_scale, b_ih0, out):
@@ -72,10 +74,17 @@ def tile_grucellstack_pa_kernel(tc, x_in, h0, gh0, w_bytes, w_scale, b_ih0, out)
         w_view = w_bytes.rearrange("(g j p) k -> p g j k", g=3, p=P)
         wq = {}
         wqs = {}
+
+        def srr(J):
+            return SRR_EARLY if J < J_EARLY else (1, 2)
+
+        def nq(J):
+            return 2 * len(srr(J))
+
         for J in range(NPAIR):
-            wqs[J] = wpool.tile([P, 4, 512], U8, name="wqs_%d" % J)
+            wqs[J] = wpool.tile([P, nq(J), 512], U8, name="wqs_%d" % J)
             for g in range(3):
-                wq[(J, g)] = wpool.tile([P, 2, KV if g > 0 else IN], U8, name="wq_%d_%d" % (J, g))
+                wq[(J, g)] = wpool.tile([P, 2, KV if g in srr(J) else IN], U8, name="wq_%d_%d" % (J, g))
         sc = const.tile([P, IN], F32, name="sc")
         s_t = const.tile([P, 4, 4], F32, name="s_t")
         x_sb = const.tile([P, 2, IN], BF16, name="x_sb")
@@ -103,11 +112,11 @@ def tile_grucellstack_pa_kernel(tc, x_in, h0, gh0, w_bytes, w_scale, b_ih0, out)
             )
 
         def load_s(J):
-            for s in range(2):
-                nc.sync.dma_start(out=wqs[J][:, 2 * s:2 * s + 2, :], in_=w_view[:, GATE[s + 1], 2 * J:2 * J + 2, KV:IN])
+            for s in range(len(srr(J))):
+                nc.sync.dma_start(out=wqs[J][:, 2 * s:2 * s + 2, :], in_=w_view[:, GATE[srr(J)[s]], 2 * J:2 * J + 2, KV:IN])
 
         def load_v(J, g):
-            nc.sync.dma_start(out=wq[(J, g)][:], in_=w_view[:, GATE[g], 2 * J:2 * J + 2, 0:(KV if g > 0 else IN)])
+            nc.sync.dma_start(out=wq[(J, g)][:], in_=w_view[:, GATE[g], 2 * J:2 * J + 2, 0:(KV if g in srr(J) else IN)])
 
         x_view = x_in.rearrange("(h p) k -> p h k", p=P)
         gh_view = gh0.rearrange("(h p) (g c) -> p h g c", p=P, g=3)
@@ -167,7 +176,7 @@ def tile_grucellstack_pa_kernel(tc, x_in, h0, gh0, w_bytes, w_scale, b_ih0, out)
             return 3 * J + ORDER[J].index(ro)
 
         def is_sr(i):
-            return role(i // 2) > 0
+            return role(i // 2) in srr(i // 6)
 
         def get_grp(m):
             if ("grp", m) not in st:
@@ -184,7 +193,7 @@ def tile_grucellstack_pa_kernel(tc, x_in, h0, gh0, w_bytes, w_scale, b_ih0, out)
 
         def sr_cast(J, s):
             if s == 0:
-                st[("wc", J)] = work.tile([P, 4 * 512], BF16, name="wc", bufs=2)
+                st[("wc", J)] = work.tile([P, nq(J) * 512], BF16, name="wc", bufs=2)
             wc = st[("wc", J)]
             nc.scalar.copy(
                 out=wc[:, s * 1024:(s + 1) * 1024],
@@ -194,28 +203,31 @@ def tile_grucellstack_pa_kernel(tc, x_in, h0, gh0, w_bytes, w_scale, b_ih0, out)
         def sr_turn(J):
             wcw = st[("wc", J)][:].bitcast(F32)
             for u in range(2):
-                tq = ring()
+                if u == 0 or nq(J) == 4:
+                    tq = ring()
                 st[("tq", J, u)] = tq
-                for q in range(4):
-                    nc.tensor.transpose(tq[:, q * P:(q + 1) * P], wcw[:, q * 256 + u:(q + 1) * 256:2], ident_f[:])
+                for q in range(nq(J)):
+                    col = (q + (2 * u if nq(J) == 2 else 0)) * P
+                    nc.tensor.transpose(tq[:, col:col + P], wcw[:, q * 256 + u:(q + 1) * 256:2], ident_f[:])
 
         def sr_scale(J, u):
             if u == 0:
-                st[("pl", J)] = work.tile([P, 4 * 512], BF16, name="pl", bufs=2)
+                st[("pl", J)] = work.tile([P, nq(J) * 512], BF16, name="pl", bufs=2)
             pl = st[("pl", J)]
             halves = st[("tq", J, u)][:].bitcast(BF16)
             for e in range(2):
                 t = 2 * u + e
+                lo = u * 512 if nq(J) == 2 else 0
                 nc.scalar.activation(
-                    out=pl[:, t * 512:(t + 1) * 512], in_=halves[:, e:1024:2],
+                    out=pl[:, t * nq(J) * P:(t + 1) * nq(J) * P], in_=halves[:, lo + e:lo + nq(J) * 256:2],
                     func=ACT.Copy, scale=s_t[:, 3, t:t + 1],
                 )
 
         def sr_weave(J, s):
-            grp = get_grp(unit(J, s + 1))
+            grp = get_grp(unit(J, srr(J)[s]))
             nc.scalar.copy(
                 out=grp[:, :, KV:IN].rearrange("p j (c t) -> p j c t", t=4),
-                in_=st[("pl", J)][:].rearrange("p (t q c) -> p q c t", t=4, q=4)[:, 2 * s:2 * s + 2, :, :],
+                in_=st[("pl", J)][:].rearrange("p (t q c) -> p q c t", t=4, q=nq(J))[:, 2 * s:2 * s + 2, :, :],
             )
 
         def tt(i):
@@ -466,13 +478,12 @@ def tile_grucellstack_pa_kernel(tc, x_in, h0, gh0, w_bytes, w_scale, b_ih0, out)
             at(qs(m) + D_EX, 26 + m % 3, ex, m)
         for J in range(NPAIR):
             q = 6 * J + (S_HEAD if J == 0 else (S_RFIRST if ORDER[J][0] == 1 else 0))
-            for s in range(2):
+            for s in range(len(srr(J))):
                 at(q + S_CAST[s], 80 + s, sr_cast, J, s)
+                at(q + S_WEAVE[srr(J)[s] - 1], 84 + s, sr_weave, J, s)
             at(q + S_TURN, 63, sr_turn, J)
             at(q + S_SCALE[0], 82, sr_scale, J, 0)
             at(q + S_SCALE[1], 83, sr_scale, J, 1)
-            at(q + S_WEAVE[0], 84, sr_weave, J, 0)
-            at(q + S_WEAVE[1], 85, sr_weave, J, 1)
             qr = qs(unit(J, 1))
             qzz = qs(unit(J, 2))
             dl = DL_LAST if J == NPAIR - 1 else DL

@@ -16,49 +16,42 @@ B, IN, L = 256, 2048, 1536
 FLOPS = 2 * B * IN * 3 * L
 
 P = 128
-NPASS = IN // 512
-NPAIR = L // 256
-NT = 6 * NPAIR
-NU = NT // 2
-KV = IN - 512
-GATE = (2, 0, 1)
-TPB = 3
-NACC = 2
-TBB = 3
-D_HEAD = 6
-D_SLOT = 0
-S_X = 2
-S_XQ = 5
-S_CAST = (-1, -1)
-S_TURN = 0
-S_SCALE = (0, 0)
-S_WEAVE = (2, 3)
-S_HEAD = 1
-QL = 5
-GRPB = 5
-QCUT = (4, 7)
-D_EX = 2
-D_OPEN = 2
-D_BACK = 3
-D_SIG = 4
-D_BACKN = 6
-D_V3 = 5
-D_V4 = 7
-D_TH = 8
-D_VD = 9
-D_VE = 9
-D_VO = 11
-ORDER = ((0, 1, 2), (0, 1, 2), (0, 1, 2), (0, 1, 2), (0, 1, 2), (1, 0, 2))
-S_RFIRST = -1
-F_TOPEN = 0
-F_OPEN = 0
-K_LATE = 0
-N_V4 = 1
-DL = (2, 3, 30, 4, 5, 6, 7, 8, 9, 9, 11, 7)
-DL_LAST = (1, 2, 32, 3, 4, 5, 5, 7, 8, 7, 9, 6)
-N_VD = 2
-SRR_EARLY = (2,)
-J_EARLY = 2
+K_PASS = 512
+PASSES = IN // K_PASS
+PAIRS = L // 256
+UNITS = 3 * PAIRS
+TILES = 2 * UNITS
+K_VECTOR = IN - K_PASS
+
+GN, GR, GZ = 0, 1, 2
+BLOCK = (2, 0, 1)
+
+ORDER = ((GN, GR, GZ),) * (PAIRS - 1) + ((GR, GN, GZ),)
+
+ROAD_EARLY, EARLY_PAIRS, ROAD = (GZ,), 2, (GR, GZ)
+
+PAIRS_SUM_ON_VECTOR, PAIRS_DIFF_ON_VECTOR = 1, 2
+
+SUM_BANKS, TURN_BANKS, BACK_BANKS = 2, 3, 3
+
+V_PRODUCT = 10
+S_TANH, S_SIGMOID, S_SUMS = 20, 21, 26
+T_BACK, T_TILE, T_BACK_LATE = 30, 31, 32
+S_TILE = 40
+X_FIRST = 41
+V_XQUANT, V_QUANT = 49, 50
+T_PASSES, T_PLAIN, T_ROAD = 60, 62, 63
+V_R_GH, V_H_N, V_OUT, V_SUM, V_Z_D = 70, 71, 72, 73, 74
+S_ROAD = 80
+
+QUANT_LAG, QUANT_CATCH_UP = 5, (4, 7)
+
+SUMS_LAG = 2
+LAGS = {"open": 2, "back": 3, "sigmoid": 4, "r_gh": 5, "sum": 6, "back_n": 7, "tanh": 8, "h_n": 9, "z_d": 9, "out": 11}
+LAGS_LAST = {"open": 1, "back": 2, "sigmoid": 3, "r_gh": 4, "back_n": 5, "sum": 6, "tanh": 7, "h_n": 8, "z_d": 7, "out": 9}
+
+ROAD_CAST, ROAD_TURN, ROAD_WEAVE = -1, 0, {GR: 2, GZ: 3}
+X_SLOT, XQUANT_SLOT = 2, 5
 
 
 def tile_grucellstack_pa_kernel(tc, x_in, h0, gh0, w_bytes, w_scale, b_ih0, out):
@@ -71,52 +64,57 @@ def tile_grucellstack_pa_kernel(tc, x_in, h0, gh0, w_bytes, w_scale, b_ih0, out)
         psum = ctx.enter_context(tc.psum_pool(name="psum", bufs=1))
         ctx.enter_context(tc.manual_schedule())
 
+        def road(J):
+            return ROAD_EARLY if J < EARLY_PAIRS else ROAD
+
+        def road_tiles(J):
+            return 2 * len(road(J))
+
+        def gate(m):
+            return ORDER[m // 3][m % 3]
+
+        def unit(J, g):
+            return 3 * J + ORDER[J].index(g)
+
+        def k_vector(J, g):
+            return K_VECTOR if g in road(J) else IN
+
         w_view = w_bytes.rearrange("(g j p) k -> p g j k", g=3, p=P)
-        wq = {}
-        wqs = {}
-
-        def srr(J):
-            return SRR_EARLY if J < J_EARLY else (1, 2)
-
-        def nq(J):
-            return 2 * len(srr(J))
-
-        for J in range(NPAIR):
-            wqs[J] = wpool.tile([P, nq(J), 512], U8, name="wqs_%d" % J)
+        w_v = {}
+        w_s = {}
+        for J in range(PAIRS):
+            w_s[J] = wpool.tile([P, road_tiles(J), K_PASS], U8, name="w_s_%d" % J)
             for g in range(3):
-                wq[(J, g)] = wpool.tile([P, 2, KV if g in srr(J) else IN], U8, name="wq_%d_%d" % (J, g))
-        sc = const.tile([P, IN], F32, name="sc")
-        s_t = const.tile([P, 4, 4], F32, name="s_t")
+                w_v[(J, g)] = wpool.tile([P, 2, k_vector(J, g)], U8, name="w_v_%d_%d" % (J, g))
+        scales_row = const.tile([P, IN], F32, name="scales_row")
+        scales_col = const.tile([P, PASSES, 4], F32, name="scales_col")
         x_sb = const.tile([P, 2, IN], BF16, name="x_sb")
         h_sb = const.tile([P, 2, L], BF16, name="h_sb")
         gh_sb = {}
-        for g in range(3):
-            gh_sb[g] = const.tile([P, 2, L], BF16, name="gh_sb_%d" % g)
+        for blk in range(3):
+            gh_sb[blk] = const.tile([P, 2, L], BF16, name="gh_sb_%d" % blk)
         b_rows = const.tile([P, P], BF16, name="b_rows")
-        warm = const.tile([P, 1], F32, name="warm")
-        warm2 = const.tile([P, 1], F32, name="warm2")
+        warm_in = const.tile([P, 1], F32, name="warm_in")
+        warm_out = const.tile([P, 1], F32, name="warm_out")
 
-        nc.vector.memset(warm[:], 0.0)
+        nc.vector.memset(warm_in[:], 0.0)
         nc.vector.memset(b_rows[:], 0.0)
-        ones = const.tile([P, 2048], BF16, name="ones", align_bytes=64)
-        fcodes = const.tile([P, 512], U32, name="fcodes", align_bytes=64)
-        fplane = const.tile([P, 512], U8, name="fplane", align_bytes=64)
-        nc.vector.memset(ones[:].bitcast(mybir.dt.int32), 1065369472)
-        nc.vector.quantize_mx(out=fcodes[:].bitcast(FP8X4), scales=fplane[:], in_=ones[:])
-        nc.scalar.activation(out=warm2[:], in_=warm[:], func=ACT.Sigmoid)
+        nc.scalar.activation(out=warm_out[:], in_=warm_in[:], func=ACT.Sigmoid)
 
-        def load_sc(c):
+        def load_scales(c):
             nc.sync.dma_start(
-                out=sc[:, c * 512:(c + 1) * 512],
+                out=scales_row[:, c * 512:(c + 1) * 512],
                 in_=w_scale[0:1, c * 512:(c + 1) * 512].rearrange("o k -> (o k)").partition_broadcast(P),
             )
 
-        def load_s(J):
-            for s in range(len(srr(J))):
-                nc.sync.dma_start(out=wqs[J][:, 2 * s:2 * s + 2, :], in_=w_view[:, GATE[srr(J)[s]], 2 * J:2 * J + 2, KV:IN])
+        def load_w_s(J):
+            for s in range(len(road(J))):
+                nc.sync.dma_start(
+                    out=w_s[J][:, 2 * s:2 * s + 2, :], in_=w_view[:, BLOCK[road(J)[s]], 2 * J:2 * J + 2, K_VECTOR:IN]
+                )
 
-        def load_v(J, g):
-            nc.sync.dma_start(out=wq[(J, g)][:], in_=w_view[:, GATE[g], 2 * J:2 * J + 2, 0:(KV if g in srr(J) else IN)])
+        def load_w_v(J, g):
+            nc.sync.dma_start(out=w_v[(J, g)][:], in_=w_view[:, BLOCK[g], 2 * J:2 * J + 2, 0:k_vector(J, g)])
 
         x_view = x_in.rearrange("(h p) k -> p h k", p=P)
         gh_view = gh0.rearrange("(h p) (g c) -> p h g c", p=P, g=3)
@@ -124,385 +122,333 @@ def tile_grucellstack_pa_kernel(tc, x_in, h0, gh0, w_bytes, w_scale, b_ih0, out)
         def load_x(h):
             nc.sync.dma_start(out=x_sb[:, h, :], in_=x_view[:, h, :])
 
-        def load_gh(g):
-            nc.sync.dma_start(out=gh_sb[g][:], in_=gh_view[:, :, g, :])
+        def load_gh(blk):
+            nc.sync.dma_start(out=gh_sb[blk][:], in_=gh_view[:, :, blk, :])
 
-        nc.sync.dma_start(out=wq[(0, 0)][:, 0, 0:512], in_=w_view[:, GATE[0], 0, 0:512])
-        load_sc(0)
-        nc.sync.dma_start(out=wq[(0, 0)][:, 0, 512:IN], in_=w_view[:, GATE[0], 0, 512:IN])
-        load_sc(1)
-        load_sc(2)
-        load_sc(3)
-        nc.sync.dma_start(out=wq[(0, 0)][:, 1, :], in_=w_view[:, GATE[0], 1, :])
-        load_s(0)
-        load_v(0, 1)
+        nc.sync.dma_start(out=w_v[(0, GN)][:, 0, 0:512], in_=w_view[:, BLOCK[GN], 0, 0:512])
+        load_scales(0)
+        nc.sync.dma_start(out=w_v[(0, GN)][:, 0, 512:IN], in_=w_view[:, BLOCK[GN], 0, 512:IN])
+        load_scales(1)
+        load_scales(2)
+        load_scales(3)
+        nc.sync.dma_start(out=w_v[(0, GN)][:, 1, :], in_=w_view[:, BLOCK[GN], 1, :])
+        load_w_s(0)
+        load_w_v(0, GR)
         load_x(0)
         load_x(1)
-        nc.sync.dma_start(out=s_t[:], in_=w_scale.rearrange("o (g p t) -> p (o g) t", p=P, t=4))
+        nc.sync.dma_start(out=scales_col[:], in_=w_scale.rearrange("o (g p t) -> p (o g) t", p=P, t=4))
         nc.sync.dma_start(out=b_rows[0:36, :], in_=b_ih0.rearrange("(c p) -> c p", p=P))
-        load_v(0, 2)
-        load_gh(0)
-        load_v(1, 0)
-        load_gh(2)
-        load_gh(1)
-        load_s(1)
-        load_v(1, 1)
+        load_w_v(0, GZ)
+        load_gh(BLOCK[GR])
+        load_w_v(1, GN)
+        load_gh(BLOCK[GN])
+        load_gh(BLOCK[GZ])
+        load_w_s(1)
+        load_w_v(1, GR)
         nc.sync.dma_start(out=h_sb[:], in_=h0.rearrange("(h p) c -> p h c", p=P))
-        load_v(1, 2)
-        for J in range(2, NPAIR):
-            load_v(J, ORDER[J][0])
-            load_s(J)
-            load_v(J, ORDER[J][1])
-            load_v(J, ORDER[J][2])
+        load_w_v(1, GZ)
+        for J in range(2, PAIRS):
+            load_w_v(J, ORDER[J][0])
+            load_w_s(J)
+            load_w_v(J, ORDER[J][1])
+            load_w_v(J, ORDER[J][2])
 
         ident_f = const.tile([P, P], F32, name="ident_f")
         make_identity(nc, ident_f[:])
         ident_b = const.tile([P, P], BF16, name="ident_b")
         make_identity(nc, ident_b[:])
-        ident_n = const.tile([P, P], F32, name="ident_n")
-        nc.scalar.mul(out=ident_n[:], in_=ident_f[:], mul=-1.0)
+        ident_neg = const.tile([P, P], F32, name="ident_neg")
+        nc.scalar.mul(out=ident_neg[:], in_=ident_f[:], mul=-1.0)
 
-        xgrp = const.tile([P, NPASS * B * 4], BF16, name="xgrp", align_bytes=64)
-        xcodes = const.tile([P, NPASS * B], U32, name="xcodes", align_bytes=64)
-        xplane = const.tile([P, NPASS * B], U8, name="xplane", align_bytes=64)
-        bias_sb = const.tile([P, 36], F32, name="bias_sb")
+        x_grouped = const.tile([P, PASSES * B * 4], BF16, name="x_grouped", align_bytes=64)
+        x_codes = const.tile([P, PASSES * B], U32, name="x_codes", align_bytes=64)
+        x_scales = const.tile([P, PASSES * B], U8, name="x_scales", align_bytes=64)
+        bias_col = const.tile([P, 36], F32, name="bias_col")
 
-        st = {}
+        live = {}
 
-        def role(m):
-            return ORDER[m // 3][m % 3]
+        def on_road(i):
+            return gate(i // 2) in road(i // 6)
 
-        def unit(J, ro):
-            return 3 * J + ORDER[J].index(ro)
+        def grouped_of(m):
+            if ("grouped", m) not in live:
+                live[("grouped", m)] = work.tile([P, 2, IN], BF16, name="grouped", bufs=5, align_bytes=64)
+            return live[("grouped", m)]
 
-        def is_sr(i):
-            return role(i // 2) in srr(i // 6)
+        def turn_bank():
+            return psum.tile([P, 512], F32, name="turn", tag="turn", bufs=TURN_BANKS)
 
-        def get_grp(m):
-            if ("grp", m) not in st:
-                st[("grp", m)] = work.tile([P, 2, IN], BF16, name="grp", bufs=GRPB, align_bytes=64)
-            return st[("grp", m)]
+        def back_bank():
+            return psum.tile([P, 512], F32, name="back", tag="back", bufs=BACK_BANKS)
 
-        def get_acc(m):
-            if ("acc", m) not in st:
-                st[("acc", m)] = psum.tile([P, 512], F32, name="acc_%d" % (m % NACC), tag="acc_%d" % (m % NACC), bufs=1)
-            return st[("acc", m)]
-
-        def ring():
-            return psum.tile([P, 512], F32, name="tp", tag="tp", bufs=TPB)
-
-        def sr_cast(J, s):
+        def road_cast(J, s):
             if s == 0:
-                st[("wc", J)] = work.tile([P, nq(J) * 512], BF16, name="wc", bufs=2)
-            wc = st[("wc", J)]
+                live[("cast", J)] = work.tile([P, road_tiles(J) * K_PASS], BF16, name="cast", bufs=2)
             nc.scalar.copy(
-                out=wc[:, s * 1024:(s + 1) * 1024],
-                in_=wqs[J][:, 2 * s:2 * s + 2, :].rearrange("p q k -> p (q k)").bitcast(FP8),
+                out=live[("cast", J)][:, s * 1024:(s + 1) * 1024],
+                in_=w_s[J][:, 2 * s:2 * s + 2, :].rearrange("p q k -> p (q k)").bitcast(FP8),
             )
 
-        def sr_turn(J):
-            wcw = st[("wc", J)][:].bitcast(F32)
+        def road_turn(J):
+            words = live[("cast", J)][:].bitcast(F32)
             for u in range(2):
-                if u == 0 or nq(J) == 4:
-                    tq = ring()
-                st[("tq", J, u)] = tq
-                for q in range(nq(J)):
-                    col = (q + (2 * u if nq(J) == 2 else 0)) * P
-                    nc.tensor.transpose(tq[:, col:col + P], wcw[:, q * 256 + u:(q + 1) * 256:2], ident_f[:])
+                if u == 0 or road_tiles(J) == 4:
+                    bank = turn_bank()
+                live[("road_bank", J, u)] = bank
+                for q in range(road_tiles(J)):
+                    col = (q + (2 * u if road_tiles(J) == 2 else 0)) * P
+                    nc.tensor.transpose(bank[:, col:col + P], words[:, q * 256 + u:(q + 1) * 256:2], ident_f[:])
 
-        def sr_scale(J, u):
+        def road_scale(J, u):
+            n_q = road_tiles(J)
             if u == 0:
-                st[("pl", J)] = work.tile([P, nq(J) * 512], BF16, name="pl", bufs=2)
-            pl = st[("pl", J)]
-            halves = st[("tq", J, u)][:].bitcast(BF16)
+                live[("planes", J)] = work.tile([P, n_q * K_PASS], BF16, name="planes", bufs=2)
+            halves = live[("road_bank", J, u)][:].bitcast(BF16)
+            first = u * 512 if n_q == 2 else 0
             for e in range(2):
                 t = 2 * u + e
-                lo = u * 512 if nq(J) == 2 else 0
                 nc.scalar.activation(
-                    out=pl[:, t * nq(J) * P:(t + 1) * nq(J) * P], in_=halves[:, lo + e:lo + nq(J) * 256:2],
-                    func=ACT.Copy, scale=s_t[:, 3, t:t + 1],
+                    out=live[("planes", J)][:, t * n_q * P:(t + 1) * n_q * P],
+                    in_=halves[:, first + e:first + n_q * 256:2],
+                    func=ACT.Copy, scale=scales_col[:, PASSES - 1, t:t + 1],
                 )
 
-        def sr_weave(J, s):
-            grp = get_grp(unit(J, srr(J)[s]))
+        def road_weave(J, s):
             nc.scalar.copy(
-                out=grp[:, :, KV:IN].rearrange("p j (c t) -> p j c t", t=4),
-                in_=st[("pl", J)][:].rearrange("p (t q c) -> p q c t", t=4, q=nq(J))[:, 2 * s:2 * s + 2, :, :],
+                out=grouped_of(unit(J, road(J)[s]))[:, :, K_VECTOR:IN].rearrange("p j (c t) -> p j c t", t=4),
+                in_=live[("planes", J)][:].rearrange("p (t q c) -> p q c t", t=4, q=road_tiles(J))[:, 2 * s:2 * s + 2, :, :],
             )
 
-        def tt(i):
-            J, g, jj = i // 6, role(i // 2), i % 2
-            wb = work.tile([P, IN], BF16, name="wb", bufs=3)
-            st[("wb", i)] = wb
-            src = wq[(J, g)][:, jj, :].bitcast(FP8)
-            width = KV if is_sr(i) else IN
-            w = 512 if i in (0, NT - 1) else width
-            for c in range(width // w):
-                nc.vector.tensor_tensor(
-                    out=wb[:, c * w:(c + 1) * w], in0=src[:, c * w:(c + 1) * w],
-                    in1=sc[:, c * w:(c + 1) * w], op=ALU.mult,
-                )
+        def product(i):
+            J, g, j = i // 6, gate(i // 2), i % 2
+            scaled = work.tile([P, IN], BF16, name="scaled", bufs=3)
+            live[("scaled", i)] = scaled
+            codes = w_v[(J, g)][:, j, :].bitcast(FP8)
+            width = k_vector(J, g)
+            piece = 512 if i == 0 else width
+            for c in range(width // piece):
+                cols = slice(c * piece, (c + 1) * piece)
+                nc.vector.tensor_tensor(out=scaled[:, cols], in0=codes[:, cols], in1=scales_row[:, cols], op=ALU.mult)
 
-        def tr(i):
-            words = st[("wb", i)][:].bitcast(F32)
-            npass = 3 if is_sr(i) else 4
-            tpa = ring()
-            tpb = ring()
-            st[("tp", i)] = (tpa, tpb)
-            for g in range(npass):
-                bank = tpa if g < 2 else tpb
+        def tile_turn(i):
+            words = live[("scaled", i)][:].bitcast(F32)
+            banks = (turn_bank(), turn_bank())
+            live[("banks", i)] = banks
+            for g in range(k_vector(i // 6, gate(i // 2)) // K_PASS):
                 for u in range(2):
                     col = ((g % 2) * 2 + u) * P
-                    nc.tensor.transpose(bank[:, col:col + P], words[:, 256 * g + u:256 * (g + 1):2], ident_f[:])
+                    nc.tensor.transpose(
+                        banks[g // 2][:, col:col + P], words[:, 256 * g + u:256 * (g + 1):2], ident_f[:]
+                    )
 
-        def te(i):
-            gw = get_grp(i // 2)[:, i % 2, :].bitcast(F32)
-            tpa, tpb = st[("tp", i)]
+        def tile_out(i):
+            dst = grouped_of(i // 2)[:, i % 2, :].bitcast(F32)
+            banks = live[("banks", i)]
             nc.scalar.copy(
-                out=gw[:, 0:512].rearrange("p (g c u) -> p g c u", g=2, u=2),
-                in_=tpa[:].rearrange("p (g u c) -> p g c u", g=2, u=2),
+                out=dst[:, 0:512].rearrange("p (g c u) -> p g c u", g=2, u=2),
+                in_=banks[0][:].rearrange("p (g u c) -> p g c u", g=2, u=2),
             )
-            if is_sr(i):
+            if on_road(i):
                 nc.scalar.copy(
-                    out=gw[:, 512:768].rearrange("p (c u) -> p c u", u=2),
-                    in_=tpb[:, 0:256].rearrange("p (u c) -> p c u", u=2),
+                    out=dst[:, 512:768].rearrange("p (c u) -> p c u", u=2),
+                    in_=banks[1][:, 0:256].rearrange("p (u c) -> p c u", u=2),
                 )
             else:
                 nc.scalar.copy(
-                    out=gw[:, 512:1024].rearrange("p (g c u) -> p g c u", g=2, u=2),
-                    in_=tpb[:].rearrange("p (g u c) -> p g c u", g=2, u=2),
+                    out=dst[:, 512:1024].rearrange("p (g c u) -> p g c u", g=2, u=2),
+                    in_=banks[1][:].rearrange("p (g u c) -> p g c u", g=2, u=2),
                 )
 
-        def qz(m):
-            codes = work.tile([P, 1024], U32, name="codes", bufs=2, align_bytes=64)
-            plane = work.tile([P, 1024], U8, name="plane", bufs=2, align_bytes=64)
-            st[("codes", m)] = codes
-            st[("plane", m)] = plane
+        def quantise(m):
+            live[("codes", m)] = work.tile([P, 1024], U32, name="codes", bufs=2, align_bytes=64)
+            live[("scales", m)] = work.tile([P, 1024], U8, name="scales", bufs=2, align_bytes=64)
             nc.vector.quantize_mx(
-                out=codes[:].bitcast(FP8X4), scales=plane[:], in_=st[("grp", m)][:].rearrange("p j k -> p (j k)"),
+                out=live[("codes", m)][:].bitcast(FP8X4), scales=live[("scales", m)][:],
+                in_=live[("grouped", m)][:].rearrange("p j k -> p (j k)"),
             )
 
-        def mm(m, jj):
-            acc = get_acc(m)
-            codes = st[("codes", m)]
-            plane = st[("plane", m)]
-            for k in range(NPASS):
-                col = jj * 512 + k * P
+        def passes(m, j):
+            if j == 0:
+                bank = "sums_%d" % (m % SUM_BANKS)
+                live[("sums", m)] = psum.tile([P, 512], F32, name=bank, tag=bank, bufs=1)
+            for g in range(PASSES):
+                col = j * 512 + g * P
                 nc.tensor.matmul_mx(
-                    out=acc[:, jj * B:(jj + 1) * B],
-                    lhsT=codes[:, col:col + P].bitcast(FP8X4),
-                    lhsT_scale=plane[:, col:col + P],
-                    rhs=xcodes[:, k * B:(k + 1) * B].bitcast(FP8X4),
-                    rhs_scale=xplane[:, k * B:(k + 1) * B],
-                    start=(k == 0), stop=(k == NPASS - 1),
-                )
-
-        def dummies(m, n, lo):
-            acc = get_acc(m)
-            for k in range(n * 512 // (512 - lo)):
-                nc.tensor.matmul_mx(
-                    out=acc[:, lo:512],
-                    lhsT=fcodes[:, 0:P].bitcast(FP8X4), lhsT_scale=fplane[:, 0:P],
-                    rhs=fcodes[:, lo:512].bitcast(FP8X4), rhs_scale=fplane[:, lo:512],
-                    start=True, stop=True,
+                    out=live[("sums", m)][:, j * B:(j + 1) * B],
+                    lhsT=live[("codes", m)][:, col:col + P].bitcast(FP8X4),
+                    lhsT_scale=live[("scales", m)][:, col:col + P],
+                    rhs=x_codes[:, g * B:(g + 1) * B].bitcast(FP8X4),
+                    rhs_scale=x_scales[:, g * B:(g + 1) * B],
+                    start=(g == 0), stop=(g == PASSES - 1),
                 )
 
         def x_turn(g):
-            tpx = ring()
-            st[("tpx", g)] = tpx
+            bank = turn_bank()
+            live[("x_bank", g)] = bank
             for u in range(2):
                 for h in range(2):
                     col = (u * 2 + h) * P
                     nc.tensor.transpose(
-                        tpx[:, col:col + P],
-                        x_sb[:, h, :].bitcast(F32)[:, 256 * g + u:256 * (g + 1):2], ident_f[:],
+                        bank[:, col:col + P], x_sb[:, h, :].bitcast(F32)[:, 256 * g + u:256 * (g + 1):2], ident_f[:]
                     )
 
-        def x_exit(g):
+        def x_out(g):
             nc.scalar.copy(
-                out=xgrp[:].bitcast(F32)[:, g * 512:(g + 1) * 512].rearrange("p (r u) -> p r u", u=2),
-                in_=st[("tpx", g)][:].rearrange("p (u r) -> p r u", u=2),
+                out=x_grouped[:].bitcast(F32)[:, g * 512:(g + 1) * 512].rearrange("p (r u) -> p r u", u=2),
+                in_=live[("x_bank", g)][:].rearrange("p (u r) -> p r u", u=2),
             )
 
-        def x_quant():
-            nc.vector.quantize_mx(out=xcodes[:].bitcast(FP8X4), scales=xplane[:], in_=xgrp[:])
+        def x_quantise():
+            nc.vector.quantize_mx(out=x_codes[:].bitcast(FP8X4), scales=x_scales[:], in_=x_grouped[:])
 
         def bias_turn():
-            tpv = psum.tile([P, 1024], BF16, name="tpv", tag="tp", bufs=TPB)
-            st["tpv"] = tpv
-            nc.tensor.transpose(tpv[:, 0:P], b_rows[:], ident_b[:])
+            live["bias_bank"] = psum.tile([P, 1024], BF16, name="bias_bank", tag="turn", bufs=TURN_BANKS)
+            nc.tensor.transpose(live["bias_bank"][:, 0:P], b_rows[:], ident_b[:])
 
-        def bias_exit():
-            nc.scalar.copy(out=bias_sb[:], in_=st["tpv"][:, 0:36])
+        def bias_out():
+            nc.scalar.copy(out=bias_col[:], in_=live["bias_bank"][:, 0:36])
 
-        def ex(m):
-            J, g = m // 3, role(m)
-            eb = ep.tile([P, 512], F32, name="en" if g == 0 else "eb", bufs=2)
-            st[("eb", m)] = eb
-            for jj in range(2):
-                c = GATE[g] * 12 + 2 * J + jj
-                nc.scalar.activation(
-                    out=eb[:, jj * B:(jj + 1) * B], in_=st[("acc", m)][:, jj * B:(jj + 1) * B],
-                    func=ACT.Identity, bias=bias_sb[:, c:c + 1], scale=1.0,
-                )
+        def sum_on_tensor(J):
+            return J < PAIRS - PAIRS_SUM_ON_VECTOR
 
-        def tbank(m):
-            if TBB:
-                return psum.tile([P, 512], F32, name="tb", tag="tb", bufs=TBB)
-            return ring()
+        def diff_on_tensor(J):
+            return J < PAIRS - PAIRS_DIFF_ON_VECTOR
 
-        def gh_open(m):
-            J, g = m // 3, role(m)
-            tb = tbank(m)
-            st[("tb", m)] = tb
-            nc.tensor.matmul(
-                out=tb[:].rearrange("p (h c) -> p h c", h=2), lhsT=ident_b[:],
-                rhs=gh_sb[GATE[g]][:, :, J * 256:(J + 1) * 256], start=True, stop=False,
-            )
-
-        def t_open(J):
-            tb = tbank(J)
-            st[("tb", unit(J, 0))] = tb
-            nc.tensor.matmul(out=tb[:], lhsT=ident_f[:], rhs=st[("r", J)][:], start=True, stop=False)
-
-        def on_pe(J):
-            return J < NPAIR - N_V4
-
-        def back(m):
-            lone = role(m) == 0 and not on_pe(m // 3)
-            if lone:
-                st[("tb", m)] = tbank(m)
-            tb = st[("tb", m)]
-            eb = st[("eb", m)]
-            for h in range(2):
-                for jj in range(2):
-                    nc.tensor.matmul(
-                        out=tb[:, h * 256 + jj * P:h * 256 + (jj + 1) * P],
-                        lhsT=eb[:, jj * 256 + h * P:jj * 256 + (h + 1) * P], rhs=ident_f[:], is_transpose=True,
-                        start=lone, stop=(lone or (h == 1 and jj == 1)),
-                    )
-
-        def cols(t, J):
-            return t[:, :, J * 256:(J + 1) * 256]
-
-        def v3d(t):
+        def by_half(t):
             return t[:].rearrange("p (h c) -> p h c", h=2)
 
-        def sig(m):
-            J, g = m // 3, role(m)
-            nm = "r" if g == 1 else "z"
-            o = ep.tile([P, 512], F32, name=nm, bufs=3)
-            st[(nm, J)] = o
-            nc.scalar.activation(out=o[:], in_=st[("tb", m)][:], func=ACT.Sigmoid)
+        def of_pair(t, J):
+            return t[:, :, J * 256:(J + 1) * 256]
 
-        def v3(J):
-            r = st[("r", J)]
-            nc.vector.tensor_tensor(out=v3d(r), in0=v3d(r), in1=cols(gh_sb[2], J), op=ALU.mult)
+        def sums_out(m):
+            J, g = m // 3, gate(m)
+            biased = ep.tile([P, 512], F32, name="biased_n" if g == GN else "biased", bufs=2)
+            live[("biased", m)] = biased
+            for j in range(2):
+                c = BLOCK[g] * 12 + 2 * J + j
+                nc.scalar.activation(
+                    out=biased[:, j * B:(j + 1) * B], in_=live[("sums", m)][:, j * B:(j + 1) * B],
+                    func=ACT.Identity, bias=bias_col[:, c:c + 1], scale=1.0,
+                )
 
-        def v4(J):
-            r = st[("r", J)]
-            nc.vector.tensor_tensor(out=r[:], in0=st[("tb", unit(J, 0))][:], in1=r[:], op=ALU.add)
+        def open_with_gh(m):
+            live[("back", m)] = back_bank()
+            nc.tensor.matmul(
+                out=by_half(live[("back", m)]), lhsT=ident_b[:], rhs=of_pair(gh_sb[BLOCK[gate(m)]], m // 3),
+                start=True, stop=False,
+            )
 
-        def th(J):
-            r = st[("r", J)]
-            nc.scalar.activation(out=r[:], in_=(st[("tb", unit(J, 0))] if on_pe(J) else r)[:], func=ACT.Tanh)
+        def open_with_r_gh(J):
+            live[("back", unit(J, GN))] = back_bank()
+            nc.tensor.matmul(
+                out=live[("back", unit(J, GN))][:], lhsT=ident_f[:], rhs=live[("r", J)][:], start=True, stop=False
+            )
 
-        def vd(J):
-            d = ep.tile([P, 512], F32, name="d")
-            st[("d", J)] = d
-            nc.vector.tensor_tensor(out=v3d(d), in0=cols(h_sb, J), in1=v3d(st[("r", J)]), op=ALU.subtract)
+        def turn_back(m):
+            alone = gate(m) == GN and not sum_on_tensor(m // 3)
+            if alone:
+                live[("back", m)] = back_bank()
+            for h in range(2):
+                for j in range(2):
+                    nc.tensor.matmul(
+                        out=live[("back", m)][:, h * 256 + j * P:h * 256 + (j + 1) * P],
+                        lhsT=live[("biased", m)][:, j * 256 + h * P:j * 256 + (h + 1) * P], rhs=ident_f[:],
+                        is_transpose=True, start=alone, stop=(alone or (h == 1 and j == 1)),
+                    )
 
-        def pd(J):
-            tb = tbank(3 * J)
-            st[("pd", J)] = tb
-            nc.tensor.matmul(out=tb[:], lhsT=ident_n[:], rhs=st[("r", J)][:], start=True, stop=False)
-            nc.tensor.matmul(out=v3d(tb), lhsT=ident_b[:], rhs=cols(h_sb, J), start=False, stop=True)
+        def sigmoid(m):
+            name = "r" if gate(m) == GR else "z"
+            live[(name, m // 3)] = ep.tile([P, 512], F32, name=name, bufs=3)
+            nc.scalar.activation(out=live[(name, m // 3)][:], in_=live[("back", m)][:], func=ACT.Sigmoid)
 
-        def d_on_pe(J):
-            return J < NPAIR - N_VD
+        def r_gh(J):
+            r = live[("r", J)]
+            nc.vector.tensor_tensor(out=by_half(r), in0=by_half(r), in1=of_pair(gh_sb[BLOCK[GN]], J), op=ALU.mult)
 
-        def ve(J):
-            if d_on_pe(J):
-                d = ep.tile([P, 512], F32, name="d")
-                st[("d", J)] = d
-                nc.vector.tensor_tensor(out=d[:], in0=st[("pd", J)][:], in1=st[("z", J)][:], op=ALU.mult)
+        def n_sum(J):
+            r = live[("r", J)]
+            nc.vector.tensor_tensor(out=r[:], in0=live[("back", unit(J, GN))][:], in1=r[:], op=ALU.add)
+
+        def tanh(J):
+            r = live[("r", J)]
+            src = live[("back", unit(J, GN))] if sum_on_tensor(J) else r
+            nc.scalar.activation(out=r[:], in_=src[:], func=ACT.Tanh)
+
+        def h_minus_n(J):
+            if diff_on_tensor(J):
+                bank = back_bank()
+                live[("diff", J)] = bank
+                nc.tensor.matmul(out=bank[:], lhsT=ident_neg[:], rhs=live[("r", J)][:], start=True, stop=False)
+                nc.tensor.matmul(out=by_half(bank), lhsT=ident_b[:], rhs=of_pair(h_sb, J), start=False, stop=True)
             else:
-                d = st[("d", J)]
-                nc.vector.tensor_tensor(out=d[:], in0=d[:], in1=st[("z", J)][:], op=ALU.mult)
+                live[("d", J)] = ep.tile([P, 512], F32, name="d")
+                nc.vector.tensor_tensor(
+                    out=by_half(live[("d", J)]), in0=of_pair(h_sb, J), in1=by_half(live[("r", J)]), op=ALU.subtract
+                )
+
+        def z_times_diff(J):
+            if diff_on_tensor(J):
+                live[("d", J)] = ep.tile([P, 512], F32, name="d")
+                diff = live[("diff", J)]
+            else:
+                diff = live[("d", J)]
+            nc.vector.tensor_tensor(out=live[("d", J)][:], in0=diff[:], in1=live[("z", J)][:], op=ALU.mult)
 
         out_view = out.rearrange("(h p) c -> p h c", p=P)
 
-        def vo(J):
-            d = st[("d", J)]
-            nc.vector.tensor_tensor(out=d[:], in0=d[:], in1=st[("r", J)][:], op=ALU.add)
-            nc.sync.dma_start(out=out_view[:, :, J * 256:(J + 1) * 256], in_=v3d(d))
+        def result(J):
+            d = live[("d", J)]
+            nc.vector.tensor_tensor(out=d[:], in0=d[:], in1=live[("r", J)][:], op=ALU.add)
+            nc.sync.dma_start(out=of_pair(out_view, J), in_=by_half(d))
 
         steps = []
 
         def at(slot, place, fn, *args):
             steps.append((slot, place, len(steps), fn, args))
 
-        def qs(m):
-            return 2 * m + QL - sum([1 for c in QCUT if m >= c])
+        def quant_slot(m):
+            return 2 * m + QUANT_LAG - sum([1 for c in QUANT_CATCH_UP if m >= c])
 
-        def late(slot):
-            return slot + K_LATE if slot >= NT - K_LATE else slot
-
-        at(-1, 0, dummies, 0, D_HEAD, 0)
-        plain = {}
-        for J in range(NPAIR):
-            dl = DL_LAST if J == NPAIR - 1 else DL
-            if J < NPAIR - N_V4:
-                plain[late(qs(unit(J, 1)) + dl[5])] = F_TOPEN
-            for ro in (1, 2):
-                plain[qs(unit(J, ro)) + dl[0]] = F_OPEN
-        for i in range(NT):
-            at(i, 10, tt, i)
-            at(i, 31, tr, i)
-            at(i, 40, te, i)
-            now = [m for m in range(NU) if qs(m) == i]
-            if now:
-                at(i, 64, dummies, now[0], D_SLOT - plain.get(i, 0), B)
+        for i in range(TILES):
+            at(i, V_PRODUCT, product, i)
+            at(i, T_TILE, tile_turn, i)
+            at(i, S_TILE, tile_out, i)
+        for g in range(PASSES):
+            at(X_SLOT, X_FIRST + 2 * g, x_turn, g)
+            at(X_SLOT, X_FIRST + 2 * g + 1, x_out, g)
+        at(XQUANT_SLOT, V_XQUANT, x_quantise)
+        at(X_SLOT + 1, X_FIRST, bias_turn)
+        at(X_SLOT + 1, X_FIRST + 1, bias_out)
+        for m in range(UNITS):
+            at(quant_slot(m), V_QUANT, quantise, m)
+            at(quant_slot(m), T_PASSES, passes, m, 0)
+            at(quant_slot(m) + 1, T_PASSES, passes, m, 1)
+            at(quant_slot(m) + SUMS_LAG, S_SUMS + m % 3, sums_out, m)
+        for J in range(PAIRS):
+            last = J == PAIRS - 1
+            first_slot = 6 * J + (1 if J == 0 else (-1 if ORDER[J][0] == GR else 0))
+            for s in range(len(road(J))):
+                at(first_slot + ROAD_CAST, S_ROAD + s, road_cast, J, s)
+                at(first_slot + ROAD_WEAVE[road(J)[s]], S_ROAD + 4 + s, road_weave, J, s)
+            at(first_slot + ROAD_TURN, T_ROAD, road_turn, J)
+            at(first_slot + ROAD_TURN, S_ROAD + 2, road_scale, J, 0)
+            at(first_slot + ROAD_TURN, S_ROAD + 3, road_scale, J, 1)
+            lags = LAGS_LAST if last else LAGS
+            from_r = quant_slot(unit(J, GR))
+            from_z = quant_slot(unit(J, GZ))
+            for m in (unit(J, GR), unit(J, GZ)):
+                at(quant_slot(m) + lags["open"], T_PLAIN, open_with_gh, m)
+                at(quant_slot(m) + lags["back"], T_BACK_LATE if last else T_BACK, turn_back, m)
+                at(quant_slot(m) + lags["sigmoid"], S_SIGMOID + m % 3, sigmoid, m)
+            at(from_r + lags["back_n"], T_BACK, turn_back, unit(J, GN))
+            at(from_r + lags["r_gh"], V_R_GH, r_gh, J)
+            if sum_on_tensor(J):
+                at(from_r + lags["sum"], T_PLAIN, open_with_r_gh, J)
             else:
-                at(i, 64, dummies, min([m for m in range(NU) if qs(m) > i] + [NU - 1]), D_SLOT - plain.get(i, 0), 0)
-        for g in range(NPASS):
-            at(S_X, 41 + 2 * g, x_turn, g)
-            at(S_X, 42 + 2 * g, x_exit, g)
-        at(S_XQ, 49, x_quant)
-        at(S_X + 1, 41, bias_turn)
-        at(S_X + 1, 42, bias_exit)
-        for m in range(NU):
-            at(qs(m), 50, qz, m)
-            at(qs(m), 60, mm, m, 0)
-            at(qs(m) + 1, 60, mm, m, 1)
-            at(qs(m) + D_EX, 26 + m % 3, ex, m)
-        for J in range(NPAIR):
-            q = 6 * J + (S_HEAD if J == 0 else (S_RFIRST if ORDER[J][0] == 1 else 0))
-            for s in range(len(srr(J))):
-                at(q + S_CAST[s], 80 + s, sr_cast, J, s)
-                at(q + S_WEAVE[srr(J)[s] - 1], 84 + s, sr_weave, J, s)
-            at(q + S_TURN, 63, sr_turn, J)
-            at(q + S_SCALE[0], 82, sr_scale, J, 0)
-            at(q + S_SCALE[1], 83, sr_scale, J, 1)
-            qr = qs(unit(J, 1))
-            qzz = qs(unit(J, 2))
-            dl = DL_LAST if J == NPAIR - 1 else DL
-            for m in (unit(J, 1), unit(J, 2)):
-                at(qs(m) + dl[0], 62, gh_open, m)
-                at(qs(m) + dl[1], dl[2], back, m)
-                at(qs(m) + dl[3], 21 + m % 3, sig, m)
-            at(late(qr + dl[6]), 30, back, unit(J, 0))
-            at(late(qr + dl[4]), 70, v3, J)
-            if on_pe(J):
-                at(late(qr + dl[5]), 62, t_open, J)
-            else:
-                at(late(qr + dl[11]), 73, v4, J)
-            at(late(qr + dl[7]), 20, th, J)
-            if d_on_pe(J):
-                at(late(qr + dl[8]), 62, pd, J)
-            else:
-                at(late(qr + dl[8]), 71, vd, J)
-            at(late(qzz + dl[9]), 74, ve, J)
-            at(late(qzz + dl[10]), 72, vo, J)
+                at(from_r + lags["sum"], V_SUM, n_sum, J)
+            at(from_r + lags["tanh"], S_TANH, tanh, J)
+            at(from_r + lags["h_n"], T_PLAIN if diff_on_tensor(J) else V_H_N, h_minus_n, J)
+            at(from_z + lags["z_d"], V_Z_D, z_times_diff, J)
+            at(from_z + lags["out"], V_OUT, result, J)
         for step in sorted(steps, key=lambda e: e[0:3]):
             step[3](*step[4])

@@ -28,7 +28,7 @@ BLOCK = (2, 0, 1)
 
 ORDER = ((GN, GR, GZ),) * (PAIRS - 1) + ((GR, GN, GZ),)
 
-ROAD_EARLY, EARLY_PAIRS, ROAD = (GZ,), 2, (GR, GZ)
+ROAD_EARLY, EARLY_PAIRS, ROAD = (GZ,), 1, (GR, GZ)
 
 PAIRS_SUM_ON_VECTOR, PAIRS_DIFF_ON_VECTOR = 1, 2
 

@@ -30,7 +30,7 @@ ORDER = ((GN, GR, GZ),) * (PAIRS - 1) + ((GR, GN, GZ),)
 
 ROAD_EARLY, EARLY_PAIRS, ROAD = (GZ,), 1, (GR, GZ)
 
-PAIRS_SUM_ON_VECTOR, PAIRS_DIFF_ON_VECTOR = 1, 2
+PAIRS_SUM_ON_VECTOR, PAIRS_DIFF_ON_VECTOR = 2, 2
 
 SUM_BANKS, TURN_BANKS, BACK_BANKS = 2, 3, 3
 
@@ -48,6 +48,7 @@ QUANT_LAG, QUANT_CATCH_UP = 5, (4, 7)
 
 SUMS_LAG = 2
 LAGS = {"open": 2, "back": 3, "sigmoid": 4, "r_gh": 5, "sum": 6, "back_n": 7, "tanh": 8, "h_n": 9, "z_d": 9, "out": 11}
+LAGS_SUM_ON_VECTOR = dict(LAGS, back_n=6, sum=7)
 LAGS_LAST = {"open": 1, "back": 2, "sigmoid": 3, "r_gh": 4, "back_n": 5, "sum": 6, "tanh": 7, "h_n": 8, "z_d": 7, "out": 9}
 
 ROAD_CAST, ROAD_TURN, ROAD_WEAVE = -1, 0, {GR: 2, GZ: 3}
@@ -433,7 +434,7 @@ def tile_grucellstack_pa_kernel(tc, x_in, h0, gh0, w_bytes, w_scale, b_ih0, out)
             at(first_slot + ROAD_TURN, T_ROAD, road_turn, J)
             at(first_slot + ROAD_TURN, S_ROAD + 2, road_scale, J, 0)
             at(first_slot + ROAD_TURN, S_ROAD + 3, road_scale, J, 1)
-            lags = LAGS_LAST if last else LAGS
+            lags = LAGS_LAST if last else (LAGS if sum_on_tensor(J) else LAGS_SUM_ON_VECTOR)
             from_r = quant_slot(unit(J, GR))
             from_z = quant_slot(unit(J, GZ))
             for m in (unit(J, GR), unit(J, GZ)):

@@ -28,7 +28,7 @@ BLOCK = (2, 0, 1)
 
 ORDER = ((GN, GR, GZ),) * (PAIRS - 1) + ((GR, GN, GZ),)
 
-ROAD_EARLY, EARLY_PAIRS, ROAD = (GZ,), 1, (GR, GZ)
+ROAD_EARLY, EARLY_PAIRS, ROAD = (GZ,), 0, (GR, GZ)
 
 PAIRS_SUM_ON_VECTOR, PAIRS_DIFF_ON_VECTOR = 2, 2
 
@@ -86,7 +86,10 @@ def tile_grucellstack_pa_kernel(tc, x_in, h0, gh0, w_bytes, w_scale, b_ih0, out)
         for J in range(PAIRS):
             w_s[J] = wpool.tile([P, road_tiles(J), K_PASS], U8, name="w_s_%d" % J)
             for g in range(3):
-                w_v[(J, g)] = wpool.tile([P, 2, k_vector(J, g)], U8, name="w_v_%d_%d" % (J, g))
+                if (J, g) == (0, GN):
+                    w_v[(J, g)] = wpool.tile([P, PASSES, 2, K_PASS], U8, name="w_v_%d_%d" % (J, g))
+                else:
+                    w_v[(J, g)] = wpool.tile([P, 2, k_vector(J, g)], U8, name="w_v_%d_%d" % (J, g))
         scales_row = const.tile([P, IN], F32, name="scales_row")
         scales_col = const.tile([P, PASSES, 4], F32, name="scales_col")
         x_sb = const.tile([P, 2, IN], BF16, name="x_sb")
@@ -126,18 +129,14 @@ def tile_grucellstack_pa_kernel(tc, x_in, h0, gh0, w_bytes, w_scale, b_ih0, out)
         def load_gh(blk):
             nc.sync.dma_start(out=gh_sb[blk][:], in_=gh_view[:, :, blk, :])
 
-        nc.sync.dma_start(out=w_v[(0, GN)][:, 0, 0:512], in_=w_view[:, BLOCK[GN], 0, 0:512])
-        load_scales(0)
-        nc.sync.dma_start(out=w_v[(0, GN)][:, 0, 512:IN], in_=w_view[:, BLOCK[GN], 0, 512:IN])
-        load_scales(1)
-        load_scales(2)
-        load_scales(3)
-        nc.sync.dma_start(out=w_v[(0, GN)][:, 1, :], in_=w_view[:, BLOCK[GN], 1, :])
         load_w_s(0)
+        nc.sync.dma_start(out=scales_col[:], in_=w_scale.rearrange("o (g p t) -> p (o g) t", p=P, t=4))
+        for c in range(PASSES):
+            load_scales(c)
+            nc.sync.dma_start(out=w_v[(0, GN)][:, c, :, :], in_=w_view[:, BLOCK[GN], 0:2, c * 512:(c + 1) * 512])
         load_w_v(0, GR)
         load_x(0)
         load_x(1)
-        nc.sync.dma_start(out=scales_col[:], in_=w_scale.rearrange("o (g p t) -> p (o g) t", p=P, t=4))
         nc.sync.dma_start(out=b_rows[0:36, :], in_=b_ih0.rearrange("(c p) -> c p", p=P))
         load_w_v(0, GZ)
         load_gh(BLOCK[GR])
@@ -224,12 +223,21 @@ def tile_grucellstack_pa_kernel(tc, x_in, h0, gh0, w_bytes, w_scale, b_ih0, out)
             J, g, j = i // 6, gate(i // 2), i % 2
             scaled = work.tile([P, IN], BF16, name="scaled", bufs=3)
             live[("scaled", i)] = scaled
-            codes = w_v[(J, g)][:, j, :].bitcast(FP8)
             width = k_vector(J, g)
-            piece = 512 if i == 0 else width
-            for c in range(width // piece):
-                cols = slice(c * piece, (c + 1) * piece)
-                nc.vector.tensor_tensor(out=scaled[:, cols], in0=codes[:, cols], in1=scales_row[:, cols], op=ALU.mult)
+            nc.vector.tensor_tensor(
+                out=scaled[:, 0:width], in0=w_v[(J, g)][:, j, :].bitcast(FP8), in1=scales_row[:, 0:width], op=ALU.mult
+            )
+
+        def first_products():
+            for j in range(2):
+                live[("scaled", j)] = work.tile([P, IN], BF16, name="scaled", bufs=3)
+            for c in range(PASSES):
+                cols = slice(c * 512, (c + 1) * 512)
+                for j in range(2):
+                    nc.vector.tensor_tensor(
+                        out=live[("scaled", j)][:, cols], in0=w_v[(0, GN)][:, c, j, :].bitcast(FP8),
+                        in1=scales_row[:, cols], op=ALU.mult,
+                    )
 
         def tile_turn(i):
             words = live[("scaled", i)][:].bitcast(F32)
@@ -410,8 +418,10 @@ def tile_grucellstack_pa_kernel(tc, x_in, h0, gh0, w_bytes, w_scale, b_ih0, out)
         def quant_slot(m):
             return 2 * m + QUANT_LAG - sum([1 for c in QUANT_CATCH_UP if m >= c])
 
+        at(0, V_PRODUCT, first_products)
         for i in range(TILES):
-            at(i, V_PRODUCT, product, i)
+            if i >= 2:
+                at(i, V_PRODUCT, product, i)
             at(i, T_TILE, tile_turn, i)
             at(i, S_TILE, tile_out, i)
         for g in range(PASSES):
@@ -427,7 +437,7 @@ def tile_grucellstack_pa_kernel(tc, x_in, h0, gh0, w_bytes, w_scale, b_ih0, out)
             at(quant_slot(m) + SUMS_LAG, S_SUMS + m % 3, sums_out, m)
         for J in range(PAIRS):
             last = J == PAIRS - 1
-            first_slot = 6 * J + (1 if J == 0 else (-1 if ORDER[J][0] == GR else 0))
+            first_slot = 6 * J + (-1 if J == 0 or ORDER[J][0] == GR else 0)
             for s in range(len(road(J))):
                 at(first_slot + ROAD_CAST, S_ROAD + s, road_cast, J, s)
                 at(first_slot + ROAD_WEAVE[road(J)[s]], S_ROAD + 4 + s, road_weave, J, s)

@@ -32,11 +32,11 @@ ROAD_EARLY, EARLY_PAIRS, ROAD = (GZ,), 0, (GR, GZ)
 
 PAIRS_SUM_ON_VECTOR, PAIRS_DIFF_ON_VECTOR = 2, 2
 
-SUM_BANKS, TURN_BANKS, BACK_BANKS = 2, 3, 3
+SUM_BANKS, TURN_BANKS, BACK_BANKS = 2, 4, 2
 
 V_PRODUCT = 10
 S_TANH, S_SIGMOID, S_SUMS = 20, 21, 26
-T_BACK, T_TILE, T_BACK_LATE = 30, 31, 32
+T_OPEN, T_BACK, T_TILE, T_BACK_LATE = 29, 30, 31, 32
 S_TILE = 40
 X_FIRST = 41
 V_XQUANT, V_QUANT = 49, 50
@@ -47,7 +47,7 @@ S_ROAD = 80
 QUANT_LAG, QUANT_CATCH_UP = 5, (4, 7)
 
 SUMS_LAG = 2
-LAGS = {"open": 2, "back": 3, "sigmoid": 4, "r_gh": 5, "sum": 6, "back_n": 7, "tanh": 8, "h_n": 9, "z_d": 9, "out": 11}
+LAGS = {"open": 3, "back": 3, "sigmoid": 4, "r_gh": 5, "sum": 7, "back_n": 7, "tanh": 8, "h_n": 9, "z_d": 8, "out": 10}
 LAGS_SUM_ON_VECTOR = dict(LAGS, back_n=6, sum=7)
 LAGS_LAST = {"open": 1, "back": 2, "sigmoid": 3, "r_gh": 4, "back_n": 5, "sum": 6, "tanh": 7, "h_n": 8, "z_d": 7, "out": 9}
 
@@ -448,17 +448,17 @@ def tile_grucellstack_pa_kernel(tc, x_in, h0, gh0, w_bytes, w_scale, b_ih0, out)
             from_r = quant_slot(unit(J, GR))
             from_z = quant_slot(unit(J, GZ))
             for m in (unit(J, GR), unit(J, GZ)):
-                at(quant_slot(m) + lags["open"], T_PLAIN, open_with_gh, m)
+                at(quant_slot(m) + lags["open"], T_PLAIN if last else T_OPEN, open_with_gh, m)
                 at(quant_slot(m) + lags["back"], T_BACK_LATE if last else T_BACK, turn_back, m)
                 at(quant_slot(m) + lags["sigmoid"], S_SIGMOID + m % 3, sigmoid, m)
             at(from_r + lags["back_n"], T_BACK, turn_back, unit(J, GN))
             at(from_r + lags["r_gh"], V_R_GH, r_gh, J)
             if sum_on_tensor(J):
-                at(from_r + lags["sum"], T_PLAIN, open_with_r_gh, J)
+                at(from_r + lags["sum"], T_OPEN, open_with_r_gh, J)
             else:
                 at(from_r + lags["sum"], V_SUM, n_sum, J)
             at(from_r + lags["tanh"], S_TANH, tanh, J)
-            at(from_r + lags["h_n"], T_PLAIN if diff_on_tensor(J) else V_H_N, h_minus_n, J)
+            at(from_r + lags["h_n"], T_BACK_LATE if diff_on_tensor(J) else V_H_N, h_minus_n, J)
             at(from_z + lags["z_d"], V_Z_D, z_times_diff, J)
             at(from_z + lags["out"], V_OUT, result, J)
         for step in sorted(steps, key=lambda e: e[0:3]):

@@ -44,11 +44,11 @@ T_PASSES, T_PLAIN, T_ROAD = 60, 62, 63
 V_R_GH, V_H_N, V_OUT, V_SUM, V_Z_D = 70, 71, 72, 73, 74
 S_ROAD = 80
 
-QUANT_LAG, QUANT_CATCH_UP = 5, (4, 7)
+QUANT_LAG, QUANT_CATCH_UP = 5, (7, 10)
 
 SUMS_LAG = 2
-LAGS = {"open": 3, "back": 3, "sigmoid": 4, "r_gh": 5, "sum": 7, "back_n": 7, "tanh": 8, "h_n": 9, "z_d": 8, "out": 10}
-LAGS_SUM_ON_VECTOR = dict(LAGS, back_n=6, sum=7)
+LAGS = {"open": 4, "back": 4, "sigmoid": 5, "r_gh": 6, "sum": 8, "back_n": 8, "tanh": 9, "h_n": 10, "z_d": 9, "out": 11}
+LAGS_SUM_ON_VECTOR = dict(LAGS, back_n=7, sum=8)
 LAGS_LAST = {"open": 1, "back": 2, "sigmoid": 3, "r_gh": 4, "back_n": 5, "sum": 6, "tanh": 7, "h_n": 8, "z_d": 7, "out": 9}
 
 ROAD_CAST, ROAD_TURN, ROAD_WEAVE = -1, 0, {GR: 2, GZ: 3}
@@ -331,7 +331,7 @@ def tile_grucellstack_pa_kernel(tc, x_in, h0, gh0, w_bytes, w_scale, b_ih0, out)
 
         def sums_out(m):
             J, g = m // 3, gate(m)
-            biased = ep.tile([P, 512], F32, name="biased_n" if g == GN else "biased", bufs=2)
+            biased = ep.tile([P, 512], F32, name="biased_n" if g == GN else "biased", bufs=3)
             live[("biased", m)] = biased
             for j in range(2):
                 c = BLOCK[g] * 12 + 2 * J + j

@@ -39,7 +39,7 @@ S_TANH, S_SIGMOID, S_SUMS = 20, 21, 26
 T_OPEN, T_BACK, T_TILE, T_BACK_LATE = 29, 30, 31, 32
 S_TILE = 40
 X_FIRST = 41
-V_XQUANT, V_QUANT = 49, 50
+V_QUANT, V_XQUANT = 50, 51
 T_PASSES, T_PLAIN, T_ROAD = 60, 62, 63
 V_R_GH, V_H_N, V_OUT, V_SUM, V_Z_D = 70, 71, 72, 73, 74
 S_ROAD = 80
@@ -49,7 +49,7 @@ QUANT_LAG, QUANT_CATCH_UP = 5, (7, 10)
 SUMS_LAG = 2
 LAGS = {"open": 4, "back": 4, "sigmoid": 5, "r_gh": 6, "sum": 8, "back_n": 8, "tanh": 9, "h_n": 10, "z_d": 9, "out": 11}
 LAGS_SUM_ON_VECTOR = dict(LAGS, back_n=7, sum=8)
-LAGS_LAST = {"open": 1, "back": 2, "sigmoid": 3, "r_gh": 4, "back_n": 5, "sum": 6, "tanh": 7, "h_n": 8, "z_d": 7, "out": 9}
+LAGS_LAST = {"open": 1, "back": 2, "sigmoid": 3, "r_gh": 4, "back_n": 5, "sum": 5, "tanh": 7, "h_n": 8, "z_d": 7, "out": 9}
 
 ROAD_CAST, ROAD_TURN, ROAD_WEAVE = -1, 0, {GR: 2, GZ: 3}
 X_SLOT, XQUANT_SLOT = 2, 5
@@ -407,8 +407,14 @@ def tile_grucellstack_pa_kernel(tc, x_in, h0, gh0, w_bytes, w_scale, b_ih0, out)
 
         def result(J):
             d = live[("d", J)]
-            nc.vector.tensor_tensor(out=d[:], in0=d[:], in1=live[("r", J)][:], op=ALU.add)
-            nc.sync.dma_start(out=of_pair(out_view, J), in_=by_half(d))
+            if J < PAIRS - 1:
+                nc.vector.tensor_tensor(out=d[:], in0=d[:], in1=live[("r", J)][:], op=ALU.add)
+                nc.sync.dma_start(out=of_pair(out_view, J), in_=by_half(d))
+            else:
+                for h in range(2):
+                    cols = slice(h * 256, (h + 1) * 256)
+                    nc.vector.tensor_tensor(out=d[:, cols], in0=d[:, cols], in1=live[("r", J)][:, cols], op=ALU.add)
+                    nc.sync.dma_start(out=of_pair(out_view, J)[:, h, :], in_=d[:, cols])
 
         steps = []
 

@@ -48,10 +48,11 @@ QUANT_LAG, QUANT_CATCH_UP = 5, (7, 10)
 
 SUMS_LAG = 2
 LAGS = {"open": 4, "back": 4, "sigmoid": 5, "r_gh": 6, "sum": 8, "back_n": 8, "tanh": 9, "h_n": 10, "z_d": 9, "out": 11}
-LAGS_SUM_ON_VECTOR = dict(LAGS, back_n=7, sum=8)
+LAGS_SUM_ON_VECTOR = dict(LAGS, back_n=8, sum=8)
 LAGS_LAST = {"open": 1, "back": 2, "sigmoid": 3, "r_gh": 4, "back_n": 5, "sum": 5, "tanh": 7, "h_n": 8, "z_d": 7, "out": 9}
 
 ROAD_CAST, ROAD_TURN, ROAD_WEAVE = -1, 0, {GR: 2, GZ: 3}
+ROAD_WEAVE_FIRST = {GR: 0, GZ: 2}
 X_SLOT, XQUANT_SLOT = 2, 5
 
 
@@ -446,7 +447,7 @@ def tile_grucellstack_pa_kernel(tc, x_in, h0, gh0, w_bytes, w_scale, b_ih0, out)
             first_slot = 6 * J + (-1 if J == 0 or ORDER[J][0] == GR else 0)
             for s in range(len(road(J))):
                 at(first_slot + ROAD_CAST, S_ROAD + s, road_cast, J, s)
-                at(first_slot + ROAD_WEAVE[road(J)[s]], S_ROAD + 4 + s, road_weave, J, s)
+                at(first_slot + (ROAD_WEAVE_FIRST if J == 0 else ROAD_WEAVE)[road(J)[s]], S_ROAD + 4 + s, road_weave, J, s)
             at(first_slot + ROAD_TURN, T_ROAD, road_turn, J)
             at(first_slot + ROAD_TURN, S_ROAD + 2, road_scale, J, 0)
             at(first_slot + ROAD_TURN, S_ROAD + 3, road_scale, J, 1)

@@ -29,6 +29,7 @@ BLOCK = (2, 0, 1)
 ORDER = ((GN, GR, GZ),) * (PAIRS - 1) + ((GR, GN, GZ),)
 
 ROAD_EARLY, EARLY_PAIRS, ROAD = (GZ,), 0, (GR, GZ)
+N_PAIRS = (1,)
 
 PAIRS_SUM_ON_VECTOR, PAIRS_DIFF_ON_VECTOR = 2, 2
 
@@ -67,6 +68,8 @@ def tile_grucellstack_pa_kernel(tc, x_in, h0, gh0, w_bytes, w_scale, b_ih0, out)
         ctx.enter_context(tc.manual_schedule())
 
         def road(J):
+            if J >= 100:
+                return (GN,)
             return ROAD_EARLY if J < EARLY_PAIRS else ROAD
 
         def road_tiles(J):
@@ -79,13 +82,15 @@ def tile_grucellstack_pa_kernel(tc, x_in, h0, gh0, w_bytes, w_scale, b_ih0, out)
             return 3 * J + ORDER[J].index(g)
 
         def k_vector(J, g):
-            return K_VECTOR if g in road(J) else IN
+            return K_VECTOR if g in road(J) or (g == GN and J in N_PAIRS) else IN
 
         w_view = w_bytes.rearrange("(g j p) k -> p g j k", g=3, p=P)
         w_v = {}
         w_s = {}
         for J in range(PAIRS):
             w_s[J] = wpool.tile([P, road_tiles(J), K_PASS], U8, name="w_s_%d" % J)
+            if J in N_PAIRS:
+                w_s[100 + J] = wpool.tile([P, 2, K_PASS], U8, name="w_s_%d" % (100 + J))
             for g in range(3):
                 if (J, g) == (0, GN):
                     w_v[(J, g)] = wpool.tile([P, PASSES, 2, K_PASS], U8, name="w_v_%d_%d" % (J, g))
@@ -115,7 +120,7 @@ def tile_grucellstack_pa_kernel(tc, x_in, h0, gh0, w_bytes, w_scale, b_ih0, out)
         def load_w_s(J):
             for s in range(len(road(J))):
                 nc.sync.dma_start(
-                    out=w_s[J][:, 2 * s:2 * s + 2, :], in_=w_view[:, BLOCK[road(J)[s]], 2 * J:2 * J + 2, K_VECTOR:IN]
+                    out=w_s[J][:, 2 * s:2 * s + 2, :], in_=w_view[:, BLOCK[road(J)[s]], 2 * (J % 100):2 * (J % 100) + 2, K_VECTOR:IN]
                 )
 
         def load_w_v(J, g):
@@ -131,6 +136,7 @@ def tile_grucellstack_pa_kernel(tc, x_in, h0, gh0, w_bytes, w_scale, b_ih0, out)
             nc.sync.dma_start(out=gh_sb[blk][:], in_=gh_view[:, :, blk, :])
 
         load_w_s(0)
+        load_w_s(101)
         nc.sync.dma_start(out=scales_col[:], in_=w_scale.rearrange("o (g p t) -> p (o g) t", p=P, t=4))
         for c in range(PASSES):
             load_scales(c)
@@ -149,6 +155,8 @@ def tile_grucellstack_pa_kernel(tc, x_in, h0, gh0, w_bytes, w_scale, b_ih0, out)
         nc.sync.dma_start(out=h_sb[:], in_=h0.rearrange("(h p) c -> p h c", p=P))
         load_w_v(1, GZ)
         for J in range(2, PAIRS):
+            if J in N_PAIRS:
+                load_w_s(100 + J)
             load_w_v(J, ORDER[J][0])
             load_w_s(J)
             load_w_v(J, ORDER[J][1])
@@ -169,7 +177,7 @@ def tile_grucellstack_pa_kernel(tc, x_in, h0, gh0, w_bytes, w_scale, b_ih0, out)
         live = {}
 
         def on_road(i):
-            return gate(i // 2) in road(i // 6)
+            return k_vector(i // 6, gate(i // 2)) == K_VECTOR
 
         def grouped_of(m):
             if ("grouped", m) not in live:
@@ -216,7 +224,7 @@ def tile_grucellstack_pa_kernel(tc, x_in, h0, gh0, w_bytes, w_scale, b_ih0, out)
 
         def road_weave(J, s):
             nc.scalar.copy(
-                out=grouped_of(unit(J, road(J)[s]))[:, :, K_VECTOR:IN].rearrange("p j (c t) -> p j c t", t=4),
+                out=grouped_of(unit(J % 100, road(J)[s]))[:, :, K_VECTOR:IN].rearrange("p j (c t) -> p j c t", t=4),
                 in_=live[("planes", J)][:].rearrange("p (t q c) -> p q c t", t=4, q=road_tiles(J))[:, 2 * s:2 * s + 2, :, :],
             )
 
@@ -451,6 +459,13 @@ def tile_grucellstack_pa_kernel(tc, x_in, h0, gh0, w_bytes, w_scale, b_ih0, out)
             at(first_slot + ROAD_TURN, T_ROAD, road_turn, J)
             at(first_slot + ROAD_TURN, S_ROAD + 2, road_scale, J, 0)
             at(first_slot + ROAD_TURN, S_ROAD + 3, road_scale, J, 1)
+            if J in N_PAIRS:
+                fs = 6 * J + (-6)
+                at(fs + ROAD_CAST, S_ROAD, road_cast, 100 + J, 0)
+                at(fs + 3, S_ROAD + 4, road_weave, 100 + J, 0)
+                at(fs + ROAD_TURN, T_ROAD, road_turn, 100 + J)
+                at(fs + ROAD_TURN, S_ROAD + 2, road_scale, 100 + J, 0)
+                at(fs + ROAD_TURN, S_ROAD + 3, road_scale, 100 + J, 1)
             lags = LAGS_LAST if last else (LAGS if sum_on_tensor(J) else LAGS_SUM_ON_VECTOR)
             from_r = quant_slot(unit(J, GR))
             from_z = quant_slot(unit(J, GZ))

@@ -20,41 +20,27 @@ K_PASS = 512
 PASSES = IN // K_PASS
 PAIRS = L // 256
 UNITS = 3 * PAIRS
-TILES = 2 * UNITS
-K_VECTOR = IN - K_PASS
+ROAD_PASS = PASSES - 1
 
 GN, GR, GZ = 0, 1, 2
 BLOCK = (2, 0, 1)
-
 ORDER = ((GN, GR, GZ),) * (PAIRS - 1) + ((GR, GN, GZ),)
 
-ROAD_EARLY, EARLY_PAIRS, ROAD = (GZ,), 0, (GR, GZ)
-N_PAIRS = (1,)
-
-PAIRS_SUM_ON_VECTOR, PAIRS_DIFF_ON_VECTOR = 2, 2
-
 SUM_BANKS, TURN_BANKS, BACK_BANKS = 2, 4, 2
+NO_ROAD = ()
+RUN = (3, 0, 1, 2)
+RUN_FIRST = (0, 3, 1, 2)
 
-V_PRODUCT = 10
-S_TANH, S_SIGMOID, S_SUMS = 20, 21, 26
-T_OPEN, T_BACK, T_TILE, T_BACK_LATE = 29, 30, 31, 32
-S_TILE = 40
-X_FIRST = 41
-V_QUANT, V_XQUANT = 50, 51
-T_PASSES, T_PLAIN, T_ROAD = 60, 62, 63
-V_R_GH, V_H_N, V_OUT, V_SUM, V_Z_D = 70, 71, 72, 73, 74
-S_ROAD = 80
+V_EVAC, V_QUANT = 10, 12
+S_SUMS0, S_CAST, S_SUMS1, S_FUNC, S_SCALED = 20, 22, 24, 26, 28
+T_RUN, T_PASSES, T_OPEN, T_BACK = 32, 40, 44, 45
+G_WEAVE, G_BLEND = 50, 52
 
-QUANT_LAG, QUANT_CATCH_UP = 5, (7, 10)
-
-SUMS_LAG = 2
-LAGS = {"open": 4, "back": 4, "sigmoid": 5, "r_gh": 6, "sum": 8, "back_n": 8, "tanh": 9, "h_n": 10, "z_d": 9, "out": 11}
-LAGS_SUM_ON_VECTOR = dict(LAGS, back_n=8, sum=8)
-LAGS_LAST = {"open": 1, "back": 2, "sigmoid": 3, "r_gh": 4, "back_n": 5, "sum": 5, "tanh": 7, "h_n": 8, "z_d": 7, "out": 9}
-
-ROAD_CAST, ROAD_TURN, ROAD_WEAVE = -1, 0, {GR: 2, GZ: 3}
-ROAD_WEAVE_FIRST = {GR: 0, GZ: 2}
-X_SLOT, XQUANT_SLOT = 2, 5
+LAG = {"cast": (-4, -4, -3, -2), "run": -2, "scaled": -1, "weave": 0, "quant": 3, "passes": 4, "sums": 5, "back": 9, "sigmoid": 10,
+       "r_gh": 11, "back_n": 17, "tanh": 18, "h_n": 21, "z_d": 25, "out": 29}
+LAG_4 = dict(LAG, back_n=13, tanh=14, h_n=17, z_d=20, out=21)
+LAG_LAST = dict(LAG, back_z=6, sigmoid_z=7, back_n=11, tanh=13, h_n=14, z_d=16, out=17)
+X_AFTER = 2
 
 
 def tile_grucellstack_pa_kernel(tc, x_in, h0, gh0, w_bytes, w_scale, b_ih0, out):
@@ -62,18 +48,10 @@ def tile_grucellstack_pa_kernel(tc, x_in, h0, gh0, w_bytes, w_scale, b_ih0, out)
     with ExitStack() as ctx:
         const = ctx.enter_context(tc.tile_pool(name="const", bufs=1))
         wpool = ctx.enter_context(tc.tile_pool(name="wpool", bufs=1))
-        work = ctx.enter_context(tc.tile_pool(name="work", bufs=3))
+        work = ctx.enter_context(tc.tile_pool(name="work", bufs=2))
         ep = ctx.enter_context(tc.tile_pool(name="ep", bufs=2))
         psum = ctx.enter_context(tc.psum_pool(name="psum", bufs=1))
         ctx.enter_context(tc.manual_schedule())
-
-        def road(J):
-            if J >= 100:
-                return (GN,)
-            return ROAD_EARLY if J < EARLY_PAIRS else ROAD
-
-        def road_tiles(J):
-            return 2 * len(road(J))
 
         def gate(m):
             return ORDER[m // 3][m % 3]
@@ -81,22 +59,13 @@ def tile_grucellstack_pa_kernel(tc, x_in, h0, gh0, w_bytes, w_scale, b_ih0, out)
         def unit(J, g):
             return 3 * J + ORDER[J].index(g)
 
-        def k_vector(J, g):
-            return K_VECTOR if g in road(J) or (g == GN and J in N_PAIRS) else IN
+        def on_road(m):
+            return m not in NO_ROAD
 
-        w_view = w_bytes.rearrange("(g j p) k -> p g j k", g=3, p=P)
-        w_v = {}
-        w_s = {}
-        for J in range(PAIRS):
-            w_s[J] = wpool.tile([P, road_tiles(J), K_PASS], U8, name="w_s_%d" % J)
-            if J in N_PAIRS:
-                w_s[100 + J] = wpool.tile([P, 2, K_PASS], U8, name="w_s_%d" % (100 + J))
-            for g in range(3):
-                if (J, g) == (0, GN):
-                    w_v[(J, g)] = wpool.tile([P, PASSES, 2, K_PASS], U8, name="w_v_%d_%d" % (J, g))
-                else:
-                    w_v[(J, g)] = wpool.tile([P, 2, k_vector(J, g)], U8, name="w_v_%d_%d" % (J, g))
-        scales_row = const.tile([P, IN], F32, name="scales_row")
+        w_view = w_bytes.rearrange("(b j q p) (g k) -> p b j q g k", b=3, q=2, p=P, k=K_PASS)
+        w_b = {}
+        for m in range(UNITS):
+            w_b[m] = wpool.tile([P, PASSES, 2, K_PASS], U8, name="w_b_%d" % m)
         scales_col = const.tile([P, PASSES, 4], F32, name="scales_col")
         x_sb = const.tile([P, 2, IN], BF16, name="x_sb")
         h_sb = const.tile([P, 2, L], BF16, name="h_sb")
@@ -111,63 +80,42 @@ def tile_grucellstack_pa_kernel(tc, x_in, h0, gh0, w_bytes, w_scale, b_ih0, out)
         nc.vector.memset(b_rows[:], 0.0)
         nc.scalar.activation(out=warm_out[:], in_=warm_in[:], func=ACT.Sigmoid)
 
-        def load_scales(c):
-            nc.sync.dma_start(
-                out=scales_row[:, c * 512:(c + 1) * 512],
-                in_=w_scale[0:1, c * 512:(c + 1) * 512].rearrange("o k -> (o k)").partition_broadcast(P),
-            )
+        def load_pass(m, g):
+            nc.sync.dma_start(out=w_b[m][:, g, :, :], in_=w_view[:, BLOCK[gate(m)], m // 3, :, g, :])
 
-        def load_w_s(J):
-            for s in range(len(road(J))):
-                nc.sync.dma_start(
-                    out=w_s[J][:, 2 * s:2 * s + 2, :], in_=w_view[:, BLOCK[road(J)[s]], 2 * (J % 100):2 * (J % 100) + 2, K_VECTOR:IN]
-                )
-
-        def load_w_v(J, g):
-            nc.sync.dma_start(out=w_v[(J, g)][:], in_=w_view[:, BLOCK[g], 2 * J:2 * J + 2, 0:k_vector(J, g)])
+        def load_unit(m):
+            for g in RUN:
+                load_pass(m, g)
 
         x_view = x_in.rearrange("(h p) k -> p h k", p=P)
         gh_view = gh0.rearrange("(h p) (g c) -> p h g c", p=P, g=3)
 
-        def load_x(h):
-            nc.sync.dma_start(out=x_sb[:, h, :], in_=x_view[:, h, :])
-
         def load_gh(blk):
             nc.sync.dma_start(out=gh_sb[blk][:], in_=gh_view[:, :, blk, :])
 
-        load_w_s(0)
-        load_w_s(101)
+        load_pass(0, RUN_FIRST[0])
         nc.sync.dma_start(out=scales_col[:], in_=w_scale.rearrange("o (g p t) -> p (o g) t", p=P, t=4))
-        for c in range(PASSES):
-            load_scales(c)
-            nc.sync.dma_start(out=w_v[(0, GN)][:, c, :, :], in_=w_view[:, BLOCK[GN], 0:2, c * 512:(c + 1) * 512])
-        load_w_v(0, GR)
-        load_x(0)
-        load_x(1)
+        for g in RUN_FIRST[1:]:
+            load_pass(0, g)
         nc.sync.dma_start(out=b_rows[0:36, :], in_=b_ih0.rearrange("(c p) -> c p", p=P))
-        load_w_v(0, GZ)
+        load_unit(1)
+        nc.sync.dma_start(out=x_sb[:, 0, :], in_=x_view[:, 0, :])
+        nc.sync.dma_start(out=x_sb[:, 1, :], in_=x_view[:, 1, :])
+        load_unit(2)
+        load_unit(3)
         load_gh(BLOCK[GR])
-        load_w_v(1, GN)
-        load_gh(BLOCK[GN])
+        load_unit(4)
         load_gh(BLOCK[GZ])
-        load_w_s(1)
-        load_w_v(1, GR)
+        load_gh(BLOCK[GN])
+        load_unit(5)
         nc.sync.dma_start(out=h_sb[:], in_=h0.rearrange("(h p) c -> p h c", p=P))
-        load_w_v(1, GZ)
-        for J in range(2, PAIRS):
-            if J in N_PAIRS:
-                load_w_s(100 + J)
-            load_w_v(J, ORDER[J][0])
-            load_w_s(J)
-            load_w_v(J, ORDER[J][1])
-            load_w_v(J, ORDER[J][2])
+        for m in range(6, UNITS):
+            load_unit(m)
 
         ident_f = const.tile([P, P], F32, name="ident_f")
         make_identity(nc, ident_f[:])
         ident_b = const.tile([P, P], BF16, name="ident_b")
         make_identity(nc, ident_b[:])
-        ident_neg = const.tile([P, P], F32, name="ident_neg")
-        nc.scalar.mul(out=ident_neg[:], in_=ident_f[:], mul=-1.0)
 
         x_grouped = const.tile([P, PASSES * B * 4], BF16, name="x_grouped", align_bytes=64)
         x_codes = const.tile([P, PASSES * B], U32, name="x_codes", align_bytes=64)
@@ -176,128 +124,90 @@ def tile_grucellstack_pa_kernel(tc, x_in, h0, gh0, w_bytes, w_scale, b_ih0, out)
 
         live = {}
 
-        def on_road(i):
-            return k_vector(i // 6, gate(i // 2)) == K_VECTOR
-
-        def grouped_of(m):
-            if ("grouped", m) not in live:
-                live[("grouped", m)] = work.tile([P, 2, IN], BF16, name="grouped", bufs=5, align_bytes=64)
-            return live[("grouped", m)]
-
         def turn_bank():
             return psum.tile([P, 512], F32, name="turn", tag="turn", bufs=TURN_BANKS)
 
         def back_bank():
             return psum.tile([P, 512], F32, name="back", tag="back", bufs=BACK_BANKS)
 
-        def road_cast(J, s):
-            if s == 0:
-                live[("cast", J)] = work.tile([P, road_tiles(J) * K_PASS], BF16, name="cast", bufs=2)
+        def cast(m, g):
+            if ("cast", m) not in live:
+                live[("cast", m)] = work.tile([P, 2 * IN], BF16, name="cast", bufs=3)
             nc.scalar.copy(
-                out=live[("cast", J)][:, s * 1024:(s + 1) * 1024],
-                in_=w_s[J][:, 2 * s:2 * s + 2, :].rearrange("p q k -> p (q k)").bitcast(FP8),
+                out=live[("cast", m)][:, g * 1024:(g + 1) * 1024],
+                in_=w_b[m][:, g, :, :].rearrange("p q k -> p (q k)").bitcast(FP8),
             )
 
-        def road_turn(J):
-            words = live[("cast", J)][:].bitcast(F32)
+        def turn(m, g):
+            words = live[("cast", m)][:].bitcast(F32)
+            bank = turn_bank()
+            live[("bank", m, g)] = bank
             for u in range(2):
-                if u == 0 or road_tiles(J) == 4:
-                    bank = turn_bank()
-                live[("road_bank", J, u)] = bank
-                for q in range(road_tiles(J)):
-                    col = (q + (2 * u if road_tiles(J) == 2 else 0)) * P
-                    nc.tensor.transpose(bank[:, col:col + P], words[:, q * 256 + u:(q + 1) * 256:2], ident_f[:])
+                for q in range(2):
+                    col = (2 * u + q) * P
+                    first = g * 512 + q * 256
+                    nc.tensor.transpose(bank[:, col:col + P], words[:, first + u:first + 256:2], ident_f[:])
 
-        def road_scale(J, u):
-            n_q = road_tiles(J)
-            if u == 0:
-                live[("planes", J)] = work.tile([P, n_q * K_PASS], BF16, name="planes", bufs=2)
-            halves = live[("road_bank", J, u)][:].bitcast(BF16)
-            first = u * 512 if n_q == 2 else 0
-            for e in range(2):
-                t = 2 * u + e
-                nc.scalar.activation(
-                    out=live[("planes", J)][:, t * n_q * P:(t + 1) * n_q * P],
-                    in_=halves[:, first + e:first + n_q * 256:2],
-                    func=ACT.Copy, scale=scales_col[:, PASSES - 1, t:t + 1],
-                )
+        def main_of(m):
+            if ("main", m) not in live:
+                live[("main", m)] = work.tile([P, 3 * 1024], BF16, name="main", bufs=2, align_bytes=64)
+            return live[("main", m)]
 
-        def road_weave(J, s):
-            nc.scalar.copy(
-                out=grouped_of(unit(J % 100, road(J)[s]))[:, :, K_VECTOR:IN].rearrange("p j (c t) -> p j c t", t=4),
-                in_=live[("planes", J)][:].rearrange("p (t q c) -> p q c t", t=4, q=road_tiles(J))[:, 2 * s:2 * s + 2, :, :],
-            )
+        def woven_of(m):
+            if ("woven", m) not in live:
+                live[("woven", m)] = work.tile([P, 1024], BF16, name="woven", bufs=1, align_bytes=64)
+            return live[("woven", m)]
 
-        def product(i):
-            J, g, j = i // 6, gate(i // 2), i % 2
-            scaled = work.tile([P, IN], BF16, name="scaled", bufs=3)
-            live[("scaled", i)] = scaled
-            width = k_vector(J, g)
+        def evac(m, g):
+            dst = woven_of(m)[:] if g == ROAD_PASS else main_of(m)[:, g * 1024:(g + 1) * 1024]
             nc.vector.tensor_tensor(
-                out=scaled[:, 0:width], in0=w_v[(J, g)][:, j, :].bitcast(FP8), in1=scales_row[:, 0:width], op=ALU.mult
+                out=dst.rearrange("p (a u e) -> p a u e", u=2, e=2),
+                in0=live[("bank", m, g)][:].bitcast(BF16).rearrange("p (u a e) -> p a u e", u=2, e=2),
+                in1=scales_col[:, g, :].unsqueeze(1).to_broadcast([P, 256, 4]).rearrange("p a (u e) -> p a u e", u=2),
+                op=ALU.mult,
             )
 
-        def first_products():
-            for j in range(2):
-                live[("scaled", j)] = work.tile([P, IN], BF16, name="scaled", bufs=3)
-            for c in range(PASSES):
-                cols = slice(c * 512, (c + 1) * 512)
-                for j in range(2):
-                    nc.vector.tensor_tensor(
-                        out=live[("scaled", j)][:, cols], in0=w_v[(0, GN)][:, c, j, :].bitcast(FP8),
-                        in1=scales_row[:, cols], op=ALU.mult,
-                    )
-
-        def tile_turn(i):
-            words = live[("scaled", i)][:].bitcast(F32)
-            banks = (turn_bank(), turn_bank())
-            live[("banks", i)] = banks
-            for g in range(k_vector(i // 6, gate(i // 2)) // K_PASS):
-                for u in range(2):
-                    col = ((g % 2) * 2 + u) * P
-                    nc.tensor.transpose(
-                        banks[g // 2][:, col:col + P], words[:, 256 * g + u:256 * (g + 1):2], ident_f[:]
-                    )
-
-        def tile_out(i):
-            dst = grouped_of(i // 2)[:, i % 2, :].bitcast(F32)
-            banks = live[("banks", i)]
-            nc.scalar.copy(
-                out=dst[:, 0:512].rearrange("p (g c u) -> p g c u", g=2, u=2),
-                in_=banks[0][:].rearrange("p (g u c) -> p g c u", g=2, u=2),
+        def scaled(m, t):
+            if t == 0:
+                live[("planes", m)] = work.tile([P, 1024], BF16, name="planes", bufs=2)
+            halves = live[("bank", m, ROAD_PASS)][:].bitcast(BF16)
+            u, e = t // 2, t % 2
+            nc.scalar.activation(
+                out=live[("planes", m)][:, t * 256:(t + 1) * 256], in_=halves[:, u * 512 + e:(u + 1) * 512:2],
+                func=ACT.Copy, scale=scales_col[:, ROAD_PASS, t:t + 1],
             )
-            if on_road(i):
-                nc.scalar.copy(
-                    out=dst[:, 512:768].rearrange("p (c u) -> p c u", u=2),
-                    in_=banks[1][:, 0:256].rearrange("p (u c) -> p c u", u=2),
-                )
-            else:
-                nc.scalar.copy(
-                    out=dst[:, 512:1024].rearrange("p (g c u) -> p g c u", g=2, u=2),
-                    in_=banks[1][:].rearrange("p (g u c) -> p g c u", g=2, u=2),
-                )
+
+        def weave(m):
+            nc.gpsimd.tensor_scalar(
+                out=woven_of(m)[:].rearrange("p (a t) -> p a t", t=4),
+                in0=live[("planes", m)][:].rearrange("p (t a) -> p a t", t=4),
+                scalar1=1.0, scalar2=0.0, op0=ALU.mult, op1=ALU.add,
+            )
 
         def quantise(m):
-            live[("codes", m)] = work.tile([P, 1024], U32, name="codes", bufs=2, align_bytes=64)
-            live[("scales", m)] = work.tile([P, 1024], U8, name="scales", bufs=2, align_bytes=64)
-            nc.vector.quantize_mx(
-                out=live[("codes", m)][:].bitcast(FP8X4), scales=live[("scales", m)][:],
-                in_=live[("grouped", m)][:].rearrange("p j k -> p (j k)"),
-            )
+            live[("codes", m)] = work.tile([P, 1024], U32, name="codes", bufs=3, align_bytes=64)
+            live[("scales", m)] = work.tile([P, 1024], U8, name="scales", bufs=3, align_bytes=64)
+            codes, scales = live[("codes", m)], live[("scales", m)]
+            for src, first, last in ((main_of(m)[:, 0:2048], 0, 512), (main_of(m)[:, 2048:3072], 512, 768)):
+                nc.vector.quantize_mx(out=codes[:, first:last].bitcast(FP8X4), scales=scales[:, first:last], in_=src)
+
+        def quantise_road(m):
+            codes, scales = live[("codes", m)], live[("scales", m)]
+            nc.vector.quantize_mx(out=codes[:, 768:1024].bitcast(FP8X4), scales=scales[:, 768:1024], in_=woven_of(m)[:])
 
         def passes(m, j):
             if j == 0:
-                bank = "sums_%d" % (m % SUM_BANKS)
-                live[("sums", m)] = psum.tile([P, 512], F32, name=bank, tag=bank, bufs=1)
-            for g in range(PASSES):
-                col = j * 512 + g * P
+                live[("sums", m)] = psum.tile([P, 512], F32, name="sums", tag="sums", bufs=SUM_BANKS)
+            order = (0, 1, 2, 3)
+            for g in order:
+                col = g * 256 + j * P
                 nc.tensor.matmul_mx(
                     out=live[("sums", m)][:, j * B:(j + 1) * B],
                     lhsT=live[("codes", m)][:, col:col + P].bitcast(FP8X4),
                     lhsT_scale=live[("scales", m)][:, col:col + P],
                     rhs=x_codes[:, g * B:(g + 1) * B].bitcast(FP8X4),
                     rhs_scale=x_scales[:, g * B:(g + 1) * B],
-                    start=(g == 0), stop=(g == PASSES - 1),
+                    start=(g == order[0]), stop=(g == order[-1]),
                 )
 
         def x_turn(g):
@@ -320,17 +230,11 @@ def tile_grucellstack_pa_kernel(tc, x_in, h0, gh0, w_bytes, w_scale, b_ih0, out)
             nc.vector.quantize_mx(out=x_codes[:].bitcast(FP8X4), scales=x_scales[:], in_=x_grouped[:])
 
         def bias_turn():
-            live["bias_bank"] = psum.tile([P, 1024], BF16, name="bias_bank", tag="turn", bufs=TURN_BANKS)
+            live["bias_bank"] = psum.tile([P, 1024], BF16, name="bias_bank", tag="back", bufs=BACK_BANKS)
             nc.tensor.transpose(live["bias_bank"][:, 0:P], b_rows[:], ident_b[:])
 
         def bias_out():
             nc.scalar.copy(out=bias_col[:], in_=live["bias_bank"][:, 0:36])
-
-        def sum_on_tensor(J):
-            return J < PAIRS - PAIRS_SUM_ON_VECTOR
-
-        def diff_on_tensor(J):
-            return J < PAIRS - PAIRS_DIFF_ON_VECTOR
 
         def by_half(t):
             return t[:].rearrange("p (h c) -> p h c", h=2)
@@ -338,16 +242,21 @@ def tile_grucellstack_pa_kernel(tc, x_in, h0, gh0, w_bytes, w_scale, b_ih0, out)
         def of_pair(t, J):
             return t[:, :, J * 256:(J + 1) * 256]
 
-        def sums_out(m):
+        def blender(J, late=True):
+            return nc.vector if J == PAIRS - 1 or (late and J == PAIRS - 2) else nc.gpsimd
+
+        def sum_on_tensor(J):
+            return J < PAIRS - 1
+
+        def sums_out(m, j):
             J, g = m // 3, gate(m)
-            biased = ep.tile([P, 512], F32, name="biased_n" if g == GN else "biased", bufs=3)
-            live[("biased", m)] = biased
-            for j in range(2):
-                c = BLOCK[g] * 12 + 2 * J + j
-                nc.scalar.activation(
-                    out=biased[:, j * B:(j + 1) * B], in_=live[("sums", m)][:, j * B:(j + 1) * B],
-                    func=ACT.Identity, bias=bias_col[:, c:c + 1], scale=1.0,
-                )
+            if j == 0:
+                live[("biased", m)] = ep.tile([P, 512], F32, name="biased_n" if g == GN else "biased", bufs=3)
+            c = BLOCK[g] * 12 + 2 * J + j
+            nc.scalar.activation(
+                out=live[("biased", m)][:, j * B:(j + 1) * B], in_=live[("sums", m)][:, j * B:(j + 1) * B],
+                func=ACT.Identity, bias=bias_col[:, c:c + 1], scale=1.0,
+            )
 
         def open_with_gh(m):
             live[("back", m)] = back_bank()
@@ -393,31 +302,21 @@ def tile_grucellstack_pa_kernel(tc, x_in, h0, gh0, w_bytes, w_scale, b_ih0, out)
             nc.scalar.activation(out=r[:], in_=src[:], func=ACT.Tanh)
 
         def h_minus_n(J):
-            if diff_on_tensor(J):
-                bank = back_bank()
-                live[("diff", J)] = bank
-                nc.tensor.matmul(out=bank[:], lhsT=ident_neg[:], rhs=live[("r", J)][:], start=True, stop=False)
-                nc.tensor.matmul(out=by_half(bank), lhsT=ident_b[:], rhs=of_pair(h_sb, J), start=False, stop=True)
-            else:
-                live[("d", J)] = ep.tile([P, 512], F32, name="d")
-                nc.vector.tensor_tensor(
-                    out=by_half(live[("d", J)]), in0=of_pair(h_sb, J), in1=by_half(live[("r", J)]), op=ALU.subtract
-                )
+            live[("d", J)] = ep.tile([P, 512], F32, name="d", bufs=2)
+            blender(J, False).tensor_tensor(
+                out=by_half(live[("d", J)]), in0=of_pair(h_sb, J), in1=by_half(live[("r", J)]), op=ALU.subtract
+            )
 
         def z_times_diff(J):
-            if diff_on_tensor(J):
-                live[("d", J)] = ep.tile([P, 512], F32, name="d")
-                diff = live[("diff", J)]
-            else:
-                diff = live[("d", J)]
-            nc.vector.tensor_tensor(out=live[("d", J)][:], in0=diff[:], in1=live[("z", J)][:], op=ALU.mult)
+            d = live[("d", J)]
+            blender(J).tensor_tensor(out=d[:], in0=d[:], in1=live[("z", J)][:], op=ALU.mult)
 
         out_view = out.rearrange("(h p) c -> p h c", p=P)
 
         def result(J):
             d = live[("d", J)]
             if J < PAIRS - 1:
-                nc.vector.tensor_tensor(out=d[:], in0=d[:], in1=live[("r", J)][:], op=ALU.add)
+                blender(J).tensor_tensor(out=d[:], in0=d[:], in1=live[("r", J)][:], op=ALU.add)
                 nc.sync.dma_start(out=of_pair(out_view, J), in_=by_half(d))
             else:
                 for h in range(2):
@@ -430,58 +329,54 @@ def tile_grucellstack_pa_kernel(tc, x_in, h0, gh0, w_bytes, w_scale, b_ih0, out)
         def at(slot, place, fn, *args):
             steps.append((slot, place, len(steps), fn, args))
 
-        def quant_slot(m):
-            return 2 * m + QUANT_LAG - sum([1 for c in QUANT_CATCH_UP if m >= c])
+        def base(m):
+            return 4 * (m if m < X_AFTER else m + 1)
 
-        at(0, V_PRODUCT, first_products)
-        for i in range(TILES):
-            if i >= 2:
-                at(i, V_PRODUCT, product, i)
-            at(i, T_TILE, tile_turn, i)
-            at(i, S_TILE, tile_out, i)
-        for g in range(PASSES):
-            at(X_SLOT, X_FIRST + 2 * g, x_turn, g)
-            at(X_SLOT, X_FIRST + 2 * g + 1, x_out, g)
-        at(XQUANT_SLOT, V_XQUANT, x_quantise)
-        at(X_SLOT + 1, X_FIRST, bias_turn)
-        at(X_SLOT + 1, X_FIRST + 1, bias_out)
+        b_x = 4 * X_AFTER
         for m in range(UNITS):
-            at(quant_slot(m), V_QUANT, quantise, m)
-            at(quant_slot(m), T_PASSES, passes, m, 0)
-            at(quant_slot(m) + 1, T_PASSES, passes, m, 1)
-            at(quant_slot(m) + SUMS_LAG, S_SUMS + m % 3, sums_out, m)
+            b = base(m)
+            lag = LAG_LAST if m >= UNITS - 3 else LAG
+            run = RUN_FIRST if m == 0 else RUN
+            for i in range(PASSES):
+                at(b + lag["cast"][i], S_CAST, cast, m, run[i])
+                at(b + lag["run"], T_RUN + i, turn, m, run[i])
+            for g in range(PASSES):
+                if g != ROAD_PASS or not on_road(m):
+                    at(b + g, V_EVAC, evac, m, g)
+            if on_road(m):
+                for t in range(4):
+                    at(b + lag["scaled"], S_SCALED, scaled, m, t)
+                at(b + lag["weave"], G_WEAVE, weave, m)
+            at(b + lag["quant"], V_QUANT, quantise, m)
+            at(b + lag["quant"], V_QUANT + 2, quantise_road, m)
+            late = max(0, b_x + 4 - (b + lag["passes"]))
+            at(b + lag["passes"] + late, T_PASSES, passes, m, 0)
+            at(b + lag["passes"] + late, T_PASSES, passes, m, 1)
+            at(b + lag["sums"] + late, S_SUMS0, sums_out, m, 0)
+            at(b + lag["sums"] + late, S_SUMS1, sums_out, m, 1)
+        for g in range(PASSES):
+            at(b_x + LAG["run"], T_RUN + g, x_turn, g)
+            at(b_x - 1 + g // 2, S_SCALED + 1, x_out, g)
+        at(b_x + 1, V_QUANT, x_quantise)
+        at(0, T_RUN, bias_turn)
+        at(b_x + 1, S_SUMS0, bias_out)
         for J in range(PAIRS):
-            last = J == PAIRS - 1
-            first_slot = 6 * J + (-1 if J == 0 or ORDER[J][0] == GR else 0)
-            for s in range(len(road(J))):
-                at(first_slot + ROAD_CAST, S_ROAD + s, road_cast, J, s)
-                at(first_slot + (ROAD_WEAVE_FIRST if J == 0 else ROAD_WEAVE)[road(J)[s]], S_ROAD + 4 + s, road_weave, J, s)
-            at(first_slot + ROAD_TURN, T_ROAD, road_turn, J)
-            at(first_slot + ROAD_TURN, S_ROAD + 2, road_scale, J, 0)
-            at(first_slot + ROAD_TURN, S_ROAD + 3, road_scale, J, 1)
-            if J in N_PAIRS:
-                fs = 6 * J + (-6)
-                at(fs + ROAD_CAST, S_ROAD, road_cast, 100 + J, 0)
-                at(fs + 3, S_ROAD + 4, road_weave, 100 + J, 0)
-                at(fs + ROAD_TURN, T_ROAD, road_turn, 100 + J)
-                at(fs + ROAD_TURN, S_ROAD + 2, road_scale, 100 + J, 0)
-                at(fs + ROAD_TURN, S_ROAD + 3, road_scale, 100 + J, 1)
-            lags = LAGS_LAST if last else (LAGS if sum_on_tensor(J) else LAGS_SUM_ON_VECTOR)
-            from_r = quant_slot(unit(J, GR))
-            from_z = quant_slot(unit(J, GZ))
+            lag = LAG_LAST if J == PAIRS - 1 else (LAG_4 if J == PAIRS - 2 else LAG)
+            b_r, b_z = base(unit(J, GR)), base(unit(J, GZ))
             for m in (unit(J, GR), unit(J, GZ)):
-                at(quant_slot(m) + lags["open"], T_PLAIN if last else T_OPEN, open_with_gh, m)
-                at(quant_slot(m) + lags["back"], T_BACK_LATE if last else T_BACK, turn_back, m)
-                at(quant_slot(m) + lags["sigmoid"], S_SIGMOID + m % 3, sigmoid, m)
-            at(from_r + lags["back_n"], T_BACK, turn_back, unit(J, GN))
-            at(from_r + lags["r_gh"], V_R_GH, r_gh, J)
+                back = lag.get("back_z", lag["back"]) if gate(m) == GZ else lag["back"]
+                at(base(m) + back, T_OPEN, open_with_gh, m)
+                at(base(m) + back, T_BACK, turn_back, m)
+                at(base(m) + back + 1, S_FUNC, sigmoid, m)
+            at(b_r + lag["r_gh"], V_QUANT + 1, r_gh, J)
             if sum_on_tensor(J):
-                at(from_r + lags["sum"], T_OPEN, open_with_r_gh, J)
-            else:
-                at(from_r + lags["sum"], V_SUM, n_sum, J)
-            at(from_r + lags["tanh"], S_TANH, tanh, J)
-            at(from_r + lags["h_n"], T_BACK_LATE if diff_on_tensor(J) else V_H_N, h_minus_n, J)
-            at(from_z + lags["z_d"], V_Z_D, z_times_diff, J)
-            at(from_z + lags["out"], V_OUT, result, J)
+                at(b_r + lag["back_n"], T_OPEN, open_with_r_gh, J)
+            at(b_r + lag["back_n"], T_BACK, turn_back, unit(J, GN))
+            if not sum_on_tensor(J):
+                at(b_r + lag["back_n"] + 1, V_QUANT + 1, n_sum, J)
+            at(b_r + lag["tanh"], S_FUNC, tanh, J)
+            at(b_r + lag["h_n"], G_BLEND, h_minus_n, J)
+            at(b_r + lag["z_d"], G_BLEND, z_times_diff, J)
+            at(b_r + lag["out"], G_BLEND, result, J)
         for step in sorted(steps, key=lambda e: e[0:3]):
             step[3](*step[4])

@@ -27,7 +27,7 @@ BLOCK = (2, 0, 1)
 ORDER = ((GN, GR, GZ),) * (PAIRS - 1) + ((GR, GN, GZ),)
 
 SUM_BANKS, TURN_BANKS, BACK_BANKS = 2, 4, 2
-NO_ROAD = ()
+NO_ROAD = (5, 11)
 RUN = (3, 0, 1, 2)
 RUN_FIRST = (0, 3, 1, 2)
 
@@ -36,11 +36,13 @@ S_SUMS0, S_CAST, S_SUMS1, S_FUNC, S_SCALED = 20, 22, 24, 26, 28
 T_RUN, T_PASSES, T_OPEN, T_BACK = 32, 40, 44, 45
 G_WEAVE, G_BLEND = 50, 52
 
-LAG = {"cast": (-4, -4, -3, -2), "run": -2, "scaled": -1, "weave": 0, "quant": 3, "passes": 4, "sums": 5, "back": 9, "sigmoid": 10,
-       "r_gh": 11, "back_n": 17, "tanh": 18, "h_n": 21, "z_d": 25, "out": 29}
-LAG_4 = dict(LAG, back_n=13, tanh=14, h_n=17, z_d=20, out=21)
-LAG_LAST = dict(LAG, back_z=6, sigmoid_z=7, back_n=11, tanh=13, h_n=14, z_d=16, out=17)
-X_AFTER = 2
+LAG = {"cast": (-4, -4, -3, -3), "run": -2, "scaled": -1, "weave": 0, "quant": 3, "passes": 4, "sums": 5, "back": 9, "sigmoid": 10,
+       "r_gh": 15, "back_n": 17, "tanh": 18, "h_n": 21, "z_d": 25, "out": 29}
+LAG_4 = dict(LAG, r_gh=11, back_n=13, tanh=14, h_n=17, z_d=20, out=21)
+LAG_LAST = dict(LAG, r_gh=11, back_z=6, sigmoid_z=7, back_n=11, tanh=13, h_n=14, z_d=16, out=17)
+X_AFTER = 0
+X_TURN, X_OUT, X_QUANT = 2, (7, 7, 7, 7), 11
+AFTER_HEAD = (8, 8, 12, 12)
 
 
 def tile_grucellstack_pa_kernel(tc, x_in, h0, gh0, w_bytes, w_scale, b_ih0, out):
@@ -80,8 +82,11 @@ def tile_grucellstack_pa_kernel(tc, x_in, h0, gh0, w_bytes, w_scale, b_ih0, out)
         nc.vector.memset(b_rows[:], 0.0)
         nc.scalar.activation(out=warm_out[:], in_=warm_in[:], func=ACT.Sigmoid)
 
+        def run_of(m):
+            return RUN_FIRST if m == 0 else RUN
+
         def load_pass(m, g):
-            nc.sync.dma_start(out=w_b[m][:, g, :, :], in_=w_view[:, BLOCK[gate(m)], m // 3, :, g, :])
+            nc.sync.dma_start(out=w_b[m][:, run_of(m).index(g), :, :], in_=w_view[:, BLOCK[gate(m)], m // 3, :, g, :])
 
         def load_unit(m):
             for g in RUN:
@@ -130,12 +135,12 @@ def tile_grucellstack_pa_kernel(tc, x_in, h0, gh0, w_bytes, w_scale, b_ih0, out)
         def back_bank():
             return psum.tile([P, 512], F32, name="back", tag="back", bufs=BACK_BANKS)
 
-        def cast(m, g):
+        def cast(m, i, n):
             if ("cast", m) not in live:
                 live[("cast", m)] = work.tile([P, 2 * IN], BF16, name="cast", bufs=3)
             nc.scalar.copy(
-                out=live[("cast", m)][:, g * 1024:(g + 1) * 1024],
-                in_=w_b[m][:, g, :, :].rearrange("p q k -> p (q k)").bitcast(FP8),
+                out=live[("cast", m)][:, i * 1024:(i + n) * 1024],
+                in_=w_b[m][:, i:i + n, :, :].rearrange("p g q k -> p (g q k)").bitcast(FP8),
             )
 
         def turn(m, g):
@@ -145,7 +150,7 @@ def tile_grucellstack_pa_kernel(tc, x_in, h0, gh0, w_bytes, w_scale, b_ih0, out)
             for u in range(2):
                 for q in range(2):
                     col = (2 * u + q) * P
-                    first = g * 512 + q * 256
+                    first = run_of(m).index(g) * 512 + q * 256
                     nc.tensor.transpose(bank[:, col:col + P], words[:, first + u:first + 256:2], ident_f[:])
 
         def main_of(m):
@@ -211,7 +216,10 @@ def tile_grucellstack_pa_kernel(tc, x_in, h0, gh0, w_bytes, w_scale, b_ih0, out)
                 )
 
         def x_turn(g):
-            bank = turn_bank()
+            if g < 2:
+                bank = psum.tile([P, 512], F32, name="sums", tag="sums", bufs=SUM_BANKS)
+            else:
+                bank = back_bank()
             live[("x_bank", g)] = bank
             for u in range(2):
                 for h in range(2):
@@ -330,44 +338,50 @@ def tile_grucellstack_pa_kernel(tc, x_in, h0, gh0, w_bytes, w_scale, b_ih0, out)
             steps.append((slot, place, len(steps), fn, args))
 
         def base(m):
-            return 4 * (m if m < X_AFTER else m + 1)
+            return 4 * m
 
         b_x = 4 * X_AFTER
+
+        def after(m):
+            return max(base(m), AFTER_HEAD[m]) if m < len(AFTER_HEAD) else base(m)
+
         for m in range(UNITS):
             b = base(m)
             lag = LAG_LAST if m >= UNITS - 3 else LAG
-            run = RUN_FIRST if m == 0 else RUN
             for i in range(PASSES):
-                at(b + lag["cast"][i], S_CAST, cast, m, run[i])
-                at(b + lag["run"], T_RUN + i, turn, m, run[i])
-            for g in range(PASSES):
-                if g != ROAD_PASS or not on_road(m):
-                    at(b + g, V_EVAC, evac, m, g)
+                if m == 0:
+                    at(b + lag["cast"][i], S_CAST, cast, m, i, 1)
+                elif i % 2 == 0:
+                    at(b + lag["cast"][i], S_CAST, cast, m, i, 2)
+                at(b + lag["run"], T_RUN + i, turn, m, run_of(m)[i])
+            if not on_road(m):
+                at(b, V_EVAC - 1, evac, m, ROAD_PASS)
+            for g in range(PASSES - 1):
+                at(b + g, V_EVAC, evac, m, g)
             if on_road(m):
                 for t in range(4):
                     at(b + lag["scaled"], S_SCALED, scaled, m, t)
                 at(b + lag["weave"], G_WEAVE, weave, m)
             at(b + lag["quant"], V_QUANT, quantise, m)
             at(b + lag["quant"], V_QUANT + 2, quantise_road, m)
-            late = max(0, b_x + 4 - (b + lag["passes"]))
-            at(b + lag["passes"] + late, T_PASSES, passes, m, 0)
-            at(b + lag["passes"] + late, T_PASSES, passes, m, 1)
-            at(b + lag["sums"] + late, S_SUMS0, sums_out, m, 0)
-            at(b + lag["sums"] + late, S_SUMS1, sums_out, m, 1)
-        for g in range(PASSES):
-            at(b_x + LAG["run"], T_RUN + g, x_turn, g)
-            at(b_x - 1 + g // 2, S_SCALED + 1, x_out, g)
-        at(b_x + 1, V_QUANT, x_quantise)
+            at(after(m) + lag["passes"], T_PASSES, passes, m, 0)
+            at(after(m) + lag["passes"], T_PASSES, passes, m, 1)
+            at(after(m) + lag["sums"], S_SUMS0, sums_out, m, 0)
+            at(after(m) + lag["sums"], S_SUMS1 if after(m) == base(m) else S_SUMS0, sums_out, m, 1)
         at(0, T_RUN, bias_turn)
-        at(b_x + 1, S_SUMS0, bias_out)
+        at(1, S_SUMS0, bias_out)
+        for g in range(PASSES):
+            at(b_x + X_TURN, T_RUN + 4 + g, x_turn, g)
+            at(b_x + X_OUT[g], S_SCALED + 1, x_out, g)
+        at(b_x + X_QUANT, V_QUANT + 3, x_quantise)
         for J in range(PAIRS):
             lag = LAG_LAST if J == PAIRS - 1 else (LAG_4 if J == PAIRS - 2 else LAG)
-            b_r, b_z = base(unit(J, GR)), base(unit(J, GZ))
+            b_r = after(unit(J, GR))
             for m in (unit(J, GR), unit(J, GZ)):
                 back = lag.get("back_z", lag["back"]) if gate(m) == GZ else lag["back"]
-                at(base(m) + back, T_OPEN, open_with_gh, m)
-                at(base(m) + back, T_BACK, turn_back, m)
-                at(base(m) + back + 1, S_FUNC, sigmoid, m)
+                at(after(m) + back, T_OPEN, open_with_gh, m)
+                at(after(m) + back, T_BACK, turn_back, m)
+                at(after(m) + back + 1, S_FUNC, sigmoid, m)
             at(b_r + lag["r_gh"], V_QUANT + 1, r_gh, J)
             if sum_on_tensor(J):
                 at(b_r + lag["back_n"], T_OPEN, open_with_r_gh, J)

@@ -27,22 +27,32 @@ BLOCK = (2, 0, 1)
 ORDER = ((GN, GR, GZ),) * (PAIRS - 1) + ((GR, GN, GZ),)
 
 SUM_BANKS, TURN_BANKS, BACK_BANKS = 2, 4, 2
-NO_ROAD = (5, 11)
+NO_ROAD = ()
 RUN = (3, 0, 1, 2)
 RUN_FIRST = (0, 3, 1, 2)
 
 V_EVAC, V_QUANT = 10, 12
-S_SUMS0, S_CAST, S_SUMS1, S_FUNC, S_SCALED = 20, 22, 24, 26, 28
-T_RUN, T_PASSES, T_OPEN, T_BACK = 32, 40, 44, 45
+S_SUMS, S_CAST, S_FUNC, S_SCALED = 20, 22, 24, 26
+T_PASSES, T_RUN, T_OPEN, T_BACK = 30, 32, 36, 37
 G_WEAVE, G_BLEND = 50, 52
 
-LAG = {"cast": (-4, -4, -3, -3), "run": -2, "scaled": -1, "weave": 0, "quant": 3, "passes": 4, "sums": 5, "back": 9, "sigmoid": 10,
-       "r_gh": 15, "back_n": 17, "tanh": 18, "h_n": 21, "z_d": 25, "out": 29}
-LAG_4 = dict(LAG, r_gh=11, back_n=13, tanh=14, h_n=17, z_d=20, out=21)
-LAG_LAST = dict(LAG, r_gh=11, back_z=6, sigmoid_z=7, back_n=11, tanh=13, h_n=14, z_d=16, out=17)
-X_AFTER = 0
+CAST, RUN_LAG, SCALED, WEAVE, QUANT = (-4, -4, -4, -4), (-3, -3, -1, -1), -2, 0, 3
+UNIT_LAG = {"passes": 4, "sums": 9, "back": 14, "func": 18}
+UNIT_LAST = {13: {"passes": 4, "sums": 9, "back": 14, "func": 15}, 14: {"passes": 4, "sums": 9, "back": 11, "func": 12},
+             15: {"passes": 4, "sums": 7, "back": 9, "func": 10}, 16: {"passes": 4, "sums": 6},
+             17: {"passes": 4, "sums": 5, "back": 6, "func": 7}}
+PAIR_LAG = {"r_gh": 19, "back_n": 22, "tanh": 26, "h_n": 29, "z_d": 33, "out": 37}
+PAIR_LAST = {3: {"r_gh": 19, "back_n": 22, "tanh": 26, "h_n": 29, "z_d": 33, "out": 34},
+             4: {"r_gh": 17, "back_n": 18, "tanh": 19, "h_n": 20, "z_d": 20, "out": 21},
+             5: {"r_gh": 11, "back_n": 11, "tanh": 13, "h_n": 14, "z_d": 16, "out": 17}}
+ON_VECTOR = (4, 5)
+SUMS_ON_VECTOR = (4, 7, 10, 13)
+SUMS_V = -2
+CAST_BUFS = 3
+HEAD_ON_VECTOR = (1, 3)
 X_TURN, X_OUT, X_QUANT = 2, (7, 7, 7, 7), 11
 AFTER_HEAD = (8, 8, 12, 12)
+HEAD_LAG = {"passes": 4, "sums": 5, "back": 10, "func": 14}
 
 
 def tile_grucellstack_pa_kernel(tc, x_in, h0, gh0, w_bytes, w_scale, b_ih0, out):
@@ -137,11 +147,13 @@ def tile_grucellstack_pa_kernel(tc, x_in, h0, gh0, w_bytes, w_scale, b_ih0, out)
 
         def cast(m, i, n):
             if ("cast", m) not in live:
-                live[("cast", m)] = work.tile([P, 2 * IN], BF16, name="cast", bufs=3)
-            nc.scalar.copy(
-                out=live[("cast", m)][:, i * 1024:(i + n) * 1024],
-                in_=w_b[m][:, i:i + n, :, :].rearrange("p g q k -> p (g q k)").bitcast(FP8),
-            )
+                live[("cast", m)] = work.tile([P, 2 * IN], BF16, name="cast", bufs=CAST_BUFS)
+            dst = live[("cast", m)][:, i * 1024:(i + n) * 1024]
+            src = w_b[m][:, i:i + n, :, :].rearrange("p g q k -> p (g q k)").bitcast(FP8)
+            if m == 0 and i in HEAD_ON_VECTOR:
+                nc.vector.tensor_copy(out=dst, in_=src)
+            else:
+                nc.scalar.copy(out=dst, in_=src)
 
         def turn(m, g):
             words = live[("cast", m)][:].bitcast(F32)
@@ -251,7 +263,7 @@ def tile_grucellstack_pa_kernel(tc, x_in, h0, gh0, w_bytes, w_scale, b_ih0, out)
             return t[:, :, J * 256:(J + 1) * 256]
 
         def blender(J, late=True):
-            return nc.vector if J == PAIRS - 1 or (late and J == PAIRS - 2) else nc.gpsimd
+            return nc.vector if J in ON_VECTOR else nc.gpsimd
 
         def sum_on_tensor(J):
             return J < PAIRS - 1
@@ -261,6 +273,14 @@ def tile_grucellstack_pa_kernel(tc, x_in, h0, gh0, w_bytes, w_scale, b_ih0, out)
             if j == 0:
                 live[("biased", m)] = ep.tile([P, 512], F32, name="biased_n" if g == GN else "biased", bufs=3)
             c = BLOCK[g] * 12 + 2 * J + j
+            if m in SUMS_ON_VECTOR:
+                if j == 0:
+                    nc.vector.tensor_tensor(
+                        out=live[("biased", m)][:].rearrange("p (j r) -> p j r", j=2),
+                        in0=live[("sums", m)][:].rearrange("p (j r) -> p j r", j=2),
+                        in1=bias_col[:, c:c + 2].unsqueeze(2).to_broadcast([P, 2, B]), op=ALU.add,
+                    )
+                return
             nc.scalar.activation(
                 out=live[("biased", m)][:, j * B:(j + 1) * B], in_=live[("sums", m)][:, j * B:(j + 1) * B],
                 func=ACT.Identity, bias=bias_col[:, c:c + 1], scale=1.0,
@@ -310,7 +330,7 @@ def tile_grucellstack_pa_kernel(tc, x_in, h0, gh0, w_bytes, w_scale, b_ih0, out)
             nc.scalar.activation(out=r[:], in_=src[:], func=ACT.Tanh)
 
         def h_minus_n(J):
-            live[("d", J)] = ep.tile([P, 512], F32, name="d", bufs=2)
+            live[("d", J)] = ep.tile([P, 512], F32, name="d", bufs=3)
             blender(J, False).tensor_tensor(
                 out=by_half(live[("d", J)]), in0=of_pair(h_sb, J), in1=by_half(live[("r", J)]), op=ALU.subtract
             )
@@ -340,54 +360,59 @@ def tile_grucellstack_pa_kernel(tc, x_in, h0, gh0, w_bytes, w_scale, b_ih0, out)
         def base(m):
             return 4 * m
 
-        b_x = 4 * X_AFTER
-
         def after(m):
             return max(base(m), AFTER_HEAD[m]) if m < len(AFTER_HEAD) else base(m)
 
+        def unit_lag(m):
+            if m < len(AFTER_HEAD):
+                return HEAD_LAG
+            return UNIT_LAST.get(m, UNIT_LAG)
+
         for m in range(UNITS):
             b = base(m)
-            lag = LAG_LAST if m >= UNITS - 3 else LAG
             for i in range(PASSES):
                 if m == 0:
-                    at(b + lag["cast"][i], S_CAST, cast, m, i, 1)
+                    at(b + CAST[i], S_CAST, cast, m, i, 1)
                 elif i % 2 == 0:
-                    at(b + lag["cast"][i], S_CAST, cast, m, i, 2)
-                at(b + lag["run"], T_RUN + i, turn, m, run_of(m)[i])
+                    at(b + CAST[i], S_CAST, cast, m, i, 2)
+                at(b + RUN_LAG[i], T_RUN + i, turn, m, run_of(m)[i])
             if not on_road(m):
                 at(b, V_EVAC - 1, evac, m, ROAD_PASS)
             for g in range(PASSES - 1):
                 at(b + g, V_EVAC, evac, m, g)
             if on_road(m):
                 for t in range(4):
-                    at(b + lag["scaled"], S_SCALED, scaled, m, t)
-                at(b + lag["weave"], G_WEAVE, weave, m)
-            at(b + lag["quant"], V_QUANT, quantise, m)
-            at(b + lag["quant"], V_QUANT + 2, quantise_road, m)
+                    at(b + SCALED, S_SCALED, scaled, m, t)
+                at(b + WEAVE, G_WEAVE, weave, m)
+            at(b + QUANT, V_QUANT, quantise, m)
+            at(b + QUANT, V_QUANT + 2, quantise_road, m)
+            lag = unit_lag(m)
             at(after(m) + lag["passes"], T_PASSES, passes, m, 0)
             at(after(m) + lag["passes"], T_PASSES, passes, m, 1)
-            at(after(m) + lag["sums"], S_SUMS0, sums_out, m, 0)
-            at(after(m) + lag["sums"], S_SUMS1 if after(m) == base(m) else S_SUMS0, sums_out, m, 1)
+            if m in SUMS_ON_VECTOR:
+                at(after(m) + lag["sums"] + SUMS_V, V_QUANT + 1, sums_out, m, 0)
+            else:
+                at(after(m) + lag["sums"], S_SUMS, sums_out, m, 0)
+                at(after(m) + lag["sums"], S_SUMS, sums_out, m, 1)
+            if gate(m) != GN:
+                at(after(m) + lag["back"], T_OPEN, open_with_gh, m)
+                at(after(m) + lag["back"], T_BACK, turn_back, m)
+                at(after(m) + lag["func"], S_FUNC, sigmoid, m)
         at(0, T_RUN, bias_turn)
-        at(1, S_SUMS0, bias_out)
+        at(1, S_SUMS, bias_out)
         for g in range(PASSES):
-            at(b_x + X_TURN, T_RUN + 4 + g, x_turn, g)
-            at(b_x + X_OUT[g], S_SCALED + 1, x_out, g)
-        at(b_x + X_QUANT, V_QUANT + 3, x_quantise)
+            at(X_TURN, T_RUN + 4 + g, x_turn, g)
+            at(X_OUT[g], S_SCALED + 1, x_out, g)
+        at(X_QUANT, V_QUANT + 3, x_quantise)
         for J in range(PAIRS):
-            lag = LAG_LAST if J == PAIRS - 1 else (LAG_4 if J == PAIRS - 2 else LAG)
+            lag = PAIR_LAST.get(J, PAIR_LAG)
             b_r = after(unit(J, GR))
-            for m in (unit(J, GR), unit(J, GZ)):
-                back = lag.get("back_z", lag["back"]) if gate(m) == GZ else lag["back"]
-                at(after(m) + back, T_OPEN, open_with_gh, m)
-                at(after(m) + back, T_BACK, turn_back, m)
-                at(after(m) + back + 1, S_FUNC, sigmoid, m)
-            at(b_r + lag["r_gh"], V_QUANT + 1, r_gh, J)
+            at(b_r + lag["r_gh"], V_QUANT + lag.get("r_gh_place", 1), r_gh, J)
             if sum_on_tensor(J):
                 at(b_r + lag["back_n"], T_OPEN, open_with_r_gh, J)
             at(b_r + lag["back_n"], T_BACK, turn_back, unit(J, GN))
             if not sum_on_tensor(J):
-                at(b_r + lag["back_n"] + 1, V_QUANT + 1, n_sum, J)
+                at(b_r + lag["back_n"] + 1, V_QUANT + 3, n_sum, J)
             at(b_r + lag["tanh"], S_FUNC, tanh, J)
             at(b_r + lag["h_n"], G_BLEND, h_minus_n, J)
             at(b_r + lag["z_d"], G_BLEND, z_times_diff, J)

@@ -24,12 +24,12 @@ ROAD_PASS = PASSES - 1
 
 GN, GR, GZ = 0, 1, 2
 BLOCK = (2, 0, 1)
-ORDER = ((GN, GR, GZ),) * (PAIRS - 1) + ((GR, GN, GZ),)
+SEQ = tuple([(J, g) for J in range(PAIRS - 2) for g in (GN, GR, GZ)]) + tuple([(J, g) for g in (GR, GN, GZ) for J in (PAIRS - 2, PAIRS - 1)])
 
 SUM_BANKS, TURN_BANKS, BACK_BANKS = 2, 4, 2
 NO_ROAD = ()
 RUN = (3, 0, 1, 2)
-RUN_FIRST = (0, 3, 1, 2)
+RUN_FIRST = (3, 0, 1, 2)
 
 V_EVAC, V_QUANT = 10, 12
 S_SUMS, S_CAST, S_FUNC, S_SCALED = 20, 22, 24, 26
@@ -38,19 +38,18 @@ G_WEAVE, G_BLEND = 50, 52
 
 CAST, RUN_LAG, SCALED, WEAVE, QUANT = (-4, -4, -4, -4), (-3, -3, -1, -1), -2, 0, 3
 UNIT_LAG = {"passes": 4, "sums": 9, "back": 14, "func": 18}
-UNIT_LAST = {13: {"passes": 4, "sums": 9, "back": 14, "func": 15}, 14: {"passes": 4, "sums": 9, "back": 11, "func": 12},
-             15: {"passes": 4, "sums": 7, "back": 9, "func": 10}, 16: {"passes": 4, "sums": 6},
-             17: {"passes": 4, "sums": 5, "back": 6, "func": 7}}
+UNIT_LAST = {16: {"passes": 4, "sums": 6, "back": 7, "func": 8}, 17: {"passes": 4, "sums": 5, "back": 6, "func": 7}}
 PAIR_LAG = {"r_gh": 19, "back_n": 22, "tanh": 26, "h_n": 29, "z_d": 33, "out": 37}
-PAIR_LAST = {3: {"r_gh": 19, "back_n": 22, "tanh": 26, "h_n": 29, "z_d": 33, "out": 34},
-             4: {"r_gh": 17, "back_n": 18, "tanh": 19, "h_n": 20, "z_d": 20, "out": 21},
-             5: {"r_gh": 11, "back_n": 11, "tanh": 13, "h_n": 14, "z_d": 16, "out": 17}}
+PAIR_LAST = {3: {"r_gh": 19, "back_n": 22, "tanh": 26, "h_n": 29, "z_d": 32, "out": 33},
+             4: {"r_gh": 19, "back_n": 22, "tanh": 23, "h_n": 24, "z_d": 26, "out": 26},
+             5: {"r_gh": 19, "r_gh_place": 3, "back_n": 20, "tanh": 21, "h_n": 22, "z_d": 24, "out": 25}}
 ON_VECTOR = (4, 5)
+STEPS_ON_VECTOR = ((3, "z_d"), (3, "out"))
 SUMS_ON_VECTOR = (4, 7, 10, 13)
 SUMS_V = -2
 CAST_BUFS = 3
 HEAD_ON_VECTOR = (1, 3)
-X_TURN, X_OUT, X_QUANT = 2, (7, 7, 7, 7), 11
+X_TURN, X_OUT, X_QUANT = 5, (7, 7, 7, 7), 11
 AFTER_HEAD = (8, 8, 12, 12)
 HEAD_LAG = {"passes": 4, "sums": 5, "back": 10, "func": 14}
 
@@ -66,10 +65,13 @@ def tile_grucellstack_pa_kernel(tc, x_in, h0, gh0, w_bytes, w_scale, b_ih0, out)
         ctx.enter_context(tc.manual_schedule())
 
         def gate(m):
-            return ORDER[m // 3][m % 3]
+            return SEQ[m][1]
+
+        def pair(m):
+            return SEQ[m][0]
 
         def unit(J, g):
-            return 3 * J + ORDER[J].index(g)
+            return SEQ.index((J, g))
 
         def on_road(m):
             return m not in NO_ROAD
@@ -96,7 +98,7 @@ def tile_grucellstack_pa_kernel(tc, x_in, h0, gh0, w_bytes, w_scale, b_ih0, out)
             return RUN_FIRST if m == 0 else RUN
 
         def load_pass(m, g):
-            nc.sync.dma_start(out=w_b[m][:, run_of(m).index(g), :, :], in_=w_view[:, BLOCK[gate(m)], m // 3, :, g, :])
+            nc.sync.dma_start(out=w_b[m][:, run_of(m).index(g), :, :], in_=w_view[:, BLOCK[gate(m)], pair(m), :, g, :])
 
         def load_unit(m):
             for g in RUN:
@@ -150,7 +152,7 @@ def tile_grucellstack_pa_kernel(tc, x_in, h0, gh0, w_bytes, w_scale, b_ih0, out)
                 live[("cast", m)] = work.tile([P, 2 * IN], BF16, name="cast", bufs=CAST_BUFS)
             dst = live[("cast", m)][:, i * 1024:(i + n) * 1024]
             src = w_b[m][:, i:i + n, :, :].rearrange("p g q k -> p (g q k)").bitcast(FP8)
-            if m == 0 and i in HEAD_ON_VECTOR:
+            if m * 4 + i in HEAD_ON_VECTOR:
                 nc.vector.tensor_copy(out=dst, in_=src)
             else:
                 nc.scalar.copy(out=dst, in_=src)
@@ -262,14 +264,14 @@ def tile_grucellstack_pa_kernel(tc, x_in, h0, gh0, w_bytes, w_scale, b_ih0, out)
         def of_pair(t, J):
             return t[:, :, J * 256:(J + 1) * 256]
 
-        def blender(J, late=True):
-            return nc.vector if J in ON_VECTOR else nc.gpsimd
+        def blender(J, step):
+            return nc.vector if J in ON_VECTOR or (J, step) in STEPS_ON_VECTOR else nc.gpsimd
 
         def sum_on_tensor(J):
-            return J < PAIRS - 1
+            return True
 
         def sums_out(m, j):
-            J, g = m // 3, gate(m)
+            J, g = pair(m), gate(m)
             if j == 0:
                 live[("biased", m)] = ep.tile([P, 512], F32, name="biased_n" if g == GN else "biased", bufs=3)
             c = BLOCK[g] * 12 + 2 * J + j
@@ -289,7 +291,7 @@ def tile_grucellstack_pa_kernel(tc, x_in, h0, gh0, w_bytes, w_scale, b_ih0, out)
         def open_with_gh(m):
             live[("back", m)] = back_bank()
             nc.tensor.matmul(
-                out=by_half(live[("back", m)]), lhsT=ident_b[:], rhs=of_pair(gh_sb[BLOCK[gate(m)]], m // 3),
+                out=by_half(live[("back", m)]), lhsT=ident_b[:], rhs=of_pair(gh_sb[BLOCK[gate(m)]], pair(m)),
                 start=True, stop=False,
             )
 
@@ -300,7 +302,7 @@ def tile_grucellstack_pa_kernel(tc, x_in, h0, gh0, w_bytes, w_scale, b_ih0, out)
             )
 
         def turn_back(m):
-            alone = gate(m) == GN and not sum_on_tensor(m // 3)
+            alone = gate(m) == GN and not sum_on_tensor(pair(m))
             if alone:
                 live[("back", m)] = back_bank()
             for h in range(2):
@@ -313,8 +315,8 @@ def tile_grucellstack_pa_kernel(tc, x_in, h0, gh0, w_bytes, w_scale, b_ih0, out)
 
         def sigmoid(m):
             name = "r" if gate(m) == GR else "z"
-            live[(name, m // 3)] = ep.tile([P, 512], F32, name=name, bufs=3)
-            nc.scalar.activation(out=live[(name, m // 3)][:], in_=live[("back", m)][:], func=ACT.Sigmoid)
+            live[(name, pair(m))] = ep.tile([P, 512], F32, name=name, bufs=3)
+            nc.scalar.activation(out=live[(name, pair(m))][:], in_=live[("back", m)][:], func=ACT.Sigmoid)
 
         def r_gh(J):
             r = live[("r", J)]
@@ -331,20 +333,20 @@ def tile_grucellstack_pa_kernel(tc, x_in, h0, gh0, w_bytes, w_scale, b_ih0, out)
 
         def h_minus_n(J):
             live[("d", J)] = ep.tile([P, 512], F32, name="d", bufs=3)
-            blender(J, False).tensor_tensor(
+            blender(J, "h_n").tensor_tensor(
                 out=by_half(live[("d", J)]), in0=of_pair(h_sb, J), in1=by_half(live[("r", J)]), op=ALU.subtract
             )
 
         def z_times_diff(J):
             d = live[("d", J)]
-            blender(J).tensor_tensor(out=d[:], in0=d[:], in1=live[("z", J)][:], op=ALU.mult)
+            blender(J, "z_d").tensor_tensor(out=d[:], in0=d[:], in1=live[("z", J)][:], op=ALU.mult)
 
         out_view = out.rearrange("(h p) c -> p h c", p=P)
 
         def result(J):
             d = live[("d", J)]
             if J < PAIRS - 1:
-                blender(J).tensor_tensor(out=d[:], in0=d[:], in1=live[("r", J)][:], op=ALU.add)
+                blender(J, "out").tensor_tensor(out=d[:], in0=d[:], in1=live[("r", J)][:], op=ALU.add)
                 nc.sync.dma_start(out=of_pair(out_view, J), in_=by_half(d))
             else:
                 for h in range(2):

@@ -169,16 +169,16 @@ def tile_grucellstack_pa_kernel(tc, x_in, h0, gh0, w_bytes, w_scale, b_ih0, out)
 
         def main_of(m):
             if ("main", m) not in live:
-                live[("main", m)] = work.tile([P, 3 * 1024], BF16, name="main", bufs=2, align_bytes=64)
+                live[("main", m)] = work.tile([P, 2 * 1024], BF16, name="main", bufs=2, align_bytes=64)
             return live[("main", m)]
 
         def woven_of(m):
             if ("woven", m) not in live:
-                live[("woven", m)] = work.tile([P, 1024], BF16, name="woven", bufs=1, align_bytes=64)
+                live[("woven", m)] = work.tile([P, 2 * 1024], BF16, name="woven", bufs=1, align_bytes=64)
             return live[("woven", m)]
 
         def evac(m, g):
-            dst = woven_of(m)[:] if g == ROAD_PASS else main_of(m)[:, g * 1024:(g + 1) * 1024]
+            dst = main_of(m)[:, g * 1024:(g + 1) * 1024] if g < 2 else woven_of(m)[:, (g - 2) * 1024:(g - 1) * 1024]
             nc.vector.tensor_tensor(
                 out=dst.rearrange("p (a u e) -> p a u e", u=2, e=2),
                 in0=live[("bank", m, g)][:].bitcast(BF16).rearrange("p (u a e) -> p a u e", u=2, e=2),
@@ -198,7 +198,7 @@ def tile_grucellstack_pa_kernel(tc, x_in, h0, gh0, w_bytes, w_scale, b_ih0, out)
 
         def weave(m):
             nc.gpsimd.tensor_scalar(
-                out=woven_of(m)[:].rearrange("p (a t) -> p a t", t=4),
+                out=woven_of(m)[:, 1024:2048].rearrange("p (a t) -> p a t", t=4),
                 in0=live[("planes", m)][:].rearrange("p (t a) -> p a t", t=4),
                 scalar1=1.0, scalar2=0.0, op0=ALU.mult, op1=ALU.add,
             )
@@ -207,12 +207,11 @@ def tile_grucellstack_pa_kernel(tc, x_in, h0, gh0, w_bytes, w_scale, b_ih0, out)
             live[("codes", m)] = work.tile([P, 1024], U32, name="codes", bufs=3, align_bytes=64)
             live[("scales", m)] = work.tile([P, 1024], U8, name="scales", bufs=3, align_bytes=64)
             codes, scales = live[("codes", m)], live[("scales", m)]
-            for src, first, last in ((main_of(m)[:, 0:2048], 0, 512), (main_of(m)[:, 2048:3072], 512, 768)):
-                nc.vector.quantize_mx(out=codes[:, first:last].bitcast(FP8X4), scales=scales[:, first:last], in_=src)
+            nc.vector.quantize_mx(out=codes[:, 0:512].bitcast(FP8X4), scales=scales[:, 0:512], in_=main_of(m)[:])
 
         def quantise_road(m):
             codes, scales = live[("codes", m)], live[("scales", m)]
-            nc.vector.quantize_mx(out=codes[:, 768:1024].bitcast(FP8X4), scales=scales[:, 768:1024], in_=woven_of(m)[:])
+            nc.vector.quantize_mx(out=codes[:, 512:1024].bitcast(FP8X4), scales=scales[:, 512:1024], in_=woven_of(m)[:])
 
         def passes(m, j):
             if j == 0:

@@ -116,9 +116,9 @@ def tile_grucellstack_pa_kernel(tc, x_in, h0, gh0, w_bytes, w_scale, b_ih0, out)
             load_pass(0, g)
         nc.sync.dma_start(out=b_rows[0:36, :], in_=b_ih0.rearrange("(c p) -> c p", p=P))
         load_unit(1)
+        load_unit(2)
         nc.sync.dma_start(out=x_sb[:, 0, :], in_=x_view[:, 0, :])
         nc.sync.dma_start(out=x_sb[:, 1, :], in_=x_view[:, 1, :])
-        load_unit(2)
         load_unit(3)
         load_gh(BLOCK[GR])
         load_unit(4)

@@ -45,9 +45,10 @@ PAIR_LAST = {3: {"r_gh": 19, "back_n": 22, "tanh": 26, "h_n": 29, "z_d": 32, "ou
              5: {"r_gh": 19, "r_gh_place": 3, "back_n": 20, "tanh": 21, "h_n": 22, "z_d": 24, "out": 25}}
 ON_VECTOR = (4, 5)
 STEPS_ON_VECTOR = ((3, "z_d"), (3, "out"))
-SUMS_ON_VECTOR = (4, 7, 10, 13)
+SUMS_ON_VECTOR = ()
 SUMS_V = -2
 CAST_BUFS = 3
+PLAIN_ROAD = (1, 4, 7, 10, 13)
 HEAD_ON_VECTOR = (1, 3)
 X_TURN, X_OUT, X_QUANT = 5, (7, 7, 7, 7), 11
 AFTER_HEAD = (8, 8, 12, 12)
@@ -189,6 +190,13 @@ def tile_grucellstack_pa_kernel(tc, x_in, h0, gh0, w_bytes, w_scale, b_ih0, out)
         def scaled(m, t):
             if t == 0:
                 live[("planes", m)] = work.tile([P, 1024], BF16, name="planes", bufs=2)
+            if m in PLAIN_ROAD:
+                if t == 0:
+                    nc.scalar.copy(
+                        out=live[("planes", m)][:].bitcast(F32).rearrange("p (a u) -> p a u", u=2),
+                        in_=live[("bank", m, ROAD_PASS)][:].rearrange("p (u a) -> p a u", u=2),
+                    )
+                return
             halves = live[("bank", m, ROAD_PASS)][:].bitcast(BF16)
             u, e = t // 2, t % 2
             nc.scalar.activation(
@@ -197,6 +205,13 @@ def tile_grucellstack_pa_kernel(tc, x_in, h0, gh0, w_bytes, w_scale, b_ih0, out)
             )
 
         def weave(m):
+            if m in PLAIN_ROAD:
+                nc.gpsimd.tensor_tensor(
+                    out=woven_of(m)[:, 1024:2048].rearrange("p (a t) -> p a t", t=4),
+                    in0=live[("planes", m)][:].rearrange("p (a t) -> p a t", t=4),
+                    in1=scales_col[:, ROAD_PASS, :].unsqueeze(1).to_broadcast([P, 256, 4]), op=ALU.mult,
+                )
+                return
             nc.gpsimd.tensor_scalar(
                 out=woven_of(m)[:, 1024:2048].rearrange("p (a t) -> p a t", t=4),
                 in0=live[("planes", m)][:].rearrange("p (t a) -> p a t", t=4),

@@ -40,7 +40,7 @@ CAST, RUN_LAG, SCALED, WEAVE, QUANT = (-4, -4, -4, -4), (-3, -3, -1, -1), -2, 0,
 UNIT_LAG = {"passes": 4, "sums": 9, "back": 14, "func": 18}
 UNIT_LAST = {16: {"passes": 4, "sums": 6, "back": 7, "func": 8}, 17: {"passes": 4, "sums": 5, "back": 6, "func": 7}}
 PAIR_LAG = {"r_gh": 19, "back_n": 22, "tanh": 26, "h_n": 29, "z_d": 33, "out": 37}
-PAIR_LAST = {3: {"r_gh": 19, "back_n": 22, "tanh": 26, "h_n": 29, "z_d": 32, "out": 33},
+PAIR_LAST = {0: {"r_gh": 15, "back_n": 18, "tanh": 22, "h_n": 25, "z_d": 29, "out": 33}, 3: {"r_gh": 19, "back_n": 22, "tanh": 26, "h_n": 29, "z_d": 32, "out": 33},
              4: {"r_gh": 19, "back_n": 22, "tanh": 23, "h_n": 24, "z_d": 26, "out": 26},
              5: {"r_gh": 19, "r_gh_place": 3, "back_n": 20, "tanh": 21, "h_n": 22, "z_d": 24, "out": 25}}
 ON_VECTOR = (4, 5)

@@ -37,7 +37,7 @@ T_PASSES, T_RUN, T_OPEN, T_BACK = 30, 32, 36, 37
 G_WEAVE, G_BLEND = 50, 52
 
 CAST, RUN_LAG, SCALED, WEAVE, QUANT = (-4, -4, -4, -4), (-3, -3, -1, -1), -2, 0, 3
-UNIT_LAG = {"passes": 4, "sums": 9, "back": 14, "func": 18}
+UNIT_LAG = {"passes": 8, "sums": 10, "back": 14, "func": 18}
 UNIT_LAST = {16: {"passes": 4, "sums": 6, "back": 7, "func": 8}, 17: {"passes": 4, "sums": 5, "back": 6, "func": 7}}
 PAIR_LAG = {"r_gh": 19, "back_n": 22, "tanh": 26, "h_n": 29, "z_d": 33, "out": 37}
 PAIR_LAST = {0: {"r_gh": 15, "back_n": 18, "tanh": 22, "h_n": 25, "z_d": 29, "out": 33}, 3: {"r_gh": 19, "back_n": 22, "tanh": 26, "h_n": 29, "z_d": 32, "out": 33},
@@ -51,7 +51,7 @@ CAST_BUFS = 3
 PLAIN_ROAD = (1, 4, 7, 10, 13)
 HEAD_ON_VECTOR = (1, 3)
 X_TURN, X_OUT, X_QUANT = 5, (7, 7, 7, 7), 11
-AFTER_HEAD = (8, 8, 12, 12)
+AFTER_HEAD = (8, 8, 12, 16)
 HEAD_LAG = {"passes": 4, "sums": 5, "back": 10, "func": 14}
 
 
@@ -64,6 +64,9 @@ def tile_grucellstack_pa_kernel(tc, x_in, h0, gh0, w_bytes, w_scale, b_ih0, out)
         ep = ctx.enter_context(tc.tile_pool(name="ep", bufs=2))
         psum = ctx.enter_context(tc.psum_pool(name="psum", bufs=1))
         ctx.enter_context(tc.manual_schedule())
+
+        def span_place(m, g):
+            return (m, 2048 + g * 1024) if g < 2 else (m + 1, (g - 2) * 1024)
 
         def gate(m):
             return SEQ[m][1]
@@ -168,18 +171,14 @@ def tile_grucellstack_pa_kernel(tc, x_in, h0, gh0, w_bytes, w_scale, b_ih0, out)
                     first = run_of(m).index(g) * 512 + q * 256
                     nc.tensor.transpose(bank[:, col:col + P], words[:, first + u:first + 256:2], ident_f[:])
 
-        def main_of(m):
-            if ("main", m) not in live:
-                live[("main", m)] = work.tile([P, 2 * 1024], BF16, name="main", bufs=2, align_bytes=64)
-            return live[("main", m)]
-
-        def woven_of(m):
-            if ("woven", m) not in live:
-                live[("woven", m)] = work.tile([P, 2 * 1024], BF16, name="woven", bufs=1, align_bytes=64)
-            return live[("woven", m)]
+        def grouped(m, g):
+            k, first = span_place(m, g)
+            if ("span", k) not in live:
+                live[("span", k)] = work.tile([P, PASSES * 1024], BF16, name="span", bufs=2, align_bytes=64)
+            return live[("span", k)][:, first:first + 1024]
 
         def evac(m, g):
-            dst = main_of(m)[:, g * 1024:(g + 1) * 1024] if g < 2 else woven_of(m)[:, (g - 2) * 1024:(g - 1) * 1024]
+            dst = grouped(m, g)
             nc.vector.tensor_tensor(
                 out=dst.rearrange("p (a u e) -> p a u e", u=2, e=2),
                 in0=live[("bank", m, g)][:].bitcast(BF16).rearrange("p (u a e) -> p a u e", u=2, e=2),
@@ -207,40 +206,40 @@ def tile_grucellstack_pa_kernel(tc, x_in, h0, gh0, w_bytes, w_scale, b_ih0, out)
         def weave(m):
             if m in PLAIN_ROAD:
                 nc.gpsimd.tensor_tensor(
-                    out=woven_of(m)[:, 1024:2048].rearrange("p (a t) -> p a t", t=4),
+                    out=grouped(m, ROAD_PASS).rearrange("p (a t) -> p a t", t=4),
                     in0=live[("planes", m)][:].rearrange("p (a t) -> p a t", t=4),
                     in1=scales_col[:, ROAD_PASS, :].unsqueeze(1).to_broadcast([P, 256, 4]), op=ALU.mult,
                 )
                 return
             nc.gpsimd.tensor_scalar(
-                out=woven_of(m)[:, 1024:2048].rearrange("p (a t) -> p a t", t=4),
+                out=grouped(m, ROAD_PASS).rearrange("p (a t) -> p a t", t=4),
                 in0=live[("planes", m)][:].rearrange("p (t a) -> p a t", t=4),
                 scalar1=1.0, scalar2=0.0, op0=ALU.mult, op1=ALU.add,
             )
 
-        def quantise(m):
-            live[("codes", m)] = work.tile([P, 1024], U32, name="codes", bufs=3, align_bytes=64)
-            live[("scales", m)] = work.tile([P, 1024], U8, name="scales", bufs=3, align_bytes=64)
-            codes, scales = live[("codes", m)], live[("scales", m)]
-            nc.vector.quantize_mx(out=codes[:, 0:512].bitcast(FP8X4), scales=scales[:, 0:512], in_=main_of(m)[:])
-
-        def quantise_road(m):
-            codes, scales = live[("codes", m)], live[("scales", m)]
-            nc.vector.quantize_mx(out=codes[:, 512:1024].bitcast(FP8X4), scales=scales[:, 512:1024], in_=woven_of(m)[:])
+        def quantise(k, halves):
+            if ("codes", k) not in live:
+                live[("codes", k)] = work.tile([P, 1024], U32, name="codes", bufs=3, align_bytes=64)
+                live[("scales", k)] = work.tile([P, 1024], U8, name="scales", bufs=3, align_bytes=64)
+            cols = slice(halves[0] * 512, (halves[-1] + 1) * 512)
+            nc.vector.quantize_mx(
+                out=live[("codes", k)][:, cols].bitcast(FP8X4), scales=live[("scales", k)][:, cols],
+                in_=live[("span", k)][:, 4 * cols.start:4 * cols.stop],
+            )
 
         def passes(m, j):
             if j == 0:
                 live[("sums", m)] = psum.tile([P, 512], F32, name="sums", tag="sums", bufs=SUM_BANKS)
-            order = (0, 1, 2, 3)
-            for g in order:
-                col = g * 256 + j * P
+            for g in range(PASSES):
+                k, first = span_place(m, g)
+                col = first // 4 + j * P
                 nc.tensor.matmul_mx(
                     out=live[("sums", m)][:, j * B:(j + 1) * B],
-                    lhsT=live[("codes", m)][:, col:col + P].bitcast(FP8X4),
-                    lhsT_scale=live[("scales", m)][:, col:col + P],
+                    lhsT=live[("codes", k)][:, col:col + P].bitcast(FP8X4),
+                    lhsT_scale=live[("scales", k)][:, col:col + P],
                     rhs=x_codes[:, g * B:(g + 1) * B].bitcast(FP8X4),
                     rhs_scale=x_scales[:, g * B:(g + 1) * B],
-                    start=(g == order[0]), stop=(g == order[-1]),
+                    start=(g == 0), stop=(g == PASSES - 1),
                 )
 
         def x_turn(g):
@@ -400,8 +399,12 @@ def tile_grucellstack_pa_kernel(tc, x_in, h0, gh0, w_bytes, w_scale, b_ih0, out)
                 for t in range(4):
                     at(b + SCALED, S_SCALED, scaled, m, t)
                 at(b + WEAVE, G_WEAVE, weave, m)
-            at(b + QUANT, V_QUANT, quantise, m)
-            at(b + QUANT, V_QUANT + 2, quantise_road, m)
+            if m == 0 or m == UNITS - 1:
+                at(b + QUANT, V_QUANT, quantise, m, (1,))
+            else:
+                at(b + QUANT, V_QUANT, quantise, m, (0, 1))
+            if m >= UNITS - 2:
+                at(b + QUANT, V_QUANT + 2, quantise, m + 1, (0,))
             lag = unit_lag(m)
             at(after(m) + lag["passes"], T_PASSES, passes, m, 0)
             at(after(m) + lag["passes"], T_PASSES, passes, m, 1)

@@ -37,14 +37,14 @@ T_PASSES, T_RUN, T_OPEN, T_BACK = 30, 32, 36, 37
 G_WEAVE, G_BLEND = 50, 52
 
 CAST, RUN_LAG, SCALED, WEAVE, QUANT = (-4, -4, -4, -4), (-3, -3, -1, -1), -2, 0, 3
-UNIT_LAG = {"passes": 8, "sums": 10, "back": 14, "func": 18}
+UNIT_LAG = {"passes": 8, "sums": 11, "back": 14, "func": 18}
 UNIT_LAST = {16: {"passes": 4, "sums": 6, "back": 7, "func": 8}, 17: {"passes": 4, "sums": 5, "back": 6, "func": 7}}
 PAIR_LAG = {"r_gh": 19, "back_n": 22, "tanh": 26, "h_n": 29, "z_d": 33, "out": 37}
-PAIR_LAST = {0: {"r_gh": 15, "back_n": 18, "tanh": 22, "h_n": 25, "z_d": 29, "out": 33}, 3: {"r_gh": 19, "back_n": 22, "tanh": 26, "h_n": 29, "z_d": 32, "out": 33},
+PAIR_LAST = {0: {"r_gh": 15, "back_n": 18, "tanh": 22, "h_n": 25, "z_d": 29, "out": 35, "out_place": 15}, 1: {"r_gh": 19, "back_n": 22, "tanh": 26, "h_n": 29, "z_d": 33, "out": 39, "out_place": 15}, 3: {"r_gh": 19, "back_n": 22, "tanh": 26, "h_n": 29, "z_d": 32, "out": 33},
              4: {"r_gh": 19, "back_n": 22, "tanh": 23, "h_n": 24, "z_d": 26, "out": 26},
              5: {"r_gh": 19, "r_gh_place": 3, "back_n": 20, "tanh": 21, "h_n": 22, "z_d": 24, "out": 25}}
 ON_VECTOR = (4, 5)
-STEPS_ON_VECTOR = ((3, "z_d"), (3, "out"))
+STEPS_ON_VECTOR = ((3, "z_d"), (3, "out"), (0, "out"), (1, "out"))
 SUMS_ON_VECTOR = ()
 SUMS_V = -2
 CAST_BUFS = 3
@@ -435,6 +435,6 @@ def tile_grucellstack_pa_kernel(tc, x_in, h0, gh0, w_bytes, w_scale, b_ih0, out)
             at(b_r + lag["tanh"], S_FUNC, tanh, J)
             at(b_r + lag["h_n"], G_BLEND, h_minus_n, J)
             at(b_r + lag["z_d"], G_BLEND, z_times_diff, J)
-            at(b_r + lag["out"], G_BLEND, result, J)
+            at(b_r + lag["out"], lag.get("out_place", G_BLEND), result, J)
         for step in sorted(steps, key=lambda e: e[0:3]):
             step[3](*step[4])

@@ -271,6 +271,9 @@ def tile_grucellstack_pa_kernel(tc, x_in, h0, gh0, w_bytes, w_scale, b_ih0, out)
         def bias_out():
             nc.scalar.copy(out=bias_col[:], in_=live["bias_bank"][:, 0:36])
 
+        whole = (slice(0, 512),)
+        pair_halves = (slice(0, 256), slice(256, 512))
+
         def by_half(t):
             return t[:].rearrange("p (h c) -> p h c", h=2)
 
@@ -301,8 +304,13 @@ def tile_grucellstack_pa_kernel(tc, x_in, h0, gh0, w_bytes, w_scale, b_ih0, out)
                 func=ACT.Identity, bias=bias_col[:, c:c + 1], scale=1.0,
             )
 
+        def by_tokens(J):
+            return pair_halves if J == PAIRS - 1 else whole
+
         def open_with_gh(m):
             live[("back", m)] = back_bank()
+            if pair(m) == PAIRS - 1:
+                return
             nc.tensor.matmul(
                 out=by_half(live[("back", m)]), lhsT=ident_b[:], rhs=of_pair(gh_sb[BLOCK[gate(m)]], pair(m)),
                 start=True, stop=False,
@@ -310,6 +318,8 @@ def tile_grucellstack_pa_kernel(tc, x_in, h0, gh0, w_bytes, w_scale, b_ih0, out)
 
         def open_with_r_gh(J):
             live[("back", unit(J, GN))] = back_bank()
+            if J == PAIRS - 1:
+                return
             nc.tensor.matmul(
                 out=live[("back", unit(J, GN))][:], lhsT=ident_f[:], rhs=live[("r", J)][:], start=True, stop=False
             )
@@ -318,21 +328,38 @@ def tile_grucellstack_pa_kernel(tc, x_in, h0, gh0, w_bytes, w_scale, b_ih0, out)
             alone = gate(m) == GN and not sum_on_tensor(pair(m))
             if alone:
                 live[("back", m)] = back_bank()
+            halved = pair(m) == PAIRS - 1
             for h in range(2):
+                if halved and gate(m) == GN:
+                    nc.tensor.matmul(
+                        out=live[("back", m)][:, h * 256:(h + 1) * 256], lhsT=ident_f[:],
+                        rhs=live[("r", pair(m))][:, h * 256:(h + 1) * 256], start=True, stop=False,
+                    )
+                elif halved:
+                    nc.tensor.matmul(
+                        out=live[("back", m)][:, h * 256:(h + 1) * 256], lhsT=ident_b[:],
+                        rhs=of_pair(gh_sb[BLOCK[gate(m)]], pair(m))[:, h, :], start=True, stop=False,
+                    )
                 for j in range(2):
                     nc.tensor.matmul(
                         out=live[("back", m)][:, h * 256 + j * P:h * 256 + (j + 1) * P],
                         lhsT=live[("biased", m)][:, j * 256 + h * P:j * 256 + (h + 1) * P], rhs=ident_f[:],
-                        is_transpose=True, start=alone, stop=(alone or (h == 1 and j == 1)),
+                        is_transpose=True, start=alone, stop=(alone or (j == 1 and (h == 1 or halved))),
                     )
 
         def sigmoid(m):
             name = "r" if gate(m) == GR else "z"
             live[(name, pair(m))] = ep.tile([P, 512], F32, name=name, bufs=3)
-            nc.scalar.activation(out=live[(name, pair(m))][:], in_=live[("back", m)][:], func=ACT.Sigmoid)
+            for cols in by_tokens(pair(m)):
+                nc.scalar.activation(out=live[(name, pair(m))][:, cols], in_=live[("back", m)][:, cols], func=ACT.Sigmoid)
 
         def r_gh(J):
             r = live[("r", J)]
+            if J == PAIRS - 1:
+                for h in range(2):
+                    cols = pair_halves[h]
+                    nc.vector.tensor_tensor(out=r[:, cols], in0=r[:, cols], in1=of_pair(gh_sb[BLOCK[GN]], J)[:, h, :], op=ALU.mult)
+                return
             nc.vector.tensor_tensor(out=by_half(r), in0=by_half(r), in1=of_pair(gh_sb[BLOCK[GN]], J), op=ALU.mult)
 
         def n_sum(J):
@@ -342,17 +369,24 @@ def tile_grucellstack_pa_kernel(tc, x_in, h0, gh0, w_bytes, w_scale, b_ih0, out)
         def tanh(J):
             r = live[("r", J)]
             src = live[("back", unit(J, GN))] if sum_on_tensor(J) else r
-            nc.scalar.activation(out=r[:], in_=src[:], func=ACT.Tanh)
+            for cols in by_tokens(J):
+                nc.scalar.activation(out=r[:, cols], in_=src[:, cols], func=ACT.Tanh)
 
         def h_minus_n(J):
             live[("d", J)] = ep.tile([P, 512], F32, name="d", bufs=3)
+            if J == PAIRS - 1:
+                for h in range(2):
+                    cols = pair_halves[h]
+                    nc.vector.tensor_tensor(out=live[("d", J)][:, cols], in0=of_pair(h_sb, J)[:, h, :], in1=live[("r", J)][:, cols], op=ALU.subtract)
+                return
             blender(J, "h_n").tensor_tensor(
                 out=by_half(live[("d", J)]), in0=of_pair(h_sb, J), in1=by_half(live[("r", J)]), op=ALU.subtract
             )
 
         def z_times_diff(J):
             d = live[("d", J)]
-            blender(J, "z_d").tensor_tensor(out=d[:], in0=d[:], in1=live[("z", J)][:], op=ALU.mult)
+            for cols in by_tokens(J):
+                blender(J, "z_d").tensor_tensor(out=d[:, cols], in0=d[:, cols], in1=live[("z", J)][:, cols], op=ALU.mult)
 
         out_view = out.rearrange("(h p) c -> p h c", p=P)
 

@@ -40,15 +40,15 @@ CAST, RUN_LAG, SCALED, WEAVE, QUANT = (-4, -4, -4, -4), (-3, -3, -1, -1), -2, 0,
 UNIT_LAG = {"passes": 8, "sums": 11, "back": 14, "func": 18}
 UNIT_LAST = {16: {"passes": 4, "sums": 6, "back": 7, "func": 8}, 17: {"passes": 4, "sums": 5, "back": 6, "func": 7}}
 PAIR_LAG = {"r_gh": 19, "back_n": 22, "tanh": 26, "h_n": 29, "z_d": 33, "out": 37}
-PAIR_LAST = {0: {"r_gh": 15, "back_n": 18, "tanh": 22, "h_n": 25, "z_d": 29, "out": 35, "out_place": 15}, 1: {"r_gh": 19, "back_n": 22, "tanh": 26, "h_n": 29, "z_d": 33, "out": 39, "out_place": 15}, 3: {"r_gh": 19, "back_n": 22, "tanh": 26, "h_n": 29, "z_d": 32, "out": 33},
+PAIR_LAST = {0: {"r_gh": 15, "back_n": 18, "tanh": 22, "h_n": 25, "z_d": 29, "out": 33}, 3: {"r_gh": 19, "back_n": 22, "tanh": 26, "h_n": 29, "z_d": 32, "out": 33},
              4: {"r_gh": 19, "back_n": 22, "tanh": 23, "h_n": 24, "z_d": 26, "out": 26},
              5: {"r_gh": 19, "r_gh_place": 3, "back_n": 20, "tanh": 21, "h_n": 22, "z_d": 24, "out": 25}}
 ON_VECTOR = (4, 5)
-STEPS_ON_VECTOR = ((3, "z_d"), (3, "out"), (0, "out"), (1, "out"))
+STEPS_ON_VECTOR = ((3, "z_d"), (3, "out"))
 SUMS_ON_VECTOR = ()
 SUMS_V = -2
 CAST_BUFS = 3
-PLAIN_ROAD = (1, 4, 7, 10, 13)
+PLAIN_ROAD = (1, 4, 7)
 HEAD_ON_VECTOR = (1, 3)
 X_TURN, X_OUT, X_QUANT = 5, (7, 7, 7, 7), 11
 AFTER_HEAD = (8, 8, 12, 16)

@@ -48,7 +48,7 @@ STEPS_ON_VECTOR = ((3, "z_d"), (3, "out"))
 SUMS_ON_VECTOR = ()
 SUMS_V = -2
 CAST_BUFS = 3
-PLAIN_ROAD = (1, 4, 7)
+PLAIN_ROAD = ()
 HEAD_ON_VECTOR = (1, 3)
 X_TURN, X_OUT, X_QUANT = 5, (7, 7, 7, 7), 11
 AFTER_HEAD = (8, 8, 12, 16)

@@ -39,18 +39,18 @@ G_WEAVE, G_BLEND = 50, 52
 CAST, RUN_LAG, SCALED, WEAVE, QUANT = (-4, -4, -4, -4), (-3, -3, -1, -1), -2, 0, 3
 UNIT_LAG = {"passes": 8, "sums": 11, "back": 14, "func": 18}
 UNIT_LAST = {16: {"passes": 4, "sums": 6, "back": 7, "func": 8}, 17: {"passes": 4, "sums": 5, "back": 6, "func": 7}}
-PAIR_LAG = {"r_gh": 19, "back_n": 22, "tanh": 26, "h_n": 29, "z_d": 33, "out": 37}
-PAIR_LAST = {0: {"r_gh": 15, "back_n": 18, "tanh": 22, "h_n": 25, "z_d": 29, "out": 33}, 3: {"r_gh": 19, "back_n": 22, "tanh": 26, "h_n": 29, "z_d": 32, "out": 33},
+PAIR_LAG = {"r_gh": 19, "back_n": 21, "tanh": 23, "h_n": 25, "z_d": 29, "out": 33}
+PAIR_LAST = {0: {"r_gh": 15, "back_n": 17, "tanh": 19, "h_n": 21, "z_d": 25, "out": 29}, 3: {"r_gh": 19, "back_n": 21, "tanh": 23, "h_n": 25, "z_d": 29, "out": 33},
              4: {"r_gh": 19, "back_n": 22, "tanh": 23, "h_n": 24, "z_d": 26, "out": 26},
              5: {"r_gh": 19, "r_gh_place": 3, "back_n": 20, "tanh": 21, "h_n": 22, "z_d": 24, "out": 25}}
 ON_VECTOR = (4, 5)
-STEPS_ON_VECTOR = ((3, "z_d"), (3, "out"))
+STEPS_ON_VECTOR = ((3, "out"),)
 SUMS_ON_VECTOR = ()
 SUMS_V = -2
 CAST_BUFS = 3
-PLAIN_ROAD = ()
+PLAIN_ROAD = (6,)
 HEAD_ON_VECTOR = (1, 3)
-X_TURN, X_OUT, X_QUANT = 5, (7, 7, 7, 7), 11
+X_TURN, X_OUT, X_QUANT = 5, (7, 7, 7, 7), 10
 AFTER_HEAD = (8, 8, 12, 16)
 HEAD_LAG = {"passes": 4, "sums": 5, "back": 10, "func": 14}
 

@@ -29,7 +29,8 @@ SEQ = tuple([(J, g) for J in range(PAIRS - 2) for g in (GN, GR, GZ)]) + tuple([(
 SUM_BANKS, TURN_BANKS, BACK_BANKS = 2, 4, 2
 NO_ROAD = ()
 RUN = (3, 0, 1, 2)
-RUN_FIRST = (3, 0, 1, 2)
+RUN_FIRST = (0, 1, 2, 3)
+SCALED_FIRST = 1
 
 V_EVAC, V_QUANT = 10, 12
 S_SUMS, S_CAST, S_FUNC, S_SCALED = 20, 22, 24, 26
@@ -431,8 +432,8 @@ def tile_grucellstack_pa_kernel(tc, x_in, h0, gh0, w_bytes, w_scale, b_ih0, out)
                 at(b + g, V_EVAC, evac, m, g)
             if on_road(m):
                 for t in range(4):
-                    at(b + SCALED, S_SCALED, scaled, m, t)
-                at(b + WEAVE, G_WEAVE, weave, m)
+                    at(SCALED_FIRST if m == 0 else b + SCALED, S_SCALED, scaled, m, t)
+                at(SCALED_FIRST if m == 0 else b + WEAVE, G_WEAVE, weave, m)
             if m == 0 or m == UNITS - 1:
                 at(b + QUANT, V_QUANT, quantise, m, (1,))
             else:

@@ -51,7 +51,7 @@ SUMS_V = -2
 CAST_BUFS = 3
 PLAIN_ROAD = (6,)
 HEAD_ON_VECTOR = (1, 3)
-X_TURN, X_OUT, X_QUANT = 5, (7, 7, 7, 7), 10
+X_TURN, X_OUT, X_QUANT = (3, 3, 5, 5), (5, 5, 7, 7), 10
 AFTER_HEAD = (8, 8, 12, 16)
 HEAD_LAG = {"passes": 4, "sums": 5, "back": 10, "func": 14}
 
@@ -86,7 +86,7 @@ def tile_grucellstack_pa_kernel(tc, x_in, h0, gh0, w_bytes, w_scale, b_ih0, out)
         for m in range(UNITS):
             w_b[m] = wpool.tile([P, PASSES, 2, K_PASS], U8, name="w_b_%d" % m)
         scales_col = const.tile([P, PASSES, 4], F32, name="scales_col")
-        x_sb = const.tile([P, 2, IN], BF16, name="x_sb")
+        x_sb = const.tile([P, PASSES, 2, K_PASS], BF16, name="x_sb")
         h_sb = const.tile([P, 2, L], BF16, name="h_sb")
         gh_sb = {}
         for blk in range(3):
@@ -122,8 +122,8 @@ def tile_grucellstack_pa_kernel(tc, x_in, h0, gh0, w_bytes, w_scale, b_ih0, out)
         nc.sync.dma_start(out=b_rows[0:36, :], in_=b_ih0.rearrange("(c p) -> c p", p=P))
         load_unit(1)
         load_unit(2)
-        nc.sync.dma_start(out=x_sb[:, 0, :], in_=x_view[:, 0, :])
-        nc.sync.dma_start(out=x_sb[:, 1, :], in_=x_view[:, 1, :])
+        for g in range(PASSES):
+            nc.sync.dma_start(out=x_sb[:, g, :, :], in_=x_view[:, :, g * K_PASS:(g + 1) * K_PASS])
         load_unit(3)
         load_gh(BLOCK[GR])
         load_unit(4)
@@ -253,7 +253,7 @@ def tile_grucellstack_pa_kernel(tc, x_in, h0, gh0, w_bytes, w_scale, b_ih0, out)
                 for h in range(2):
                     col = (u * 2 + h) * P
                     nc.tensor.transpose(
-                        bank[:, col:col + P], x_sb[:, h, :].bitcast(F32)[:, 256 * g + u:256 * (g + 1):2], ident_f[:]
+                        bank[:, col:col + P], x_sb[:, g, h, :].bitcast(F32)[:, u:256:2], ident_f[:]
                     )
 
         def x_out(g):
@@ -455,7 +455,7 @@ def tile_grucellstack_pa_kernel(tc, x_in, h0, gh0, w_bytes, w_scale, b_ih0, out)
         at(0, T_RUN, bias_turn)
         at(1, S_SUMS, bias_out)
         for g in range(PASSES):
-            at(X_TURN, T_RUN + 4 + g, x_turn, g)
+            at(X_TURN[g], T_RUN + 4 + g, x_turn, g)
             at(X_OUT[g], S_SCALED + 1, x_out, g)
         at(X_QUANT, V_QUANT + 3, x_quantise)
         for J in range(PAIRS):

@@ -50,7 +50,7 @@ SUMS_ON_VECTOR = ()
 SUMS_V = -2
 CAST_BUFS = 3
 PLAIN_ROAD = (6,)
-HEAD_ON_VECTOR = (1, 3)
+HEAD_ON_VECTOR = (1,)
 X_TURN, X_OUT, X_QUANT = (3, 3, 5, 5), (5, 5, 7, 7), 10
 AFTER_HEAD = (8, 8, 12, 16)
 HEAD_LAG = {"passes": 4, "sums": 5, "back": 10, "func": 14}
@@ -115,7 +115,8 @@ def tile_grucellstack_pa_kernel(tc, x_in, h0, gh0, w_bytes, w_scale, b_ih0, out)
         def load_gh(blk):
             nc.sync.dma_start(out=gh_sb[blk][:], in_=gh_view[:, :, blk, :])
 
-        load_pass(0, RUN_FIRST[0])
+        for q in range(2):
+            nc.sync.dma_start(out=w_b[0][:, 0, q, :], in_=w_view[:, BLOCK[gate(0)], pair(0), q, RUN_FIRST[0], :])
         nc.sync.dma_start(out=scales_col[:], in_=w_scale.rearrange("o (g p t) -> p (o g) t", p=P, t=4))
         for g in RUN_FIRST[1:]:
             load_pass(0, g)
@@ -161,6 +162,33 @@ def tile_grucellstack_pa_kernel(tc, x_in, h0, gh0, w_bytes, w_scale, b_ih0, out)
                 nc.vector.tensor_copy(out=dst, in_=src)
             else:
                 nc.scalar.copy(out=dst, in_=src)
+
+        def cast_tile(q):
+            if ("cast", 0) not in live:
+                live[("cast", 0)] = work.tile([P, 2 * IN], BF16, name="cast", bufs=CAST_BUFS)
+            dst = live[("cast", 0)][:, q * 512:(q + 1) * 512]
+            src = w_b[0][:, 0, q, :].bitcast(FP8)
+            if q == 0:
+                nc.scalar.copy(out=dst, in_=src)
+            else:
+                nc.vector.tensor_copy(out=dst, in_=src)
+
+        def turn_tile(q):
+            words = live[("cast", 0)][:].bitcast(F32)
+            bank = turn_bank()
+            live[("tile_bank", q)] = bank
+            for u in range(2):
+                nc.tensor.transpose(bank[:, u * P:(u + 1) * P], words[:, q * 256 + u:(q + 1) * 256:2], ident_f[:])
+
+        def evac_tile(q):
+            g = RUN_FIRST[0]
+            dst = grouped(0, g)[:, q * 512:(q + 1) * 512]
+            nc.vector.tensor_tensor(
+                out=dst.rearrange("p (a u e) -> p a u e", u=2, e=2),
+                in0=live[("tile_bank", q)][:, 0:256].bitcast(BF16).rearrange("p (u a e) -> p a u e", u=2, e=2),
+                in1=scales_col[:, g, :].unsqueeze(1).to_broadcast([P, 128, 4]).rearrange("p a (u e) -> p a u e", u=2),
+                op=ALU.mult,
+            )
 
         def turn(m, g):
             words = live[("cast", m)][:].bitcast(F32)
@@ -421,14 +449,23 @@ def tile_grucellstack_pa_kernel(tc, x_in, h0, gh0, w_bytes, w_scale, b_ih0, out)
         for m in range(UNITS):
             b = base(m)
             for i in range(PASSES):
+                if m == 0 and i == 0:
+                    for q in range(2):
+                        at(b + CAST[i], S_CAST, cast_tile, q)
+                        at(b + RUN_LAG[i], T_RUN + i, turn_tile, q)
+                    continue
                 if m == 0:
                     at(b + CAST[i], S_CAST, cast, m, i, 1)
                 elif i % 2 == 0:
                     at(b + CAST[i], S_CAST, cast, m, i, 2)
-                at(b + RUN_LAG[i], T_RUN + i, turn, m, run_of(m)[i])
+                at(0 if (m == 0 and i == PASSES - 1) else b + RUN_LAG[i], T_RUN + i, turn, m, run_of(m)[i])
             if not on_road(m):
                 at(b, V_EVAC - 1, evac, m, ROAD_PASS)
             for g in range(PASSES - 1):
+                if m == 0 and g == RUN_FIRST[0]:
+                    for q in range(2):
+                        at(b + g, V_EVAC, evac_tile, q)
+                    continue
                 at(b + g, V_EVAC, evac, m, g)
             if on_road(m):
                 for t in range(4):

from contextlib import ExitStack

import concourse.mybir as mybir
from concourse.masks import make_identity

F32 = mybir.dt.float32
BF16 = mybir.dt.bfloat16
U8 = mybir.dt.uint8
U32 = mybir.dt.uint32
FP8 = mybir.dt.float8_e4m3fn
FP8X4 = mybir.dt.float8_e4m3fn_x4
ACT = mybir.ActivationFunctionType
ALU = mybir.AluOpType

B, IN, L = 256, 2048, 1536
FLOPS = 2 * B * IN * 3 * L

P = 128
K_PASS = 512
PASSES = IN // K_PASS
PAIRS = L // 256
UNITS = 3 * PAIRS
ROAD_PASS = PASSES - 1

GN, GR, GZ = 0, 1, 2
BLOCK = (2, 0, 1)
SEQ = tuple([(J, g) for J in range(PAIRS - 2) for g in (GN, GR, GZ)]) + tuple([(J, g) for g in (GR, GN, GZ) for J in (PAIRS - 2, PAIRS - 1)])

SUM_BANKS, TURN_BANKS, BACK_BANKS = 2, 4, 2
NO_ROAD = ()
RUN = (3, 0, 1, 2)
RUN_FIRST = (0, 1, 2, 3)
SCALED_FIRST = 1

V_EVAC, V_QUANT = 10, 12
S_SUMS, S_CAST, S_FUNC, S_SCALED = 20, 22, 24, 26
T_PASSES, T_RUN, T_OPEN, T_BACK = 30, 32, 36, 37
G_WEAVE, G_BLEND = 50, 52

CAST, RUN_LAG, SCALED, WEAVE, QUANT = (-4, -4, -4, -4), (-3, -3, -1, -1), -2, 0, 3
UNIT_LAG = {"passes": 8, "sums": 11, "back": 14, "func": 18}
UNIT_LAST = {16: {"passes": 4, "sums": 6, "back": 7, "func": 8}, 17: {"passes": 4, "sums": 5, "back": 6, "func": 7}}
PAIR_LAG = {"r_gh": 19, "back_n": 21, "tanh": 23, "h_n": 25, "z_d": 29, "out": 33}
PAIR_LAST = {0: {"r_gh": 15, "back_n": 17, "tanh": 19, "h_n": 21, "z_d": 25, "out": 29}, 3: {"r_gh": 19, "back_n": 21, "tanh": 23, "h_n": 25, "z_d": 29, "out": 33},
             4: {"r_gh": 19, "back_n": 22, "tanh": 23, "h_n": 24, "z_d": 26, "out": 26},
             5: {"r_gh": 19, "r_gh_place": 3, "back_n": 20, "tanh": 21, "h_n": 22, "z_d": 24, "out": 25}}
ON_VECTOR = (4, 5)
STEPS_ON_VECTOR = ((3, "out"),)
SUMS_ON_VECTOR = ()
SUMS_V = -2
CAST_BUFS = 3
PLAIN_ROAD = (6,)
HEAD_ON_VECTOR = (1,)
X_TURN, X_OUT, X_QUANT = (3, 3, 5, 5), (5, 5, 7, 7), 10
AFTER_HEAD = (8, 8, 12, 16)
HEAD_LAG = {"passes": 4, "sums": 5, "back": 10, "func": 14}


def tile_grucellstack_pa_kernel(tc, x_in, h0, gh0, w_bytes, w_scale, b_ih0, out):
    nc = tc.nc
    with ExitStack() as ctx:
        const = ctx.enter_context(tc.tile_pool(name="const", bufs=1))
        wpool = ctx.enter_context(tc.tile_pool(name="wpool", bufs=1))
        work = ctx.enter_context(tc.tile_pool(name="work", bufs=2))
        ep = ctx.enter_context(tc.tile_pool(name="ep", bufs=2))
        psum = ctx.enter_context(tc.psum_pool(name="psum", bufs=1))
        ctx.enter_context(tc.manual_schedule())

        def span_place(m, g):
            return (m, 2048 + g * 1024) if g < 2 else (m + 1, (g - 2) * 1024)

        def gate(m):
            return SEQ[m][1]

        def pair(m):
            return SEQ[m][0]

        def unit(J, g):
            return SEQ.index((J, g))

        def on_road(m):
            return m not in NO_ROAD

        w_view = w_bytes.rearrange("(b j q p) (g k) -> p b j q g k", b=3, q=2, p=P, k=K_PASS)
        w_b = {}
        for m in range(UNITS):
            w_b[m] = wpool.tile([P, PASSES, 2, K_PASS], U8, name="w_b_%d" % m)
        scales_col = const.tile([P, PASSES, 4], F32, name="scales_col")
        x_sb = const.tile([P, PASSES, 2, K_PASS], BF16, name="x_sb")
        h_sb = const.tile([P, 2, L], BF16, name="h_sb")
        gh_sb = {}
        for blk in range(3):
            gh_sb[blk] = const.tile([P, 2, L], BF16, name="gh_sb_%d" % blk)
        b_rows = const.tile([P, P], BF16, name="b_rows")
        warm_in = const.tile([P, 1], F32, name="warm_in")
        warm_out = const.tile([P, 1], F32, name="warm_out")

        nc.vector.memset(warm_in[:], 0.0)
        nc.vector.memset(b_rows[:], 0.0)
        nc.scalar.activation(out=warm_out[:], in_=warm_in[:], func=ACT.Sigmoid)

        def run_of(m):
            return RUN_FIRST if m == 0 else RUN

        def load_pass(m, g):
            nc.sync.dma_start(out=w_b[m][:, run_of(m).index(g), :, :], in_=w_view[:, BLOCK[gate(m)], pair(m), :, g, :])

        def load_unit(m):
            for g in RUN:
                load_pass(m, g)

        x_view = x_in.rearrange("(h p) k -> p h k", p=P)
        gh_view = gh0.rearrange("(h p) (g c) -> p h g c", p=P, g=3)

        def load_gh(blk):
            nc.sync.dma_start(out=gh_sb[blk][:], in_=gh_view[:, :, blk, :])

        for q in range(2):
            nc.sync.dma_start(out=w_b[0][:, 0, q, :], in_=w_view[:, BLOCK[gate(0)], pair(0), q, RUN_FIRST[0], :])
        nc.sync.dma_start(out=scales_col[:], in_=w_scale.rearrange("o (g p t) -> p (o g) t", p=P, t=4))
        for g in RUN_FIRST[1:]:
            load_pass(0, g)
        nc.sync.dma_start(out=b_rows[0:36, :], in_=b_ih0.rearrange("(c p) -> c p", p=P))
        load_unit(1)
        load_unit(2)
        for g in range(PASSES):
            nc.sync.dma_start(out=x_sb[:, g, :, :], in_=x_view[:, :, g * K_PASS:(g + 1) * K_PASS])
        load_unit(3)
        load_gh(BLOCK[GR])
        load_unit(4)
        load_gh(BLOCK[GZ])
        load_gh(BLOCK[GN])
        load_unit(5)
        nc.sync.dma_start(out=h_sb[:], in_=h0.rearrange("(h p) c -> p h c", p=P))
        for m in range(6, UNITS):
            load_unit(m)

        ident_f = const.tile([P, P], F32, name="ident_f")
        make_identity(nc, ident_f[:])
        ident_b = const.tile([P, P], BF16, name="ident_b")
        make_identity(nc, ident_b[:])

        x_grouped = const.tile([P, PASSES * B * 4], BF16, name="x_grouped", align_bytes=64)
        x_codes = const.tile([P, PASSES * B], U32, name="x_codes", align_bytes=64)
        x_scales = const.tile([P, PASSES * B], U8, name="x_scales", align_bytes=64)
        bias_col = const.tile([P, 36], F32, name="bias_col")

        live = {}

        def turn_bank():
            return psum.tile([P, 512], F32, name="turn", tag="turn", bufs=TURN_BANKS)

        def back_bank():
            return psum.tile([P, 512], F32, name="back", tag="back", bufs=BACK_BANKS)

        def cast(m, i, n):
            if ("cast", m) not in live:
                live[("cast", m)] = work.tile([P, 2 * IN], BF16, name="cast", bufs=CAST_BUFS)
            dst = live[("cast", m)][:, i * 1024:(i + n) * 1024]
            src = w_b[m][:, i:i + n, :, :].rearrange("p g q k -> p (g q k)").bitcast(FP8)
            if m * 4 + i in HEAD_ON_VECTOR:
                nc.vector.tensor_copy(out=dst, in_=src)
            else:
                nc.scalar.copy(out=dst, in_=src)

        def cast_tile(q):
            if ("cast", 0) not in live:
                live[("cast", 0)] = work.tile([P, 2 * IN], BF16, name="cast", bufs=CAST_BUFS)
            dst = live[("cast", 0)][:, q * 512:(q + 1) * 512]
            src = w_b[0][:, 0, q, :].bitcast(FP8)
            if q == 0:
                nc.scalar.copy(out=dst, in_=src)
            else:
                nc.vector.tensor_copy(out=dst, in_=src)

        def turn_tile(q):
            words = live[("cast", 0)][:].bitcast(F32)
            bank = turn_bank()
            live[("tile_bank", q)] = bank
            for u in range(2):
                nc.tensor.transpose(bank[:, u * P:(u + 1) * P], words[:, q * 256 + u:(q + 1) * 256:2], ident_f[:])

        def evac_tile(q):
            g = RUN_FIRST[0]
            dst = grouped(0, g)[:, q * 512:(q + 1) * 512]
            nc.vector.tensor_tensor(
                out=dst.rearrange("p (a u e) -> p a u e", u=2, e=2),
                in0=live[("tile_bank", q)][:, 0:256].bitcast(BF16).rearrange("p (u a e) -> p a u e", u=2, e=2),
                in1=scales_col[:, g, :].unsqueeze(1).to_broadcast([P, 128, 4]).rearrange("p a (u e) -> p a u e", u=2),
                op=ALU.mult,
            )

        def turn(m, g):
            words = live[("cast", m)][:].bitcast(F32)
            bank = turn_bank()
            live[("bank", m, g)] = bank
            for u in range(2):
                for q in range(2):
                    col = (2 * u + q) * P
                    first = run_of(m).index(g) * 512 + q * 256
                    nc.tensor.transpose(bank[:, col:col + P], words[:, first + u:first + 256:2], ident_f[:])

        def grouped(m, g):
            k, first = span_place(m, g)
            if ("span", k) not in live:
                live[("span", k)] = work.tile([P, PASSES * 1024], BF16, name="span", bufs=2, align_bytes=64)
            return live[("span", k)][:, first:first + 1024]

        def evac(m, g):
            dst = grouped(m, g)
            nc.vector.tensor_tensor(
                out=dst.rearrange("p (a u e) -> p a u e", u=2, e=2),
                in0=live[("bank", m, g)][:].bitcast(BF16).rearrange("p (u a e) -> p a u e", u=2, e=2),
                in1=scales_col[:, g, :].unsqueeze(1).to_broadcast([P, 256, 4]).rearrange("p a (u e) -> p a u e", u=2),
                op=ALU.mult,
            )

        def scaled(m, t):
            if t == 0:
                live[("planes", m)] = work.tile([P, 1024], BF16, name="planes", bufs=2)
            if m in PLAIN_ROAD:
                if t == 0:
                    nc.scalar.copy(
                        out=live[("planes", m)][:].bitcast(F32).rearrange("p (a u) -> p a u", u=2),
                        in_=live[("bank", m, ROAD_PASS)][:].rearrange("p (u a) -> p a u", u=2),
                    )
                return
            halves = live[("bank", m, ROAD_PASS)][:].bitcast(BF16)
            u, e = t // 2, t % 2
            nc.scalar.activation(
                out=live[("planes", m)][:, t * 256:(t + 1) * 256], in_=halves[:, u * 512 + e:(u + 1) * 512:2],
                func=ACT.Copy, scale=scales_col[:, ROAD_PASS, t:t + 1],
            )

        def weave(m):
            if m in PLAIN_ROAD:
                nc.gpsimd.tensor_tensor(
                    out=grouped(m, ROAD_PASS).rearrange("p (a t) -> p a t", t=4),
                    in0=live[("planes", m)][:].rearrange("p (a t) -> p a t", t=4),
                    in1=scales_col[:, ROAD_PASS, :].unsqueeze(1).to_broadcast([P, 256, 4]), op=ALU.mult,
                )
                return
            nc.gpsimd.tensor_scalar(
                out=grouped(m, ROAD_PASS).rearrange("p (a t) -> p a t", t=4),
                in0=live[("planes", m)][:].rearrange("p (t a) -> p a t", t=4),
                scalar1=1.0, scalar2=0.0, op0=ALU.mult, op1=ALU.add,
            )

        def quantise(k, halves):
            if ("codes", k) not in live:
                live[("codes", k)] = work.tile([P, 1024], U32, name="codes", bufs=3, align_bytes=64)
                live[("scales", k)] = work.tile([P, 1024], U8, name="scales", bufs=3, align_bytes=64)
            cols = slice(halves[0] * 512, (halves[-1] + 1) * 512)
            nc.vector.quantize_mx(
                out=live[("codes", k)][:, cols].bitcast(FP8X4), scales=live[("scales", k)][:, cols],
                in_=live[("span", k)][:, 4 * cols.start:4 * cols.stop],
            )

        def passes(m, j):
            if j == 0:
                live[("sums", m)] = psum.tile([P, 512], F32, name="sums", tag="sums", bufs=SUM_BANKS)
            for g in range(PASSES):
                k, first = span_place(m, g)
                col = first // 4 + j * P
                nc.tensor.matmul_mx(
                    out=live[("sums", m)][:, j * B:(j + 1) * B],
                    lhsT=live[("codes", k)][:, col:col + P].bitcast(FP8X4),
                    lhsT_scale=live[("scales", k)][:, col:col + P],
                    rhs=x_codes[:, g * B:(g + 1) * B].bitcast(FP8X4),
                    rhs_scale=x_scales[:, g * B:(g + 1) * B],
                    start=(g == 0), stop=(g == PASSES - 1),
                )

        def x_turn(g):
            if g < 2:
                bank = psum.tile([P, 512], F32, name="sums", tag="sums", bufs=SUM_BANKS)
            else:
                bank = back_bank()
            live[("x_bank", g)] = bank
            for u in range(2):
                for h in range(2):
                    col = (u * 2 + h) * P
                    nc.tensor.transpose(
                        bank[:, col:col + P], x_sb[:, g, h, :].bitcast(F32)[:, u:256:2], ident_f[:]
                    )

        def x_out(g):
            nc.scalar.copy(
                out=x_grouped[:].bitcast(F32)[:, g * 512:(g + 1) * 512].rearrange("p (r u) -> p r u", u=2),
                in_=live[("x_bank", g)][:].rearrange("p (u r) -> p r u", u=2),
            )

        def x_quantise():
            nc.vector.quantize_mx(out=x_codes[:].bitcast(FP8X4), scales=x_scales[:], in_=x_grouped[:])

        def bias_turn():
            live["bias_bank"] = psum.tile([P, 1024], BF16, name="bias_bank", tag="back", bufs=BACK_BANKS)
            nc.tensor.transpose(live["bias_bank"][:, 0:P], b_rows[:], ident_b[:])

        def bias_out():
            nc.scalar.copy(out=bias_col[:], in_=live["bias_bank"][:, 0:36])

        whole = (slice(0, 512),)
        pair_halves = (slice(0, 256), slice(256, 512))

        def by_half(t):
            return t[:].rearrange("p (h c) -> p h c", h=2)

        def of_pair(t, J):
            return t[:, :, J * 256:(J + 1) * 256]

        def blender(J, step):
            return nc.vector if J in ON_VECTOR or (J, step) in STEPS_ON_VECTOR else nc.gpsimd

        def sum_on_tensor(J):
            return True

        def sums_out(m, j):
            J, g = pair(m), gate(m)
            if j == 0:
                live[("biased", m)] = ep.tile([P, 512], F32, name="biased_n" if g == GN else "biased", bufs=3)
            c = BLOCK[g] * 12 + 2 * J + j
            if m in SUMS_ON_VECTOR:
                if j == 0:
                    nc.vector.tensor_tensor(
                        out=live[("biased", m)][:].rearrange("p (j r) -> p j r", j=2),
                        in0=live[("sums", m)][:].rearrange("p (j r) -> p j r", j=2),
                        in1=bias_col[:, c:c + 2].unsqueeze(2).to_broadcast([P, 2, B]), op=ALU.add,
                    )
                return
            nc.scalar.activation(
                out=live[("biased", m)][:, j * B:(j + 1) * B], in_=live[("sums", m)][:, j * B:(j + 1) * B],
                func=ACT.Identity, bias=bias_col[:, c:c + 1], scale=1.0,
            )

        def by_tokens(J):
            return pair_halves if J == PAIRS - 1 else whole

        def open_with_gh(m):
            live[("back", m)] = back_bank()
            if pair(m) == PAIRS - 1:
                return
            nc.tensor.matmul(
                out=by_half(live[("back", m)]), lhsT=ident_b[:], rhs=of_pair(gh_sb[BLOCK[gate(m)]], pair(m)),
                start=True, stop=False,
            )

        def open_with_r_gh(J):
            live[("back", unit(J, GN))] = back_bank()
            if J == PAIRS - 1:
                return
            nc.tensor.matmul(
                out=live[("back", unit(J, GN))][:], lhsT=ident_f[:], rhs=live[("r", J)][:], start=True, stop=False
            )

        def turn_back(m):
            alone = gate(m) == GN and not sum_on_tensor(pair(m))
            if alone:
                live[("back", m)] = back_bank()
            halved = pair(m) == PAIRS - 1
            for h in range(2):
                if halved and gate(m) == GN:
                    nc.tensor.matmul(
                        out=live[("back", m)][:, h * 256:(h + 1) * 256], lhsT=ident_f[:],
                        rhs=live[("r", pair(m))][:, h * 256:(h + 1) * 256], start=True, stop=False,
                    )
                elif halved:
                    nc.tensor.matmul(
                        out=live[("back", m)][:, h * 256:(h + 1) * 256], lhsT=ident_b[:],
                        rhs=of_pair(gh_sb[BLOCK[gate(m)]], pair(m))[:, h, :], start=True, stop=False,
                    )
                for j in range(2):
                    nc.tensor.matmul(
                        out=live[("back", m)][:, h * 256 + j * P:h * 256 + (j + 1) * P],
                        lhsT=live[("biased", m)][:, j * 256 + h * P:j * 256 + (h + 1) * P], rhs=ident_f[:],
                        is_transpose=True, start=alone, stop=(alone or (j == 1 and (h == 1 or halved))),
                    )

        def sigmoid(m):
            name = "r" if gate(m) == GR else "z"
            live[(name, pair(m))] = ep.tile([P, 512], F32, name=name, bufs=3)
            for cols in by_tokens(pair(m)):
                nc.scalar.activation(out=live[(name, pair(m))][:, cols], in_=live[("back", m)][:, cols], func=ACT.Sigmoid)

        def r_gh(J):
            r = live[("r", J)]
            if J == PAIRS - 1:
                for h in range(2):
                    cols = pair_halves[h]
                    nc.vector.tensor_tensor(out=r[:, cols], in0=r[:, cols], in1=of_pair(gh_sb[BLOCK[GN]], J)[:, h, :], op=ALU.mult)
                return
            nc.vector.tensor_tensor(out=by_half(r), in0=by_half(r), in1=of_pair(gh_sb[BLOCK[GN]], J), op=ALU.mult)

        def n_sum(J):
            r = live[("r", J)]
            nc.vector.tensor_tensor(out=r[:], in0=live[("back", unit(J, GN))][:], in1=r[:], op=ALU.add)

        def tanh(J):
            r = live[("r", J)]
            src = live[("back", unit(J, GN))] if sum_on_tensor(J) else r
            for cols in by_tokens(J):
                nc.scalar.activation(out=r[:, cols], in_=src[:, cols], func=ACT.Tanh)

        def h_minus_n(J):
            live[("d", J)] = ep.tile([P, 512], F32, name="d", bufs=3)
            if J == PAIRS - 1:
                for h in range(2):
                    cols = pair_halves[h]
                    nc.vector.tensor_tensor(out=live[("d", J)][:, cols], in0=of_pair(h_sb, J)[:, h, :], in1=live[("r", J)][:, cols], op=ALU.subtract)
                return
            blender(J, "h_n").tensor_tensor(
                out=by_half(live[("d", J)]), in0=of_pair(h_sb, J), in1=by_half(live[("r", J)]), op=ALU.subtract
            )

        def z_times_diff(J):
            d = live[("d", J)]
            for cols in by_tokens(J):
                blender(J, "z_d").tensor_tensor(out=d[:, cols], in0=d[:, cols], in1=live[("z", J)][:, cols], op=ALU.mult)

        out_view = out.rearrange("(h p) c -> p h c", p=P)

        def result(J):
            d = live[("d", J)]
            if J < PAIRS - 1:
                blender(J, "out").tensor_tensor(out=d[:], in0=d[:], in1=live[("r", J)][:], op=ALU.add)
                nc.sync.dma_start(out=of_pair(out_view, J), in_=by_half(d))
            else:
                for h in range(2):
                    cols = slice(h * 256, (h + 1) * 256)
                    nc.vector.tensor_tensor(out=d[:, cols], in0=d[:, cols], in1=live[("r", J)][:, cols], op=ALU.add)
                    nc.sync.dma_start(out=of_pair(out_view, J)[:, h, :], in_=d[:, cols])

        steps = []

        def at(slot, place, fn, *args):
            steps.append((slot, place, len(steps), fn, args))

        def base(m):
            return 4 * m

        def after(m):
            return max(base(m), AFTER_HEAD[m]) if m < len(AFTER_HEAD) else base(m)

        def unit_lag(m):
            if m < len(AFTER_HEAD):
                return HEAD_LAG
            return UNIT_LAST.get(m, UNIT_LAG)

        for m in range(UNITS):
            b = base(m)
            for i in range(PASSES):
                if m == 0 and i == 0:
                    for q in range(2):
                        at(b + CAST[i], S_CAST, cast_tile, q)
                        at(b + RUN_LAG[i], T_RUN + i, turn_tile, q)
                    continue
                if m == 0:
                    at(b + CAST[i], S_CAST, cast, m, i, 1)
                elif i % 2 == 0:
                    at(b + CAST[i], S_CAST, cast, m, i, 2)
                at(0 if (m == 0 and i == PASSES - 1) else b + RUN_LAG[i], T_RUN + i, turn, m, run_of(m)[i])
            if not on_road(m):
                at(b, V_EVAC - 1, evac, m, ROAD_PASS)
            for g in range(PASSES - 1):
                if m == 0 and g == RUN_FIRST[0]:
                    for q in range(2):
                        at(b + g, V_EVAC, evac_tile, q)
                    continue
                at(b + g, V_EVAC, evac, m, g)
            if on_road(m):
                for t in range(4):
                    at(SCALED_FIRST if m == 0 else b + SCALED, S_SCALED, scaled, m, t)
                at(SCALED_FIRST if m == 0 else b + WEAVE, G_WEAVE, weave, m)
            if m == 0 or m == UNITS - 1:
                at(b + QUANT, V_QUANT, quantise, m, (1,))
            else:
                at(b + QUANT, V_QUANT, quantise, m, (0, 1))
            if m >= UNITS - 2:
                at(b + QUANT, V_QUANT + 2, quantise, m + 1, (0,))
            lag = unit_lag(m)
            at(after(m) + lag["passes"], T_PASSES, passes, m, 0)
            at(after(m) + lag["passes"], T_PASSES, passes, m, 1)
            if m in SUMS_ON_VECTOR:
                at(after(m) + lag["sums"] + SUMS_V, V_QUANT + 1, sums_out, m, 0)
            else:
                at(after(m) + lag["sums"], S_SUMS, sums_out, m, 0)
                at(after(m) + lag["sums"], S_SUMS, sums_out, m, 1)
            if gate(m) != GN:
                at(after(m) + lag["back"], T_OPEN, open_with_gh, m)
                at(after(m) + lag["back"], T_BACK, turn_back, m)
                at(after(m) + lag["func"], S_FUNC, sigmoid, m)
        at(0, T_RUN, bias_turn)
        at(1, S_SUMS, bias_out)
        for g in range(PASSES):
            at(X_TURN[g], T_RUN + 4 + g, x_turn, g)
            at(X_OUT[g], S_SCALED + 1, x_out, g)
        at(X_QUANT, V_QUANT + 3, x_quantise)
        for J in range(PAIRS):
            lag = PAIR_LAST.get(J, PAIR_LAG)
            b_r = after(unit(J, GR))
            at(b_r + lag["r_gh"], V_QUANT + lag.get("r_gh_place", 1), r_gh, J)
            if sum_on_tensor(J):
                at(b_r + lag["back_n"], T_OPEN, open_with_r_gh, J)
            at(b_r + lag["back_n"], T_BACK, turn_back, unit(J, GN))
            if not sum_on_tensor(J):
                at(b_r + lag["back_n"] + 1, V_QUANT + 3, n_sum, J)
            at(b_r + lag["tanh"], S_FUNC, tanh, J)
            at(b_r + lag["h_n"], G_BLEND, h_minus_n, J)
            at(b_r + lag["z_d"], G_BLEND, z_times_diff, J)
            at(b_r + lag["out"], lag.get("out_place", G_BLEND), result, J)
        for step in sorted(steps, key=lambda e: e[0:3]):
            step[3](*step[4])
